import numpy as np
import ml_dtypes


def mxq(x, axis, fmt="e4m3"):
    dtype, down = {"e4m3": (ml_dtypes.float8_e4m3fn, 7), "e5m2": (ml_dtypes.float8_e5m2, 14)}[fmt]
    v = np.moveaxis(np.asarray(x, np.float32).astype(ml_dtypes.bfloat16).astype(np.float64), axis, -1)
    blocks = v.reshape(v.shape[:-1] + (-1, 32))
    amax = np.abs(blocks).max(-1, keepdims=True)
    byte = np.maximum(np.where(amax > 0, np.frexp(amax)[1] - 1 + 127, 0) - down, 1)
    scale = np.exp2(byte - 127.0)
    codes = (blocks / scale).astype(np.float32).astype(dtype).astype(np.float64)
    return np.moveaxis((codes * scale).reshape(v.shape), -1, axis)


WIDE = False


def mx_kscale(k):
    if not WIDE:
        return np.ones(k)
    levels = np.array([10, -10, 5, -5, 0])
    a = np.random.permutation(np.resize(levels, k // 512 * 4)).reshape(k // 512, 4)
    idx = np.arange(k)
    return np.exp2(a[idx // 512, idx % 128 // 32])


BF16 = ml_dtypes.bfloat16


def bf(x):
    return np.asarray(x, np.float32).astype(BF16)


def f64(x):
    return np.asarray(x).astype(np.float64)


B, T, F, N, SR, GROUPS = 2, 128, 16385, 128, 2048, ((0, 256, 16), (256, 512, 32), (512, 1024, 64))
EPS = 1e-8
TAGS = ('16', '32', '64')
R = (F - 1) * 2 // SR


def setup_inputs():
    lev = 10.0 ** np.random.uniform(-4.5, 0.0, (B, 1, T))
    inp = {'x_real': bf(lev * (np.random.standard_normal((B, F, T)) + 0.5 * np.random.standard_normal((B, 1, T)))),
           'x_imag': bf(lev * (np.random.standard_normal((B, F, T)) + 0.5 * np.random.standard_normal((B, 1, T)))),
           'sample_rate': SR}
    for (s0, e0, w0), tag in zip(GROUPS, TAGS):
        k = (e0 - s0) // w0
        ch = 2 * w0 * R
        s = mx_kscale(ch)
        inp['g' + tag] = bf(np.random.uniform(0.5, 1.5, (k, ch)) * s)
        inp['b' + tag] = bf(0.1 * np.random.standard_normal((k, ch)) * s)
        inp['W' + tag] = bf(np.random.standard_normal((k, ch, N)) / np.sqrt(ch) / s[:, None])
        inp['c' + tag] = bf(0.1 * np.random.standard_normal((k, N)))
    return inp


def _band_group(x_real, x_imag, s, e, w, g, b, W, c):
    nb, _, nt = x_real.shape
    k = (e - s) // w
    xr = x_real[:, s:e, :].reshape(nb, k, w, nt)
    xi = x_imag[:, s:e, :].reshape(nb, k, w, nt)
    X = np.concatenate([xr, xi], axis=2)
    mu = X.mean(axis=2, keepdims=True)
    var = X.var(axis=2, keepdims=True)
    Xn = (X - mu) / np.sqrt(var + EPS)
    Xn = Xn * g[None, :, :, None] + b[None, :, :, None]
    Xq = mxq(Xn, 2, 'e4m3')
    Wq = mxq(W, 1, 'e4m3')
    y = Xq.transpose(0, 1, 3, 2) @ Wq[None]
    return y.transpose(0, 2, 1, 3) + c[None, None, :, :]


def reference(x_real, x_imag, sample_rate, g16, b16, W16, c16, g32, b32, W32, c32, g64, b64, W64, c64):
    x_real, x_imag = f64(x_real), f64(x_imag)
    nf = x_real.shape[1]
    n_fft = (nf - 1) * 2
    sr = int(sample_rate)
    params = [(g16, b16, W16, c16), (g32, b32, W32, c32), (g64, b64, W64, c64)]
    feats = []
    for (s, e, w), (g, b, W, c) in zip(GROUPS, params):
        sb = s * n_fft // sr
        eb = min(e * n_fft // sr, nf)
        wb = w * n_fft // sr
        feats.append(_band_group(x_real, x_imag, sb, eb, wb, f64(g), f64(b), f64(W), f64(c)))
    out = np.concatenate(feats, axis=2)
    return np.transpose(out, (0, 3, 2, 1))

@@ -1,0 +1,277 @@
+from contextlib import ExitStack
+
+import concourse.mybir as mybir
+from concourse.masks import make_identity
+
+FLOPS = 2 * 256 * 32768 * 128
+
+F32 = mybir.dt.float32
+BF16 = mybir.dt.bfloat16
+U32 = mybir.dt.uint32
+U8 = mybir.dt.uint8
+FP8X4 = mybir.dt.float8_e4m3fn_x4
+ACT = mybir.ActivationFunctionType
+ALU = mybir.AluOpType
+
+P = 128
+EPS = 1e-8
+ROUNDS = 16
+
+
+def round_slots(r):
+    if r < 4:
+        return [(0, 2 * r), (0, 2 * r + 1), (1, 2 * r), (1, 2 * r + 1)], 4
+    if r < 8:
+        a = 8 + 2 * (r - 4)
+        return [(0, a), (1, a), (0, a + 1), (1, a + 1)], 2
+    a = 16 + 2 * (r - 8)
+    return [(0, a), (0, a + 1), (1, a), (1, a + 1)], 1
+
+
+def first_band(r):
+    if r < 4:
+        return 4 * r
+    if r < 8:
+        return 16 + 2 * (r - 4)
+    return 24 + (r - 8)
+
+
+def tile_bandsplitmodule_kernel(
+    tc, x_real, x_imag, sample_rate,
+    g16, b16, W16, c16, g32, b32, W32, c32, g64, b64, W64, c64, out,
+):
+    nc = tc.nc
+    with ExitStack() as ctx:
+        const = ctx.enter_context(tc.tile_pool(name="const", bufs=1))
+        xpool = ctx.enter_context(tc.tile_pool(name="xpool", bufs=4))
+        wpool = ctx.enter_context(tc.tile_pool(name="wpool", bufs=3))
+        small = ctx.enter_context(tc.tile_pool(name="small", bufs=3))
+        zpool = ctx.enter_context(tc.tile_pool(name="zpool", bufs=6))
+        qpool = ctx.enter_context(tc.tile_pool(name="qpool", bufs=4))
+        opool = ctx.enter_context(tc.tile_pool(name="opool", bufs=2))
+        ps1 = ctx.enter_context(tc.psum_pool(name="ps1", bufs=4))
+        ps2 = ctx.enter_context(tc.psum_pool(name="ps2", bufs=3))
+        psa = ctx.enter_context(tc.psum_pool(name="psa", bufs=1))
+
+        xs_t = {}
+        wraw_t = {}
+        wq_t = {}
+        p1_t = {}
+        stat_t = {}
+        z_t = {}
+        o_t = {}
+
+        def load(r):
+            slots, nb = round_slots(r)
+            xs = xpool.tile([P, 4096], BF16, name="xs", tag="xs")
+            xs_t[r] = xs
+            xv = xs[:].rearrange("p (s j b t) -> p s j b t", s=4, j=4, b=2)
+            for s in range(4):
+                imag, a = slots[s]
+                src = x_imag if imag else x_real
+                for b in range(2):
+                    nc.sync.dma_start(
+                        out=xv[:, s, :, b, :],
+                        in_=src[b, 512 * a:512 * a + 512, :].rearrange("(p j) t -> p j t", j=4),
+                    )
+            wraw = wpool.tile([P, 4, 512], BF16, name="wraw", tag="wraw")
+            wraw_t[r] = wraw
+            if r < 4:
+                wsrc = W16[4 * r:4 * r + 4].rearrange("k (p j) n -> p k (j n)", j=4)
+            elif r < 8:
+                k0 = 2 * (r - 4)
+                wsrc = W32[k0:k0 + 2].rearrange("k (u p j) n -> p (k u) (j n)", u=2, j=4)
+            else:
+                wsrc = W64[r - 8].rearrange("(u p j) n -> p u (j n)", u=4, j=4)
+            nc.sync.dma_start(out=wraw[:], in_=wsrc)
+
+        def wprep(r):
+            wraw = wraw_t.pop(r)
+            wg = wpool.tile([P, 4, P, 4], BF16, name="wg", tag="wg", align_bytes=64)
+            nc.vector.tensor_copy(
+                out=wg[:],
+                in_=wraw[:].rearrange("p u (j n) -> p u n j", j=4),
+            )
+            wc = wpool.tile([P, 512], U32, name="wc", tag="wc", align_bytes=64)
+            wsc = wpool.tile([P, 512], U8, name="wsc", tag="wsc", align_bytes=64)
+            nc.vector.quantize_mx(
+                out=wc[:].bitcast(FP8X4),
+                scales=wsc[:],
+                in_=wg[:].rearrange("p u n j -> p (u n j)"),
+            )
+            wq_t[r] = (wc, wsc)
+
+        def stats(r):
+            slots, nb = round_slots(r)
+            xw = xs_t.pop(r)[:].bitcast(F32)
+            st = small.tile([P, 8, 6], F32, name="st", tag="st")
+            views = []
+            for s in range(4):
+                p1 = ps1.tile([P, 512], F32, name="p1", tag="p1")
+                for j in range(4):
+                    c0 = (s * 4 + j) * P
+                    nc.tensor.transpose(p1[:, j * P:(j + 1) * P], xw[:, c0:c0 + P], ident[:])
+                views.append(p1[:].bitcast(BF16).rearrange("q (j p e) -> q j p e", j=4, e=2))
+            p1_t[r] = views
+            if nb == 4:
+                for i in range(4):
+                    a, h = i // 2, i % 2
+                    for part in range(2):
+                        v = views[2 * part + a][:, :, 64 * h:64 * h + 64, :]
+                        nc.vector.bn_stats(out=st[:, 2 * i + part, :], in_=v.rearrange("q j p e -> q j (p e)"))
+            else:
+                for s in range(4):
+                    for half in range(2):
+                        v = views[s][:, 2 * half:2 * half + 2, :, :]
+                        nc.vector.bn_stats(out=st[:, 2 * s + half, :], in_=v.rearrange("q j p e -> q (j p e)"))
+            kk = 2 * nb
+            cpb = 8 // nb
+            mv = small.tile([P, 8, 2], F32, name="mv", tag="mv")
+            for i in range(nb):
+                for e in range(2):
+                    nc.vector.bn_aggr(
+                        out=mv[:, 2 * i + e, :],
+                        in_=st[:, cpb * i:cpb * (i + 1), 3 * e:3 * e + 3],
+                    )
+            ve = small.tile([P, 8], F32, name="ve", tag="ve")
+            nc.vector.tensor_scalar(out=ve[:, 0:kk], in0=mv[:, 0:kk, 1], scalar1=EPS, scalar2=None, op0=ALU.add)
+            sd = small.tile([P, 8], F32, name="sd", tag="sd")
+            nc.scalar.activation(out=sd[:, 0:kk], in_=ve[:, 0:kk], func=ACT.Sqrt)
+            rs = small.tile([P, 8], F32, name="rs", tag="rs")
+            nc.vector.reciprocal(out=rs[:, 0:kk], in_=sd[:, 0:kk])
+            nm = small.tile([P, 8], F32, name="nm", tag="nm")
+            nc.vector.scalar_tensor_tensor(
+                out=nm[:, 0:kk], in0=mv[:, 0:kk, 0], scalar=-1.0, in1=rs[:, 0:kk],
+                op0=ALU.mult, op1=ALU.mult,
+            )
+            stat_t[r] = (rs, nm)
+
+        def e1(r):
+            slots, nb = round_slots(r)
+            views = p1_t.pop(r)
+            rs, nm = stat_t.pop(r)
+            zs = []
+            for i in range(4):
+                z = zpool.tile([P, 2, 4, P], F32, name="z", tag="z")
+                zs.append(z)
+                for e in range(2):
+                    if nb == 4:
+                        a, h = i // 2, i % 2
+                        k = 2 * i + e
+                        for part in range(2):
+                            nc.scalar.activation(
+                                out=z[:, e, :, 64 * part:64 * part + 64],
+                                in_=views[2 * part + a][:, :, 64 * h:64 * h + 64, e],
+                                func=ACT.Identity, scale=rs[:, k:k + 1], bias=nm[:, k:k + 1],
+                            )
+                    else:
+                        k = 2 * (i * nb // 4) + e
+                        nc.scalar.activation(
+                            out=z[:, e, :, :], in_=views[i][:, :, :, e],
+                            func=ACT.Identity, scale=rs[:, k:k + 1], bias=nm[:, k:k + 1],
+                        )
+            z_t[r] = zs
+
+        def rest(r):
+            slots, nb = round_slots(r)
+            zs = z_t.pop(r)
+            wc, wsc = wq_t.pop(r)
+            upb = 4 // nb
+            band0 = first_band(r)
+            acc = None
+            for i in range(4):
+                u = 4 * r + i
+                z = zs[i]
+                xp = qpool.tile([P, 4, 256], BF16, name="xp", tag="xp")
+                for jp in range(2):
+                    p2 = ps2.tile([P, 2, 2, P], F32, name="p2", tag="p2")
+                    for jl in range(2):
+                        for e in range(2):
+                            nc.tensor.transpose(p2[:, jl, e, :], z[:, e, 2 * jp + jl, :], ident[:])
+                    for jl in range(2):
+                        j = 2 * jp + jl
+                        nc.scalar.activation(
+                            out=xp[:, j, :], in_=p2[:, jl, :, :].rearrange("p e q -> p (e q)"),
+                            func=ACT.Identity, scale=gb[:, j, u:u + 1], bias=gb[:, j, 64 + u:65 + u],
+                        )
+                xg = qpool.tile([P, 256, 4], BF16, name="xg", tag="xg", align_bytes=64)
+                nc.vector.tensor_copy(
+                    out=xg[:].rearrange("p (c i) j -> p c j i", i=4),
+                    in_=xp[:].rearrange("p j (c i) -> p c j i", i=4),
+                )
+                xc = qpool.tile([P, 256], U32, name="xc", tag="xc", align_bytes=64)
+                xsc = qpool.tile([P, 256], U8, name="xsc", tag="xsc", align_bytes=64)
+                nc.vector.quantize_mx(
+                    out=xc[:].bitcast(FP8X4), scales=xsc[:],
+                    in_=xg[:].rearrange("p c j -> p (c j)"),
+                )
+                if i % upb == 0:
+                    acc = psa.tile([P, 512], F32, name="acc", tag="acc")
+                nc.tensor.matmul_mx(
+                    out=acc[:, 0:256],
+                    lhsT=wc[:, i * P:(i + 1) * P].bitcast(FP8X4),
+                    lhsT_scale=wsc[:, i * P:(i + 1) * P],
+                    rhs=xc[:].bitcast(FP8X4),
+                    rhs_scale=xsc[:],
+                    start=(i % upb == 0),
+                    stop=(i % upb == upb - 1),
+                )
+                if i % upb == upb - 1:
+                    band = band0 + i // upb
+                    if band % 4 == 0:
+                        o_t[0] = opool.tile([P, 2, 4, P], F32, name="osb", tag="osb")
+                    osb = o_t[0]
+                    nc.scalar.activation(
+                        out=osb[:, :, band % 4, :].rearrange("n b (q e) -> n b q e", e=2),
+                        in_=acc[:, 0:256].rearrange("n (e b q) -> n b q e", e=2, b=2),
+                        func=ACT.Identity, bias=csb[:, band:band + 1], scale=1.0,
+                    )
+                    if band % 4 == 3:
+                        nc.gpsimd.dma_start(
+                            out=out[:, :, band - 3:band + 1, :].rearrange("b n k t -> n b (k t)"),
+                            in_=osb[:].rearrange("n b k t -> n b (k t)"),
+                        )
+
+        ident = const.tile([P, P], F32, name="ident")
+        make_identity(nc, ident[:])
+
+        load(0)
+
+        gbrow = const.tile([P, 512], BF16, name="gbrow")
+        nc.scalar.dma_start(out=gbrow[0:16, :], in_=g16)
+        nc.scalar.dma_start(out=gbrow[16:32, :], in_=g32.rearrange("k (u c) -> (k u) c", u=2))
+        nc.scalar.dma_start(out=gbrow[32:64, :], in_=g64.rearrange("k (u c) -> (k u) c", u=4))
+        nc.scalar.dma_start(out=gbrow[64:80, :], in_=b16)
+        nc.scalar.dma_start(out=gbrow[80:96, :], in_=b32.rearrange("k (u c) -> (k u) c", u=2))
+        nc.scalar.dma_start(out=gbrow[96:128, :], in_=b64.rearrange("k (u c) -> (k u) c", u=4))
+        crow = const.tile([P, P], BF16, name="crow")
+        nc.vector.memset(crow[:], 0.0)
+        nc.scalar.dma_start(out=crow[0:16, :], in_=c16)
+        nc.scalar.dma_start(out=crow[16:24, :], in_=c32)
+        nc.scalar.dma_start(out=crow[24:32, :], in_=c64)
+
+        gbp = const.tile([P, 4, P], F32, name="gbp")
+        nc.vector.tensor_copy(out=gbp[:], in_=gbrow[:].rearrange("r (p j) -> r j p", j=4))
+        pg = ps2.tile([P, 4, P], F32, name="pg", tag="p2")
+        for j in range(4):
+            nc.tensor.transpose(pg[:, j, :], gbp[:, j, :], ident[:])
+        gb = const.tile([P, 4, P], F32, name="gb")
+        nc.vector.tensor_copy(out=gb[:], in_=pg[:])
+        crf = const.tile([P, P], F32, name="crf")
+        nc.vector.tensor_copy(out=crf[:], in_=crow[:])
+        pc = ps2.tile([P, 4, P], F32, name="pc", tag="p2")
+        nc.tensor.transpose(pc[:, 0, :], crf[:], ident[:])
+        csb = const.tile([P, 32], F32, name="csb")
+        nc.vector.tensor_copy(out=csb[:], in_=pc[:, 0, 0:32])
+
+        load(1)
+        stats(0)
+        wprep(0)
+        for r in range(ROUNDS):
+            if r + 2 < ROUNDS:
+                load(r + 2)
+            e1(r)
+            if r + 1 < ROUNDS:
+                stats(r + 1)
+                wprep(r + 1)
+            rest(r)

@@ -16,14 +16,12 @@ ALU = mybir.AluOpType
 P = 128
 EPS = 1e-8
 ROUNDS = 16
+W_ON_GPSIMD = True
 
 
 def round_slots(r):
-    if r < 4:
-        return [(0, 2 * r), (0, 2 * r + 1), (1, 2 * r), (1, 2 * r + 1)], 4
     if r < 8:
-        a = 8 + 2 * (r - 4)
-        return [(0, a), (1, a), (0, a + 1), (1, a + 1)], 2
+        return [(0, 2 * r), (1, 2 * r), (0, 2 * r + 1), (1, 2 * r + 1)], (4 if r < 4 else 2)
     a = 16 + 2 * (r - 8)
     return [(0, a), (0, a + 1), (1, a), (1, a + 1)], 1
 
@@ -45,23 +43,34 @@ def tile_bandsplitmodule_kernel(
         const = ctx.enter_context(tc.tile_pool(name="const", bufs=1))
         xpool = ctx.enter_context(tc.tile_pool(name="xpool", bufs=4))
         wpool = ctx.enter_context(tc.tile_pool(name="wpool", bufs=3))
+        wgpool = ctx.enter_context(tc.tile_pool(name="wgpool", bufs=1))
         small = ctx.enter_context(tc.tile_pool(name="small", bufs=3))
         zpool = ctx.enter_context(tc.tile_pool(name="zpool", bufs=6))
-        qpool = ctx.enter_context(tc.tile_pool(name="qpool", bufs=4))
+        qpool = ctx.enter_context(tc.tile_pool(name="qpool", bufs=3))
         opool = ctx.enter_context(tc.tile_pool(name="opool", bufs=2))
         ps1 = ctx.enter_context(tc.psum_pool(name="ps1", bufs=4))
         ps2 = ctx.enter_context(tc.psum_pool(name="ps2", bufs=3))
         psa = ctx.enter_context(tc.psum_pool(name="psa", bufs=1))
+        ctx.enter_context(tc.manual_schedule())
 
         xs_t = {}
         wraw_t = {}
+        wg_t = {}
         wq_t = {}
         p1_t = {}
+        st_t = {}
         stat_t = {}
         z_t = {}
+        p2_t = {}
+        xp_t = {}
+        xg_t = {}
+        xq_t = {}
+        acc_t = {}
         o_t = {}
 
         def load(r):
+            if r >= ROUNDS:
+                return
             slots, nb = round_slots(r)
             xs = xpool.tile([P, 4096], BF16, name="xs", tag="xs")
             xs_t[r] = xs
@@ -85,45 +94,68 @@ def tile_bandsplitmodule_kernel(
                 wsrc = W64[r - 8].rearrange("(u p j) n -> p u (j n)", u=4, j=4)
             nc.sync.dma_start(out=wraw[:], in_=wsrc)
 
-        def wprep(r):
+        def wrg(r):
+            if r >= ROUNDS:
+                return
             wraw = wraw_t.pop(r)
-            wg = wpool.tile([P, 4, P, 4], BF16, name="wg", tag="wg", align_bytes=64)
-            nc.vector.tensor_copy(
-                out=wg[:],
-                in_=wraw[:].rearrange("p u (j n) -> p u n j", j=4),
-            )
+            wg = wgpool.tile([P, 4, P, 4], BF16, name="wg", tag="wg", align_bytes=64)
+            wg_t[r] = wg
+            if W_ON_GPSIMD:
+                for u in range(4):
+                    nc.gpsimd.tensor_scalar(
+                        out=wg[:, u, :, :], in0=wraw[:, u, :].rearrange("p (j n) -> p n j", j=4),
+                        scalar1=1.0, scalar2=0.0, op0=ALU.mult, op1=ALU.add,
+                    )
+            else:
+                nc.vector.tensor_copy(out=wg[:], in_=wraw[:].rearrange("p u (j n) -> p u n j", j=4))
+
+        def wq(r):
+            if r >= ROUNDS:
+                return
+            wg = wg_t.pop(r)
             wc = wpool.tile([P, 512], U32, name="wc", tag="wc", align_bytes=64)
             wsc = wpool.tile([P, 512], U8, name="wsc", tag="wsc", align_bytes=64)
             nc.vector.quantize_mx(
-                out=wc[:].bitcast(FP8X4),
-                scales=wsc[:],
+                out=wc[:].bitcast(FP8X4), scales=wsc[:],
                 in_=wg[:].rearrange("p u n j -> p (u n j)"),
             )
             wq_t[r] = (wc, wsc)
 
-        def stats(r):
+        def t1bn(r, s):
+            if r >= ROUNDS:
+                return
             slots, nb = round_slots(r)
-            xw = xs_t.pop(r)[:].bitcast(F32)
-            st = small.tile([P, 8, 6], F32, name="st", tag="st")
-            views = []
-            for s in range(4):
-                p1 = ps1.tile([P, 512], F32, name="p1", tag="p1")
-                for j in range(4):
-                    c0 = (s * 4 + j) * P
-                    nc.tensor.transpose(p1[:, j * P:(j + 1) * P], xw[:, c0:c0 + P], ident[:])
-                views.append(p1[:].bitcast(BF16).rearrange("q (j p e) -> q j p e", j=4, e=2))
-            p1_t[r] = views
-            if nb == 4:
-                for i in range(4):
-                    a, h = i // 2, i % 2
-                    for part in range(2):
-                        v = views[2 * part + a][:, :, 64 * h:64 * h + 64, :]
-                        nc.vector.bn_stats(out=st[:, 2 * i + part, :], in_=v.rearrange("q j p e -> q j (p e)"))
-            else:
-                for s in range(4):
-                    for half in range(2):
-                        v = views[s][:, 2 * half:2 * half + 2, :, :]
-                        nc.vector.bn_stats(out=st[:, 2 * s + half, :], in_=v.rearrange("q j p e -> q (j p e)"))
+            if s == 0:
+                st_t[r] = small.tile([P, 8, 6], F32, name="st", tag="st")
+                p1_t[r] = []
+            st = st_t[r]
+            xw = xs_t[r][:].bitcast(F32)
+            p1 = ps1.tile([P, 512], F32, name="p1", tag="p1")
+            for j in range(4):
+                c0 = (s * 4 + j) * P
+                nc.tensor.transpose(p1[:, j * P:(j + 1) * P], xw[:, c0:c0 + P], ident[:])
+            v = p1[:].bitcast(BF16).rearrange("q (j p e) -> q j p e", j=4, e=2)
+            p1_t[r].append(v)
+            for h in range(2):
+                if nb == 4:
+                    idx = 2 * (2 * (s // 2) + h) + s % 2
+                    nc.vector.bn_stats(
+                        out=st[:, idx, :],
+                        in_=v[:, :, 64 * h:64 * h + 64, :].rearrange("q j p e -> q j (p e)"),
+                    )
+                else:
+                    nc.vector.bn_stats(
+                        out=st[:, 2 * s + h, :],
+                        in_=v[:, 2 * h:2 * h + 2, :, :].rearrange("q j p e -> q (j p e)"),
+                    )
+            if s == 3:
+                xs_t.pop(r)
+
+        def chain_a(r):
+            if r >= ROUNDS:
+                return
+            slots, nb = round_slots(r)
+            st = st_t.pop(r)
             kk = 2 * nb
             cpb = 8 // nb
             mv = small.tile([P, 8, 2], F32, name="mv", tag="mv")
@@ -135,8 +167,24 @@ def tile_bandsplitmodule_kernel(
                     )
             ve = small.tile([P, 8], F32, name="ve", tag="ve")
             nc.vector.tensor_scalar(out=ve[:, 0:kk], in0=mv[:, 0:kk, 1], scalar1=EPS, scalar2=None, op0=ALU.add)
+            stat_t[r] = (mv, ve)
+
+        def chain_b(r):
+            if r >= ROUNDS:
+                return
+            slots, nb = round_slots(r)
+            kk = 2 * nb
+            mv, ve = stat_t[r]
             sd = small.tile([P, 8], F32, name="sd", tag="sd")
             nc.scalar.activation(out=sd[:, 0:kk], in_=ve[:, 0:kk], func=ACT.Sqrt)
+            stat_t[r] = (mv, sd)
+
+        def chain_c(r):
+            if r >= ROUNDS:
+                return
+            slots, nb = round_slots(r)
+            kk = 2 * nb
+            mv, sd = stat_t[r]
             rs = small.tile([P, 8], F32, name="rs", tag="rs")
             nc.vector.reciprocal(out=rs[:, 0:kk], in_=sd[:, 0:kk])
             nm = small.tile([P, 8], F32, name="nm", tag="nm")
@@ -146,97 +194,132 @@ def tile_bandsplitmodule_kernel(
             )
             stat_t[r] = (rs, nm)
 
-        def e1(r):
+        def e1(r, i):
             slots, nb = round_slots(r)
-            views = p1_t.pop(r)
-            rs, nm = stat_t.pop(r)
-            zs = []
-            for i in range(4):
-                z = zpool.tile([P, 2, 4, P], F32, name="z", tag="z")
-                zs.append(z)
-                for e in range(2):
-                    if nb == 4:
-                        a, h = i // 2, i % 2
-                        k = 2 * i + e
-                        for part in range(2):
-                            nc.scalar.activation(
-                                out=z[:, e, :, 64 * part:64 * part + 64],
-                                in_=views[2 * part + a][:, :, 64 * h:64 * h + 64, e],
-                                func=ACT.Identity, scale=rs[:, k:k + 1], bias=nm[:, k:k + 1],
-                            )
-                    else:
-                        k = 2 * (i * nb // 4) + e
+            views = p1_t[r]
+            rs, nm = stat_t[r]
+            z = zpool.tile([P, 2, 4, P], F32, name="z", tag="z")
+            z_t[(r, i)] = z
+            for e in range(2):
+                if nb == 4:
+                    a, h = i // 2, i % 2
+                    k = 2 * i + e
+                    for part in range(2):
                         nc.scalar.activation(
-                            out=z[:, e, :, :], in_=views[i][:, :, :, e],
+                            out=z[:, e, :, 64 * part:64 * part + 64],
+                            in_=views[2 * a + part][:, :, 64 * h:64 * h + 64, e],
                             func=ACT.Identity, scale=rs[:, k:k + 1], bias=nm[:, k:k + 1],
                         )
-            z_t[r] = zs
+                else:
+                    k = 2 * (i * nb // 4) + e
+                    nc.scalar.activation(
+                        out=z[:, e, :, :], in_=views[i][:, :, :, e],
+                        func=ACT.Identity, scale=rs[:, k:k + 1], bias=nm[:, k:k + 1],
+                    )
 
-        def rest(r):
+        def t2(r, i, jp):
+            z = z_t[(r, i)]
+            p2 = ps2.tile([P, 2, 2, P], F32, name="p2", tag="p2")
+            p2_t[(r, i, jp)] = p2
+            for jl in range(2):
+                for e in range(2):
+                    nc.tensor.transpose(p2[:, jl, e, :], z[:, e, 2 * jp + jl, :], ident[:])
+            if jp == 1:
+                z_t.pop((r, i))
+
+        def e2(r, i, jp):
+            u = 4 * r + i
+            if i % 2 == 0 and jp == 0:
+                xp_t[(r, i // 2)] = qpool.tile([P, 4, 2, 256], BF16, name="xp", tag="xp")
+            xp = xp_t[(r, i // 2)]
+            p2 = p2_t.pop((r, i, jp))
+            for jl in range(2):
+                j = 2 * jp + jl
+                nc.scalar.activation(
+                    out=xp[:, j, i % 2, :], in_=p2[:, jl, :, :].rearrange("p e q -> p (e q)"),
+                    func=ACT.Identity, scale=gb[:, j, u:u + 1], bias=gb[:, j, 64 + u:65 + u],
+                )
+
+        def rg(r, pair):
+            if r < 0:
+                return
+            xp = xp_t.pop((r, pair))
+            xg = qpool.tile([P, 512, 4], BF16, name="xg", tag="xg", align_bytes=64)
+            xg_t[(r, pair)] = xg
+            nc.vector.tensor_copy(
+                out=xg[:].rearrange("p (c i) j -> p c j i", i=4),
+                in_=xp[:].rearrange("p j u c -> p j (u c)").rearrange("p j (c i) -> p c j i", i=4),
+            )
+
+        def qx(r, pair):
+            if r < 0:
+                return
+            xg = xg_t.pop((r, pair))
+            xc = qpool.tile([P, 512], U32, name="xc", tag="xc", align_bytes=64)
+            xsc = qpool.tile([P, 512], U8, name="xsc", tag="xsc", align_bytes=64)
+            nc.vector.quantize_mx(
+                out=xc[:].bitcast(FP8X4), scales=xsc[:],
+                in_=xg[:].rearrange("p c j -> p (c j)"),
+            )
+            xq_t[(r, pair)] = (xc, xsc)
+
+        def mx(r, pair):
+            if r < 0:
+                return
             slots, nb = round_slots(r)
-            zs = z_t.pop(r)
-            wc, wsc = wq_t.pop(r)
             upb = 4 // nb
-            band0 = first_band(r)
-            acc = None
-            for i in range(4):
-                u = 4 * r + i
-                z = zs[i]
-                xp = qpool.tile([P, 4, 256], BF16, name="xp", tag="xp")
-                for jp in range(2):
-                    p2 = ps2.tile([P, 2, 2, P], F32, name="p2", tag="p2")
-                    for jl in range(2):
-                        for e in range(2):
-                            nc.tensor.transpose(p2[:, jl, e, :], z[:, e, 2 * jp + jl, :], ident[:])
-                    for jl in range(2):
-                        j = 2 * jp + jl
-                        nc.scalar.activation(
-                            out=xp[:, j, :], in_=p2[:, jl, :, :].rearrange("p e q -> p (e q)"),
-                            func=ACT.Identity, scale=gb[:, j, u:u + 1], bias=gb[:, j, 64 + u:65 + u],
-                        )
-                xg = qpool.tile([P, 256, 4], BF16, name="xg", tag="xg", align_bytes=64)
-                nc.vector.tensor_copy(
-                    out=xg[:].rearrange("p (c i) j -> p c j i", i=4),
-                    in_=xp[:].rearrange("p j (c i) -> p c j i", i=4),
-                )
-                xc = qpool.tile([P, 256], U32, name="xc", tag="xc", align_bytes=64)
-                xsc = qpool.tile([P, 256], U8, name="xsc", tag="xsc", align_bytes=64)
-                nc.vector.quantize_mx(
-                    out=xc[:].bitcast(FP8X4), scales=xsc[:],
-                    in_=xg[:].rearrange("p c j -> p (c j)"),
-                )
-                if i % upb == 0:
-                    acc = psa.tile([P, 512], F32, name="acc", tag="acc")
+            wc, wsc = wq_t[r]
+            xc, xsc = xq_t.pop((r, pair))
+            if pair == 0 or nb > 1:
+                acc_t[r] = psa.tile([P, 512], F32, name="acc", tag="acc")
+            acc = acc_t[r]
+            for il in range(2):
+                i = 2 * pair + il
+                col = 256 * il if nb == 4 else 0
                 nc.tensor.matmul_mx(
-                    out=acc[:, 0:256],
+                    out=acc[:, col:col + 256],
                     lhsT=wc[:, i * P:(i + 1) * P].bitcast(FP8X4),
                     lhsT_scale=wsc[:, i * P:(i + 1) * P],
-                    rhs=xc[:].bitcast(FP8X4),
-                    rhs_scale=xsc[:],
+                    rhs=xc[:, 256 * il:256 * il + 256].bitcast(FP8X4),
+                    rhs_scale=xsc[:, 256 * il:256 * il + 256],
                     start=(i % upb == 0),
                     stop=(i % upb == upb - 1),
                 )
-                if i % upb == upb - 1:
-                    band = band0 + i // upb
-                    if band % 4 == 0:
-                        o_t[0] = opool.tile([P, 2, 4, P], F32, name="osb", tag="osb")
-                    osb = o_t[0]
-                    nc.scalar.activation(
-                        out=osb[:, :, band % 4, :].rearrange("n b (q e) -> n b q e", e=2),
-                        in_=acc[:, 0:256].rearrange("n (e b q) -> n b q e", e=2, b=2),
-                        func=ACT.Identity, bias=csb[:, band:band + 1], scale=1.0,
+            if pair == 1:
+                wq_t.pop(r)
+
+        def oe(r, pair):
+            if r < 0:
+                return
+            slots, nb = round_slots(r)
+            if nb == 1 and pair == 0:
+                return
+            acc = acc_t[r]
+            band0 = first_band(r)
+            if nb == 4:
+                todo = [(band0 + 2 * pair, 0), (band0 + 2 * pair + 1, 256)]
+            elif nb == 2:
+                todo = [(band0 + pair, 0)]
+            else:
+                todo = [(band0, 0)]
+            for band, col in todo:
+                if band % 4 == 0:
+                    o_t[0] = opool.tile([P, 2, 4, P], F32, name="osb", tag="osb")
+                osb = o_t[0]
+                nc.scalar.activation(
+                    out=osb[:, :, band % 4, :].rearrange("n b (q e) -> n b q e", e=2),
+                    in_=acc[:, col:col + 256].rearrange("n (e b q) -> n b q e", e=2, b=2),
+                    func=ACT.Identity, bias=csb[:, band:band + 1], scale=1.0,
+                )
+                if band % 4 == 3:
+                    nc.sync.dma_start(
+                        out=out[:, :, band - 3:band + 1, :].rearrange("b n k t -> n b (k t)"),
+                        in_=osb[:].rearrange("n b k t -> n b (k t)"),
                     )
-                    if band % 4 == 3:
-                        nc.gpsimd.dma_start(
-                            out=out[:, :, band - 3:band + 1, :].rearrange("b n k t -> n b (k t)"),
-                            in_=osb[:].rearrange("n b k t -> n b (k t)"),
-                        )
 
         ident = const.tile([P, P], F32, name="ident")
         make_identity(nc, ident[:])
-
         load(0)
-
         gbrow = const.tile([P, 512], BF16, name="gbrow")
         nc.scalar.dma_start(out=gbrow[0:16, :], in_=g16)
         nc.scalar.dma_start(out=gbrow[16:32, :], in_=g32.rearrange("k (u c) -> (k u) c", u=2))
@@ -249,6 +332,14 @@ def tile_bandsplitmodule_kernel(
         nc.scalar.dma_start(out=crow[0:16, :], in_=c16)
         nc.scalar.dma_start(out=crow[16:24, :], in_=c32)
         nc.scalar.dma_start(out=crow[24:32, :], in_=c64)
+        load(1)
+        load(2)
+
+        for s in range(4):
+            t1bn(0, s)
+        chain_a(0)
+        chain_b(0)
+        chain_c(0)
 
         gbp = const.tile([P, 4, P], F32, name="gbp")
         nc.vector.tensor_copy(out=gbp[:], in_=gbrow[:].rearrange("r (p j) -> r j p", j=4))
@@ -264,14 +355,61 @@ def tile_bandsplitmodule_kernel(
         csb = const.tile([P, 32], F32, name="csb")
         nc.vector.tensor_copy(out=csb[:], in_=pc[:, 0, 0:32])
 
-        load(1)
-        stats(0)
-        wprep(0)
+        wrg(0)
+        wq(0)
+        wrg(1)
+
         for r in range(ROUNDS):
-            if r + 2 < ROUNDS:
-                load(r + 2)
-            e1(r)
-            if r + 1 < ROUNDS:
-                stats(r + 1)
-                wprep(r + 1)
-            rest(r)
+            nb = round_slots(r)[1]
+            load(r + 3)
+            rg(r - 1, 1)
+            qx(r - 1, 1)
+            wq(r + 1)
+            wrg(r + 2)
+
+            e1(r, 0)
+            oe(r - 1, 0)
+            if nb != 4:
+                t1bn(r + 1, 0)
+            t2(r, 0, 0)
+            t2(r, 0, 1)
+            e1(r, 1)
+            if nb == 4:
+                t1bn(r + 1, 0)
+            t1bn(r + 1, 1)
+            t2(r, 1, 0)
+            mx(r - 1, 1)
+            e1(r, 2)
+            if nb != 4:
+                t1bn(r + 1, 2)
+            e1(r, 3)
+            if nb == 4:
+                t1bn(r + 1, 2)
+            t1bn(r + 1, 3)
+            oe(r - 1, 1)
+            chain_a(r + 1)
+
+            e2(r, 0, 0)
+            t2(r, 1, 1)
+            e2(r, 0, 1)
+            t2(r, 2, 0)
+            e2(r, 1, 0)
+            t2(r, 2, 1)
+            e2(r, 1, 1)
+            t2(r, 3, 0)
+            rg(r, 0)
+            e2(r, 2, 0)
+            t2(r, 3, 1)
+            e2(r, 2, 1)
+            chain_b(r + 1)
+            chain_c(r + 1)
+            qx(r, 0)
+            mx(r, 0)
+            e2(r, 3, 0)
+            e2(r, 3, 1)
+
+        rg(ROUNDS - 1, 1)
+        qx(ROUNDS - 1, 1)
+        oe(ROUNDS - 1, 0)
+        mx(ROUNDS - 1, 1)
+        oe(ROUNDS - 1, 1)

@@ -16,7 +16,7 @@ ALU = mybir.AluOpType
 P = 128
 EPS = 1e-8
 ROUNDS = 16
-W_ON_GPSIMD = True
+LAST = ROUNDS - 1
 
 
 def round_slots(r):
@@ -24,6 +24,10 @@ def round_slots(r):
         return [(0, 2 * r), (1, 2 * r), (0, 2 * r + 1), (1, 2 * r + 1)], (4 if r < 4 else 2)
     a = 16 + 2 * (r - 8)
     return [(0, a), (0, a + 1), (1, a), (1, a + 1)], 1
+
+
+def bands_of(r):
+    return round_slots(r)[1]
 
 
 def first_band(r):
@@ -46,7 +50,7 @@ def tile_bandsplitmodule_kernel(
         wgpool = ctx.enter_context(tc.tile_pool(name="wgpool", bufs=1))
         small = ctx.enter_context(tc.tile_pool(name="small", bufs=3))
         zpool = ctx.enter_context(tc.tile_pool(name="zpool", bufs=6))
-        qpool = ctx.enter_context(tc.tile_pool(name="qpool", bufs=3))
+        qpool = ctx.enter_context(tc.tile_pool(name="qpool", bufs=4))
         opool = ctx.enter_context(tc.tile_pool(name="opool", bufs=2))
         ps1 = ctx.enter_context(tc.psum_pool(name="ps1", bufs=4))
         ps2 = ctx.enter_context(tc.psum_pool(name="ps2", bufs=3))
@@ -100,14 +104,11 @@ def tile_bandsplitmodule_kernel(
             wraw = wraw_t.pop(r)
             wg = wgpool.tile([P, 4, P, 4], BF16, name="wg", tag="wg", align_bytes=64)
             wg_t[r] = wg
-            if W_ON_GPSIMD:
-                for u in range(4):
-                    nc.gpsimd.tensor_scalar(
-                        out=wg[:, u, :, :], in0=wraw[:, u, :].rearrange("p (j n) -> p n j", j=4),
-                        scalar1=1.0, scalar2=0.0, op0=ALU.mult, op1=ALU.add,
-                    )
-            else:
-                nc.vector.tensor_copy(out=wg[:], in_=wraw[:].rearrange("p u (j n) -> p u n j", j=4))
+            for u in range(4):
+                nc.gpsimd.tensor_scalar(
+                    out=wg[:, u, :, :], in0=wraw[:, u, :].rearrange("p (j n) -> p n j", j=4),
+                    scalar1=1.0, scalar2=0.0, op0=ALU.mult, op1=ALU.add,
+                )
 
         def wq(r):
             if r >= ROUNDS:
@@ -151,53 +152,50 @@ def tile_bandsplitmodule_kernel(
             if s == 3:
                 xs_t.pop(r)
 
-        def chain_a(r):
+        def chain_a(r, lo=0, hi=None):
             if r >= ROUNDS:
                 return
-            slots, nb = round_slots(r)
-            st = st_t.pop(r)
-            kk = 2 * nb
+            nb = bands_of(r)
+            hi = nb if hi is None else hi
+            st = st_t[r]
             cpb = 8 // nb
-            mv = small.tile([P, 8, 2], F32, name="mv", tag="mv")
-            for i in range(nb):
+            if lo == 0:
+                stat_t[r] = [
+                    small.tile([P, 8, 2], F32, name="mv", tag="mv"),
+                    small.tile([P, 8], F32, name="sd", tag="sd"),
+                    small.tile([P, 8], F32, name="rs", tag="rs"),
+                    small.tile([P, 8], F32, name="nm", tag="nm"),
+                ]
+            mv = stat_t[r][0]
+            for i in range(lo, hi):
                 for e in range(2):
                     nc.vector.bn_aggr(
                         out=mv[:, 2 * i + e, :],
                         in_=st[:, cpb * i:cpb * (i + 1), 3 * e:3 * e + 3],
                     )
-            ve = small.tile([P, 8], F32, name="ve", tag="ve")
-            nc.vector.tensor_scalar(out=ve[:, 0:kk], in0=mv[:, 0:kk, 1], scalar1=EPS, scalar2=None, op0=ALU.add)
-            stat_t[r] = (mv, ve)
 
-        def chain_b(r):
+        def chain_b(r, lo=0, hi=None):
             if r >= ROUNDS:
                 return
-            slots, nb = round_slots(r)
-            kk = 2 * nb
-            mv, ve = stat_t[r]
-            sd = small.tile([P, 8], F32, name="sd", tag="sd")
-            nc.scalar.activation(out=sd[:, 0:kk], in_=ve[:, 0:kk], func=ACT.Sqrt)
-            stat_t[r] = (mv, sd)
+            hi = bands_of(r) if hi is None else hi
+            mv, sd = stat_t[r][0], stat_t[r][1]
+            nc.scalar.activation(out=sd[:, 2 * lo:2 * hi], in_=mv[:, 2 * lo:2 * hi, 1], func=ACT.Sqrt, bias=EPS, scale=1.0)
 
-        def chain_c(r):
+        def chain_c(r, lo=0, hi=None):
             if r >= ROUNDS:
                 return
-            slots, nb = round_slots(r)
-            kk = 2 * nb
-            mv, sd = stat_t[r]
-            rs = small.tile([P, 8], F32, name="rs", tag="rs")
-            nc.vector.reciprocal(out=rs[:, 0:kk], in_=sd[:, 0:kk])
-            nm = small.tile([P, 8], F32, name="nm", tag="nm")
+            hi = bands_of(r) if hi is None else hi
+            mv, sd, rs, nm = stat_t[r]
+            nc.vector.reciprocal(out=rs[:, 2 * lo:2 * hi], in_=sd[:, 2 * lo:2 * hi])
             nc.vector.scalar_tensor_tensor(
-                out=nm[:, 0:kk], in0=mv[:, 0:kk, 0], scalar=-1.0, in1=rs[:, 0:kk],
+                out=nm[:, 2 * lo:2 * hi], in0=mv[:, 2 * lo:2 * hi, 0], scalar=-1.0, in1=rs[:, 2 * lo:2 * hi],
                 op0=ALU.mult, op1=ALU.mult,
             )
-            stat_t[r] = (rs, nm)
 
         def e1(r, i):
-            slots, nb = round_slots(r)
+            nb = bands_of(r)
             views = p1_t[r]
-            rs, nm = stat_t[r]
+            rs, nm = stat_t[r][2], stat_t[r][3]
             z = zpool.tile([P, 2, 4, P], F32, name="z", tag="z")
             z_t[(r, i)] = z
             for e in range(2):
@@ -240,42 +238,48 @@ def tile_bandsplitmodule_kernel(
                     func=ACT.Identity, scale=gb[:, j, u:u + 1], bias=gb[:, j, 64 + u:65 + u],
                 )
 
-        def rg(r, pair):
+        def rg(r, pair, units=(0, 1)):
             if r < 0:
                 return
-            xp = xp_t.pop((r, pair))
-            xg = qpool.tile([P, 512, 4], BF16, name="xg", tag="xg", align_bytes=64)
-            xg_t[(r, pair)] = xg
+            xp = xp_t[(r, pair)]
+            if units[0] == 0:
+                xg_t[(r, pair)] = qpool.tile([P, 512, 4], BF16, name="xg", tag="xg", align_bytes=64)
+            xg = xg_t[(r, pair)]
+            c0, c1 = 256 * units[0], 256 * units[-1] + 256
             nc.vector.tensor_copy(
-                out=xg[:].rearrange("p (c i) j -> p c j i", i=4),
-                in_=xp[:].rearrange("p j u c -> p j (u c)").rearrange("p j (c i) -> p c j i", i=4),
+                out=xg[:, c0:c1, :].rearrange("p (c i) j -> p c j i", i=4),
+                in_=xp[:].rearrange("p j u c -> p j (u c)")[:, :, c0:c1].rearrange("p j (c i) -> p c j i", i=4),
             )
 
-        def qx(r, pair):
+        def qx(r, pair, units=(0, 1)):
             if r < 0:
                 return
-            xg = xg_t.pop((r, pair))
-            xc = qpool.tile([P, 512], U32, name="xc", tag="xc", align_bytes=64)
-            xsc = qpool.tile([P, 512], U8, name="xsc", tag="xsc", align_bytes=64)
+            xg = xg_t[(r, pair)]
+            if units[0] == 0:
+                xq_t[(r, pair)] = (
+                    qpool.tile([P, 512], U32, name="xc", tag="xc", align_bytes=64),
+                    qpool.tile([P, 512], U8, name="xsc", tag="xsc", align_bytes=64),
+                )
+            xc, xsc = xq_t[(r, pair)]
+            c0, c1 = 256 * units[0], 256 * units[-1] + 256
             nc.vector.quantize_mx(
-                out=xc[:].bitcast(FP8X4), scales=xsc[:],
-                in_=xg[:].rearrange("p c j -> p (c j)"),
+                out=xc[:, c0:c1].bitcast(FP8X4), scales=xsc[:, c0:c1],
+                in_=xg[:, c0:c1, :].rearrange("p c j -> p (c j)"),
             )
-            xq_t[(r, pair)] = (xc, xsc)
 
-        def mx(r, pair):
+        def mx(r, pair, units=(0, 1)):
             if r < 0:
                 return
-            slots, nb = round_slots(r)
+            nb = bands_of(r)
             upb = 4 // nb
             wc, wsc = wq_t[r]
-            xc, xsc = xq_t.pop((r, pair))
-            if pair == 0 or nb > 1:
+            xc, xsc = xq_t[(r, pair)]
+            if units[0] == 0 and (pair == 0 or nb == 4):
                 acc_t[r] = psa.tile([P, 512], F32, name="acc", tag="acc")
             acc = acc_t[r]
-            for il in range(2):
+            for il in units:
                 i = 2 * pair + il
-                col = 256 * il if nb == 4 else 0
+                col = 256 * il if nb == 4 else (256 * pair if nb == 2 else 0)
                 nc.tensor.matmul_mx(
                     out=acc[:, col:col + 256],
                     lhsT=wc[:, i * P:(i + 1) * P].bitcast(FP8X4),
@@ -285,13 +289,11 @@ def tile_bandsplitmodule_kernel(
                     start=(i % upb == 0),
                     stop=(i % upb == upb - 1),
                 )
-            if pair == 1:
-                wq_t.pop(r)
 
         def oe(r, pair):
             if r < 0:
                 return
-            slots, nb = round_slots(r)
+            nb = bands_of(r)
             if nb == 1 and pair == 0:
                 return
             acc = acc_t[r]
@@ -299,19 +301,29 @@ def tile_bandsplitmodule_kernel(
             if nb == 4:
                 todo = [(band0 + 2 * pair, 0), (band0 + 2 * pair + 1, 256)]
             elif nb == 2:
-                todo = [(band0 + pair, 0)]
+                todo = [(band0 + pair, 256 * pair)]
             else:
                 todo = [(band0, 0)]
             for band, col in todo:
                 if band % 4 == 0:
                     o_t[0] = opool.tile([P, 2, 4, P], F32, name="osb", tag="osb")
                 osb = o_t[0]
-                nc.scalar.activation(
+                nc.vector.tensor_scalar(
                     out=osb[:, :, band % 4, :].rearrange("n b (q e) -> n b q e", e=2),
-                    in_=acc[:, col:col + 256].rearrange("n (e b q) -> n b q e", e=2, b=2),
-                    func=ACT.Identity, bias=csb[:, band:band + 1], scale=1.0,
+                    in0=acc[:, col:col + 256].rearrange("n (e b q) -> n b q e", e=2, b=2),
+                    scalar1=csb[:, band:band + 1], scalar2=None, op0=ALU.add,
                 )
-                if band % 4 == 3:
+                if band == 30:
+                    nc.sync.dma_start(
+                        out=out[:, :, 28:31, :].rearrange("b n k t -> n b (k t)"),
+                        in_=osb[:, :, 0:3, :].rearrange("n b k t -> n b (k t)"),
+                    )
+                elif band == 31:
+                    nc.sync.dma_start(
+                        out=out[:, :, 31, :].rearrange("b n t -> n b t"),
+                        in_=osb[:, :, 3, :],
+                    )
+                elif band % 4 == 3:
                     nc.sync.dma_start(
                         out=out[:, :, band - 3:band + 1, :].rearrange("b n k t -> n b (k t)"),
                         in_=osb[:].rearrange("n b k t -> n b (k t)"),
@@ -335,23 +347,28 @@ def tile_bandsplitmodule_kernel(
         load(1)
         load(2)
 
-        for s in range(4):
-            t1bn(0, s)
-        chain_a(0)
-        chain_b(0)
-        chain_c(0)
+        t1bn(0, 0)
+        t1bn(0, 1)
+        chain_a(0, 0, 2)
+        chain_b(0, 0, 2)
+        chain_c(0, 0, 2)
 
         gbp = const.tile([P, 4, P], F32, name="gbp")
         nc.vector.tensor_copy(out=gbp[:], in_=gbrow[:].rearrange("r (p j) -> r j p", j=4))
         pg = ps2.tile([P, 4, P], F32, name="pg", tag="p2")
         for j in range(4):
             nc.tensor.transpose(pg[:, j, :], gbp[:, j, :], ident[:])
-        gb = const.tile([P, 4, P], F32, name="gb")
-        nc.vector.tensor_copy(out=gb[:], in_=pg[:])
         crf = const.tile([P, P], F32, name="crf")
         nc.vector.tensor_copy(out=crf[:], in_=crow[:])
         pc = ps2.tile([P, 4, P], F32, name="pc", tag="p2")
         nc.tensor.transpose(pc[:, 0, :], crf[:], ident[:])
+
+        t1bn(0, 2)
+        t1bn(0, 3)
+        chain_a(0, 2, 4)
+
+        gb = const.tile([P, 4, P], F32, name="gb")
+        nc.vector.tensor_copy(out=gb[:], in_=pg[:])
         csb = const.tile([P, 32], F32, name="csb")
         nc.vector.tensor_copy(out=csb[:], in_=pc[:, 0, 0:32])
 
@@ -360,33 +377,43 @@ def tile_bandsplitmodule_kernel(
         wrg(1)
 
         for r in range(ROUNDS):
-            nb = round_slots(r)[1]
+            nb = bands_of(r)
+            prev4 = r > 0 and bands_of(r - 1) == 4
             load(r + 3)
             rg(r - 1, 1)
             qx(r - 1, 1)
             wq(r + 1)
             wrg(r + 2)
+            if prev4:
+                oe(r - 1, 0)
+            elif r > 1 and bands_of(r - 2) != 4:
+                oe(r - 2, 0)
+                oe(r - 2, 1)
 
             e1(r, 0)
-            oe(r - 1, 0)
             if nb != 4:
                 t1bn(r + 1, 0)
             t2(r, 0, 0)
             t2(r, 0, 1)
             e1(r, 1)
+            if r == 0:
+                chain_b(0, 2, 4)
+                chain_c(0, 2, 4)
             if nb == 4:
                 t1bn(r + 1, 0)
             t1bn(r + 1, 1)
             t2(r, 1, 0)
-            mx(r - 1, 1)
+            if prev4:
+                mx(r - 1, 1)
             e1(r, 2)
             if nb != 4:
                 t1bn(r + 1, 2)
             e1(r, 3)
             if nb == 4:
                 t1bn(r + 1, 2)
+            if prev4:
+                oe(r - 1, 1)
             t1bn(r + 1, 3)
-            oe(r - 1, 1)
             chain_a(r + 1)
 
             e2(r, 0, 0)
@@ -404,12 +431,21 @@ def tile_bandsplitmodule_kernel(
             chain_b(r + 1)
             chain_c(r + 1)
             qx(r, 0)
-            mx(r, 0)
+            if nb == 4:
+                mx(r, 0)
+            elif not prev4:
+                mx(r - 1, 0)
+                mx(r - 1, 1)
+            if r == LAST:
+                oe(r - 1, 1)
+                mx(r, 0)
+                rg(r, 1, (0,))
+                qx(r, 1, (0,))
+                mx(r, 1, (0,))
             e2(r, 3, 0)
             e2(r, 3, 1)
 
-        rg(ROUNDS - 1, 1)
-        qx(ROUNDS - 1, 1)
-        oe(ROUNDS - 1, 0)
-        mx(ROUNDS - 1, 1)
-        oe(ROUNDS - 1, 1)
+        rg(LAST, 1, (1,))
+        qx(LAST, 1, (1,))
+        mx(LAST, 1, (1,))
+        oe(LAST, 1)

@@ -17,6 +17,7 @@ P = 128
 EPS = 1e-8
 ROUNDS = 16
 LAST = ROUNDS - 1
+SHARE = (0, 1, 2, 3, 4, 5, 6, 7, 8, 9, 10, 11, 12, 13, 14, 15)
 
 
 def round_slots(r):
@@ -51,6 +52,7 @@ def tile_bandsplitmodule_kernel(
         small = ctx.enter_context(tc.tile_pool(name="small", bufs=3))
         zpool = ctx.enter_context(tc.tile_pool(name="zpool", bufs=6))
         qpool = ctx.enter_context(tc.tile_pool(name="qpool", bufs=4))
+        gpool = ctx.enter_context(tc.tile_pool(name="gpool", bufs=2))
         opool = ctx.enter_context(tc.tile_pool(name="opool", bufs=2))
         ps1 = ctx.enter_context(tc.psum_pool(name="ps1", bufs=4))
         ps2 = ctx.enter_context(tc.psum_pool(name="ps2", bufs=3))
@@ -225,7 +227,9 @@ def tile_bandsplitmodule_kernel(
             if jp == 1:
                 z_t.pop((r, i))
 
-        def e2(r, i, jp):
+        def e2(r, i, jp, on_vector=False):
+            if r < 0:
+                return
             u = 4 * r + i
             if i % 2 == 0 and jp == 0:
                 xp_t[(r, i // 2)] = qpool.tile([P, 4, 2, 256], BF16, name="xp", tag="xp")
@@ -233,59 +237,74 @@ def tile_bandsplitmodule_kernel(
             p2 = p2_t.pop((r, i, jp))
             for jl in range(2):
                 j = 2 * jp + jl
-                nc.scalar.activation(
-                    out=xp[:, j, i % 2, :], in_=p2[:, jl, :, :].rearrange("p e q -> p (e q)"),
-                    func=ACT.Identity, scale=gb[:, j, u:u + 1], bias=gb[:, j, 64 + u:65 + u],
-                )
+                if on_vector:
+                    nc.vector.tensor_scalar(
+                        out=xp[:, j, i % 2, :], in0=p2[:, jl, :, :].rearrange("p e q -> p (e q)"),
+                        scalar1=gb[:, j, u:u + 1], scalar2=gb[:, j, 64 + u:65 + u], op0=ALU.mult, op1=ALU.add,
+                    )
+                else:
+                    nc.scalar.activation(
+                        out=xp[:, j, i % 2, :], in_=p2[:, jl, :, :].rearrange("p e q -> p (e q)"),
+                        func=ACT.Identity, scale=gb[:, j, u:u + 1], bias=gb[:, j, 64 + u:65 + u],
+                    )
 
-        def rg(r, pair, units=(0, 1)):
+        def rg(r, u0, u1, on_gpsimd=False):
             if r < 0:
                 return
-            xp = xp_t[(r, pair)]
-            if units[0] == 0:
-                xg_t[(r, pair)] = qpool.tile([P, 512, 4], BF16, name="xg", tag="xg", align_bytes=64)
-            xg = xg_t[(r, pair)]
-            c0, c1 = 256 * units[0], 256 * units[-1] + 256
-            nc.vector.tensor_copy(
-                out=xg[:, c0:c1, :].rearrange("p (c i) j -> p c j i", i=4),
-                in_=xp[:].rearrange("p j u c -> p j (u c)")[:, :, c0:c1].rearrange("p j (c i) -> p c j i", i=4),
-            )
+            if u0 == 0:
+                xg_t[r] = gpool.tile([P, 1024, 4], BF16, name="xg", tag="xg", align_bytes=64)
+            xg = xg_t[r]
+            if on_gpsimd:
+                for i in range(u0, u1):
+                    nc.gpsimd.tensor_scalar(
+                        out=xg[:, 256 * i:256 * i + 256, :],
+                        in0=xp_t[(r, i // 2)][:, :, i % 2, :].rearrange("p j c -> p c j"),
+                        scalar1=1.0, scalar2=0.0, op0=ALU.mult, op1=ALU.add,
+                    )
+            elif u1 - u0 == 2:
+                nc.vector.tensor_copy(
+                    out=xg[:, 256 * u0:256 * u1, :].rearrange("p (c i) j -> p c j i", i=4),
+                    in_=xp_t[(r, u0 // 2)][:].rearrange("p j u c -> p j (u c)").rearrange("p j (c i) -> p c j i", i=4),
+                )
+            else:
+                nc.vector.tensor_copy(
+                    out=xg[:, 256 * u0:256 * u1, :].rearrange("p (c i) j -> p c j i", i=4),
+                    in_=xp_t[(r, u0 // 2)][:, :, u0 % 2, :].rearrange("p j (c i) -> p c j i", i=4),
+                )
 
-        def qx(r, pair, units=(0, 1)):
+        def qx(r, u0, u1):
             if r < 0:
                 return
-            xg = xg_t[(r, pair)]
-            if units[0] == 0:
-                xq_t[(r, pair)] = (
-                    qpool.tile([P, 512], U32, name="xc", tag="xc", align_bytes=64),
-                    qpool.tile([P, 512], U8, name="xsc", tag="xsc", align_bytes=64),
+            xg = xg_t[r]
+            if u0 == 0:
+                xq_t[r] = (
+                    gpool.tile([P, 1024], U32, name="xc", tag="xc", align_bytes=64),
+                    gpool.tile([P, 1024], U8, name="xsc", tag="xsc", align_bytes=64),
                 )
-            xc, xsc = xq_t[(r, pair)]
-            c0, c1 = 256 * units[0], 256 * units[-1] + 256
+            xc, xsc = xq_t[r]
             nc.vector.quantize_mx(
-                out=xc[:, c0:c1].bitcast(FP8X4), scales=xsc[:, c0:c1],
-                in_=xg[:, c0:c1, :].rearrange("p c j -> p (c j)"),
+                out=xc[:, 256 * u0:256 * u1].bitcast(FP8X4), scales=xsc[:, 256 * u0:256 * u1],
+                in_=xg[:, 256 * u0:256 * u1, :].rearrange("p c j -> p (c j)"),
             )
 
-        def mx(r, pair, units=(0, 1)):
+        def mx(r, u0, u1):
             if r < 0:
                 return
             nb = bands_of(r)
             upb = 4 // nb
             wc, wsc = wq_t[r]
-            xc, xsc = xq_t[(r, pair)]
-            if units[0] == 0 and (pair == 0 or nb == 4):
-                acc_t[r] = psa.tile([P, 512], F32, name="acc", tag="acc")
-            acc = acc_t[r]
-            for il in units:
-                i = 2 * pair + il
-                col = 256 * il if nb == 4 else (256 * pair if nb == 2 else 0)
+            xc, xsc = xq_t[r]
+            for i in range(u0, u1):
+                if i == 0 or (nb == 4 and i == 2):
+                    acc_t[r] = psa.tile([P, 512], F32, name="acc", tag="acc")
+                acc = acc_t[r]
+                col = 256 * (i % 2) if nb == 4 else (256 * (i // 2) if nb == 2 else 0)
                 nc.tensor.matmul_mx(
                     out=acc[:, col:col + 256],
                     lhsT=wc[:, i * P:(i + 1) * P].bitcast(FP8X4),
                     lhsT_scale=wsc[:, i * P:(i + 1) * P],
-                    rhs=xc[:, 256 * il:256 * il + 256].bitcast(FP8X4),
-                    rhs_scale=xsc[:, 256 * il:256 * il + 256],
+                    rhs=xc[:, 256 * i:256 * i + 256].bitcast(FP8X4),
+                    rhs_scale=xsc[:, 256 * i:256 * i + 256],
                     start=(i % upb == 0),
                     stop=(i % upb == upb - 1),
                 )
@@ -374,21 +393,19 @@ def tile_bandsplitmodule_kernel(
 
         wrg(0)
         wq(0)
-        wrg(1)
 
         for r in range(ROUNDS):
             nb = bands_of(r)
-            prev4 = r > 0 and bands_of(r - 1) == 4
+            old4 = r > 1 and bands_of(r - 2) == 4
+            last = r == LAST
             load(r + 3)
-            rg(r - 1, 1)
-            qx(r - 1, 1)
-            wq(r + 1)
-            wrg(r + 2)
-            if prev4:
-                oe(r - 1, 0)
-            elif r > 1 and bands_of(r - 2) != 4:
-                oe(r - 2, 0)
+            oe(r - 2, 0)
+            if not old4:
                 oe(r - 2, 1)
+            if r - 1 in SHARE:
+                e2(r - 1, 3, 1, True)
+            wrg(r + 1)
+            rg(r - 1, 2, 4, not last)
 
             e1(r, 0)
             if nb != 4:
@@ -403,49 +420,60 @@ def tile_bandsplitmodule_kernel(
                 t1bn(r + 1, 0)
             t1bn(r + 1, 1)
             t2(r, 1, 0)
-            if prev4:
-                mx(r - 1, 1)
+            if old4:
+                mx(r - 2, 2, 4)
+            if last:
+                qx(r - 1, 0, 4)
+                mx(r - 1, 0, 4)
             e1(r, 2)
             if nb != 4:
                 t1bn(r + 1, 2)
             e1(r, 3)
             if nb == 4:
                 t1bn(r + 1, 2)
-            if prev4:
-                oe(r - 1, 1)
+            if old4:
+                oe(r - 2, 1)
             t1bn(r + 1, 3)
             chain_a(r + 1)
+            if last:
+                oe(r - 1, 1)
 
             e2(r, 0, 0)
             t2(r, 1, 1)
             e2(r, 0, 1)
             t2(r, 2, 0)
+            if last:
+                rg(r, 0, 1)
             e2(r, 1, 0)
             t2(r, 2, 1)
             e2(r, 1, 1)
             t2(r, 3, 0)
-            rg(r, 0)
+            chain_b(r + 1)
+            if not last:
+                qx(r - 1, 0, 4)
+                chain_c(r + 1)
+                rg(r, 0, 2)
+                wq(r + 1)
+            else:
+                rg(r, 1, 2)
+                qx(r, 0, 2)
+                mx(r, 0, 2)
             e2(r, 2, 0)
             t2(r, 3, 1)
             e2(r, 2, 1)
-            chain_b(r + 1)
-            chain_c(r + 1)
-            qx(r, 0)
-            if nb == 4:
-                mx(r, 0)
-            elif not prev4:
-                mx(r - 1, 0)
-                mx(r - 1, 1)
-            if r == LAST:
-                oe(r - 1, 1)
-                mx(r, 0)
-                rg(r, 1, (0,))
-                qx(r, 1, (0,))
-                mx(r, 1, (0,))
+            if last:
+                rg(r, 2, 3)
+                qx(r, 2, 3)
+                mx(r, 2, 3)
             e2(r, 3, 0)
-            e2(r, 3, 1)
+            if r not in SHARE:
+                e2(r, 3, 1)
+            if not last:
+                mx(r - 1, 0, 2 if (r > 0 and bands_of(r - 1) == 4) else 4)
 
-        rg(LAST, 1, (1,))
-        qx(LAST, 1, (1,))
-        mx(LAST, 1, (1,))
+        if LAST in SHARE:
+            e2(LAST, 3, 1, True)
+        rg(LAST, 3, 4)
+        qx(LAST, 3, 4)
+        mx(LAST, 3, 4)
         oe(LAST, 1)

@@ -100,13 +100,14 @@ def tile_bandsplitmodule_kernel(
                 wsrc = W64[r - 8].rearrange("(u p j) n -> p u (j n)", u=4, j=4)
             nc.sync.dma_start(out=wraw[:], in_=wsrc)
 
-        def wrg(r):
+        def wrg(r, u0=0, u1=4):
             if r >= ROUNDS:
                 return
-            wraw = wraw_t.pop(r)
-            wg = wgpool.tile([P, 4, P, 4], BF16, name="wg", tag="wg", align_bytes=64)
-            wg_t[r] = wg
-            for u in range(4):
+            wraw = wraw_t[r]
+            if u0 == 0:
+                wg_t[r] = wgpool.tile([P, 4, P, 4], BF16, name="wg", tag="wg", align_bytes=64)
+            wg = wg_t[r]
+            for u in range(u0, u1):
                 nc.gpsimd.tensor_scalar(
                     out=wg[:, u, :, :], in0=wraw[:, u, :].rearrange("p (j n) -> p n j", j=4),
                     scalar1=1.0, scalar2=0.0, op0=ALU.mult, op1=ALU.add,
@@ -404,22 +405,22 @@ def tile_bandsplitmodule_kernel(
                 oe(r - 2, 1)
             if r - 1 in SHARE:
                 e2(r - 1, 3, 1, True)
-            wrg(r + 1)
+            wrg(r + 1, 0, 1)
             rg(r - 1, 2, 4, not last)
+            wrg(r + 1, 1, 4)
 
             e1(r, 0)
             if nb != 4:
                 t1bn(r + 1, 0)
             t2(r, 0, 0)
-            t2(r, 0, 1)
             e1(r, 1)
             if r == 0:
                 chain_b(0, 2, 4)
                 chain_c(0, 2, 4)
+            t1bn(r + 1, 0 if nb == 4 else 1)
+            t2(r, 0, 1)
             if nb == 4:
-                t1bn(r + 1, 0)
-            t1bn(r + 1, 1)
-            t2(r, 1, 0)
+                t1bn(r + 1, 1)
             if old4:
                 mx(r - 2, 2, 4)
             if last:
@@ -428,6 +429,7 @@ def tile_bandsplitmodule_kernel(
             e1(r, 2)
             if nb != 4:
                 t1bn(r + 1, 2)
+            t2(r, 1, 0)
             e1(r, 3)
             if nb == 4:
                 t1bn(r + 1, 2)

@@ -14,29 +14,20 @@ ACT = mybir.ActivationFunctionType
 ALU = mybir.AluOpType
 
 P = 128
+PACK = 4
+COLS = 256
 EPS = 1e-8
 ROUNDS = 16
 LAST = ROUNDS - 1
-SHARE = (0, 1, 2, 3, 4, 5, 6, 7, 8, 9, 10, 11, 12, 13, 14, 15)
+PASSES = 4
 
 
-def round_slots(r):
-    if r < 8:
-        return [(0, 2 * r), (1, 2 * r), (0, 2 * r + 1), (1, 2 * r + 1)], (4 if r < 4 else 2)
-    a = 16 + 2 * (r - 8)
-    return [(0, a), (0, a + 1), (1, a), (1, a + 1)], 1
-
-
-def bands_of(r):
-    return round_slots(r)[1]
+def bands_in(r):
+    return 4 if r < 4 else (2 if r < 8 else 1)
 
 
 def first_band(r):
-    if r < 4:
-        return 4 * r
-    if r < 8:
-        return 16 + 2 * (r - 4)
-    return 24 + (r - 8)
+    return 4 * r if r < 4 else (2 * r + 8 if r < 8 else r + 16)
 
 
 def tile_bandsplitmodule_kernel(
@@ -51,431 +42,354 @@ def tile_bandsplitmodule_kernel(
         wgpool = ctx.enter_context(tc.tile_pool(name="wgpool", bufs=1))
         small = ctx.enter_context(tc.tile_pool(name="small", bufs=3))
         zpool = ctx.enter_context(tc.tile_pool(name="zpool", bufs=6))
-        qpool = ctx.enter_context(tc.tile_pool(name="qpool", bufs=4))
+        ppool = ctx.enter_context(tc.tile_pool(name="ppool", bufs=4))
         gpool = ctx.enter_context(tc.tile_pool(name="gpool", bufs=2))
         opool = ctx.enter_context(tc.tile_pool(name="opool", bufs=2))
-        ps1 = ctx.enter_context(tc.psum_pool(name="ps1", bufs=4))
-        ps2 = ctx.enter_context(tc.psum_pool(name="ps2", bufs=3))
-        psa = ctx.enter_context(tc.psum_pool(name="psa", bufs=1))
+        ps_x = ctx.enter_context(tc.psum_pool(name="ps_x", bufs=4))
+        ps_z = ctx.enter_context(tc.psum_pool(name="ps_z", bufs=3))
+        ps_y = ctx.enter_context(tc.psum_pool(name="ps_y", bufs=1))
         ctx.enter_context(tc.manual_schedule())
 
-        xs_t = {}
-        wraw_t = {}
-        wg_t = {}
-        wq_t = {}
-        p1_t = {}
-        st_t = {}
-        stat_t = {}
-        z_t = {}
-        p2_t = {}
-        xp_t = {}
-        xg_t = {}
-        xq_t = {}
-        acc_t = {}
-        o_t = {}
+        x_sb, w_raw, w_grouped, w_mx = {}, {}, {}, {}
+        x_frames, pieces, stats = {}, {}, {}
+        z_sb, z_chan, xn_planes, xn_grouped, xn_mx, sums, out_sb = {}, {}, {}, {}, {}, {}, {}
 
-        def load(r):
-            if r >= ROUNDS:
+        def load_round(r):
+            if r > LAST:
                 return
-            slots, nb = round_slots(r)
-            xs = xpool.tile([P, 4096], BF16, name="xs", tag="xs")
-            xs_t[r] = xs
-            xv = xs[:].rearrange("p (s j b t) -> p s j b t", s=4, j=4, b=2)
-            for s in range(4):
-                imag, a = slots[s]
-                src = x_imag if imag else x_real
-                for b in range(2):
-                    nc.sync.dma_start(
-                        out=xv[:, s, :, b, :],
-                        in_=src[b, 512 * a:512 * a + 512, :].rearrange("(p j) t -> p j t", j=4),
-                    )
-            wraw = wpool.tile([P, 4, 512], BF16, name="wraw", tag="wraw")
-            wraw_t[r] = wraw
-            if r < 4:
-                wsrc = W16[4 * r:4 * r + 4].rearrange("k (p j) n -> p k (j n)", j=4)
-            elif r < 8:
-                k0 = 2 * (r - 4)
-                wsrc = W32[k0:k0 + 2].rearrange("k (u p j) n -> p (k u) (j n)", u=2, j=4)
+            nb = bands_in(r)
+            x_sb[r] = xpool.tile([P, PASSES * PACK * COLS], BF16, name="x_sb", tag="x_sb")
+            xv = x_sb[r][:].rearrange("p (s j b t) -> p s j b t", s=PASSES, j=PACK, b=2)
+            for s in range(PASSES):
+                if nb == 4:
+                    parts = [(x_real, 1024 * r + 256 * s, 0, 64), (x_imag, 1024 * r + 256 * s, 64, 64)]
+                elif nb == 2:
+                    parts = [((x_real, x_imag)[s % 2], 1024 * r + 512 * (s // 2), 0, P)]
+                else:
+                    parts = [((x_real, x_imag)[s // 2], 1024 * r + 512 * (s % 2), 0, P)]
+                for src, bin0, p0, n in parts:
+                    for b in range(2):
+                        nc.sync.dma_start(
+                            out=xv[p0:p0 + n, s, :, b, :],
+                            in_=src[b, bin0:bin0 + PACK * n, :].rearrange("(p j) t -> p j t", j=PACK),
+                        )
+            w_raw[r] = wpool.tile([P, PASSES, PACK * P], BF16, name="w_raw", tag="w_raw")
+            if nb == 4:
+                w_rows = W16[4 * r:4 * r + 4].rearrange("k (p j) n -> p k (j n)", j=PACK)
+            elif nb == 2:
+                w_rows = W32[2 * r - 8:2 * r - 6].rearrange("k (s p j) n -> p (k s) (j n)", s=2, j=PACK)
             else:
-                wsrc = W64[r - 8].rearrange("(u p j) n -> p u (j n)", u=4, j=4)
-            nc.sync.dma_start(out=wraw[:], in_=wsrc)
+                w_rows = W64[r - 8].rearrange("(s p j) n -> p s (j n)", s=PASSES, j=PACK)
+            nc.sync.dma_start(out=w_raw[r][:], in_=w_rows)
 
-        def wrg(r, u0=0, u1=4):
-            if r >= ROUNDS:
+        def copy_w(r, s0, s1):
+            if r > LAST:
                 return
-            wraw = wraw_t[r]
-            if u0 == 0:
-                wg_t[r] = wgpool.tile([P, 4, P, 4], BF16, name="wg", tag="wg", align_bytes=64)
-            wg = wg_t[r]
-            for u in range(u0, u1):
-                nc.gpsimd.tensor_scalar(
-                    out=wg[:, u, :, :], in0=wraw[:, u, :].rearrange("p (j n) -> p n j", j=4),
-                    scalar1=1.0, scalar2=0.0, op0=ALU.mult, op1=ALU.add,
+            if s0 == 0:
+                w_grouped[r] = wgpool.tile([P, PASSES, P, PACK], BF16, name="w_grouped", tag="w_grouped", align_bytes=64)
+            nc.gpsimd.tensor_scalar(
+                out=w_grouped[r][:, s0:s1, :, :],
+                in0=w_raw[r][:, s0:s1, :].rearrange("p s (j n) -> p s n j", j=PACK),
+                scalar1=1.0, scalar2=0.0, op0=ALU.mult, op1=ALU.add,
+            )
+
+        def quantise_w(r):
+            if r > LAST:
+                return
+            codes = wpool.tile([P, PASSES * P], U32, name="w_codes", tag="w_codes", align_bytes=64)
+            scales = wpool.tile([P, PASSES * P], U8, name="w_scales", tag="w_scales", align_bytes=64)
+            nc.vector.quantize_mx(
+                out=codes[:].bitcast(FP8X4), scales=scales[:],
+                in_=w_grouped[r][:].rearrange("p s n j -> p (s n j)"),
+            )
+            w_mx[r] = (codes, scales)
+
+        def to_frames(r, s):
+            if r > LAST:
+                return
+            if s == 0:
+                pieces[r] = small.tile([P, 2 * PASSES, 6], F32, name="pieces", tag="pieces")
+                x_frames[r] = []
+            words = x_sb[r][:].bitcast(F32)
+            bank = ps_x.tile([P, PACK * P], F32, name="x_bank", tag="x_bank")
+            for j in range(PACK):
+                c0 = (s * PACK + j) * P
+                nc.tensor.transpose(bank[:, j * P:(j + 1) * P], words[:, c0:c0 + P], ident[:])
+            view = bank[:].bitcast(BF16).rearrange("q (j p e) -> q j p e", j=PACK, e=2)
+            x_frames[r].append(view)
+            for h in range(2):
+                nc.vector.bn_stats(
+                    out=pieces[r][:, 2 * s + h, :],
+                    in_=view[:, 2 * h:2 * h + 2, :, :].rearrange("q j p e -> q (j p e)"),
                 )
 
-        def wq(r):
-            if r >= ROUNDS:
+        def stats_join(r, k0, k1):
+            if r > LAST:
                 return
-            wg = wg_t.pop(r)
-            wc = wpool.tile([P, 512], U32, name="wc", tag="wc", align_bytes=64)
-            wsc = wpool.tile([P, 512], U8, name="wsc", tag="wsc", align_bytes=64)
-            nc.vector.quantize_mx(
-                out=wc[:].bitcast(FP8X4), scales=wsc[:],
-                in_=wg[:].rearrange("p u n j -> p (u n j)"),
-            )
-            wq_t[r] = (wc, wsc)
-
-        def t1bn(r, s):
-            if r >= ROUNDS:
-                return
-            slots, nb = round_slots(r)
-            if s == 0:
-                st_t[r] = small.tile([P, 8, 6], F32, name="st", tag="st")
-                p1_t[r] = []
-            st = st_t[r]
-            xw = xs_t[r][:].bitcast(F32)
-            p1 = ps1.tile([P, 512], F32, name="p1", tag="p1")
-            for j in range(4):
-                c0 = (s * 4 + j) * P
-                nc.tensor.transpose(p1[:, j * P:(j + 1) * P], xw[:, c0:c0 + P], ident[:])
-            v = p1[:].bitcast(BF16).rearrange("q (j p e) -> q j p e", j=4, e=2)
-            p1_t[r].append(v)
-            for h in range(2):
-                if nb == 4:
-                    idx = 2 * (2 * (s // 2) + h) + s % 2
-                    nc.vector.bn_stats(
-                        out=st[:, idx, :],
-                        in_=v[:, :, 64 * h:64 * h + 64, :].rearrange("q j p e -> q j (p e)"),
-                    )
-                else:
-                    nc.vector.bn_stats(
-                        out=st[:, 2 * s + h, :],
-                        in_=v[:, 2 * h:2 * h + 2, :, :].rearrange("q j p e -> q (j p e)"),
-                    )
-            if s == 3:
-                xs_t.pop(r)
-
-        def chain_a(r, lo=0, hi=None):
-            if r >= ROUNDS:
-                return
-            nb = bands_of(r)
-            hi = nb if hi is None else hi
-            st = st_t[r]
-            cpb = 8 // nb
-            if lo == 0:
-                stat_t[r] = [
-                    small.tile([P, 8, 2], F32, name="mv", tag="mv"),
-                    small.tile([P, 8], F32, name="sd", tag="sd"),
-                    small.tile([P, 8], F32, name="rs", tag="rs"),
-                    small.tile([P, 8], F32, name="nm", tag="nm"),
+            per_band = 2 * PASSES // bands_in(r)
+            if k0 == 0:
+                stats[r] = [
+                    small.tile([P, 8, 2], F32, name="mean_var", tag="mean_var"),
+                    small.tile([P, 8], F32, name="std", tag="std"),
+                    small.tile([P, 8], F32, name="rstd", tag="rstd"),
+                    small.tile([P, 8], F32, name="shift", tag="shift"),
                 ]
-            mv = stat_t[r][0]
-            for i in range(lo, hi):
+            for k in range(k0, k1):
                 for e in range(2):
                     nc.vector.bn_aggr(
-                        out=mv[:, 2 * i + e, :],
-                        in_=st[:, cpb * i:cpb * (i + 1), 3 * e:3 * e + 3],
+                        out=stats[r][0][:, 2 * k + e, :],
+                        in_=pieces[r][:, per_band * k:per_band * (k + 1), 3 * e:3 * e + 3],
                     )
 
-        def chain_b(r, lo=0, hi=None):
-            if r >= ROUNDS:
+        def stats_sqrt(r, k0, k1):
+            if r > LAST:
                 return
-            hi = bands_of(r) if hi is None else hi
-            mv, sd = stat_t[r][0], stat_t[r][1]
-            nc.scalar.activation(out=sd[:, 2 * lo:2 * hi], in_=mv[:, 2 * lo:2 * hi, 1], func=ACT.Sqrt, bias=EPS, scale=1.0)
-
-        def chain_c(r, lo=0, hi=None):
-            if r >= ROUNDS:
-                return
-            hi = bands_of(r) if hi is None else hi
-            mv, sd, rs, nm = stat_t[r]
-            nc.vector.reciprocal(out=rs[:, 2 * lo:2 * hi], in_=sd[:, 2 * lo:2 * hi])
-            nc.vector.scalar_tensor_tensor(
-                out=nm[:, 2 * lo:2 * hi], in0=mv[:, 2 * lo:2 * hi, 0], scalar=-1.0, in1=rs[:, 2 * lo:2 * hi],
-                op0=ALU.mult, op1=ALU.mult,
+            nc.scalar.activation(
+                out=stats[r][1][:, 2 * k0:2 * k1], in_=stats[r][0][:, 2 * k0:2 * k1, 1],
+                func=ACT.Sqrt, bias=EPS, scale=1.0,
             )
 
-        def e1(r, i):
-            nb = bands_of(r)
-            views = p1_t[r]
-            rs, nm = stat_t[r][2], stat_t[r][3]
-            z = zpool.tile([P, 2, 4, P], F32, name="z", tag="z")
-            z_t[(r, i)] = z
-            for e in range(2):
-                if nb == 4:
-                    a, h = i // 2, i % 2
-                    k = 2 * i + e
-                    for part in range(2):
-                        nc.scalar.activation(
-                            out=z[:, e, :, 64 * part:64 * part + 64],
-                            in_=views[2 * a + part][:, :, 64 * h:64 * h + 64, e],
-                            func=ACT.Identity, scale=rs[:, k:k + 1], bias=nm[:, k:k + 1],
-                        )
-                else:
-                    k = 2 * (i * nb // 4) + e
-                    nc.scalar.activation(
-                        out=z[:, e, :, :], in_=views[i][:, :, :, e],
-                        func=ACT.Identity, scale=rs[:, k:k + 1], bias=nm[:, k:k + 1],
-                    )
+        def stats_finish(r, k0, k1):
+            if r > LAST:
+                return
+            mean_var, std, rstd, shift = stats[r]
+            nc.vector.reciprocal(out=rstd[:, 2 * k0:2 * k1], in_=std[:, 2 * k0:2 * k1])
+            nc.vector.scalar_tensor_tensor(
+                out=shift[:, 2 * k0:2 * k1], in0=mean_var[:, 2 * k0:2 * k1, 0], scalar=-1.0,
+                in1=rstd[:, 2 * k0:2 * k1], op0=ALU.mult, op1=ALU.mult,
+            )
 
-        def t2(r, i, jp):
-            z = z_t[(r, i)]
-            p2 = ps2.tile([P, 2, 2, P], F32, name="p2", tag="p2")
-            p2_t[(r, i, jp)] = p2
+        def normalise(r, s):
+            rstd, shift = stats[r][2], stats[r][3]
+            z_sb[(r, s)] = zpool.tile([P, 2, PACK, P], F32, name="z_sb", tag="z_sb")
+            for e in range(2):
+                col = 2 * (s * bands_in(r) // PASSES) + e
+                nc.scalar.activation(
+                    out=z_sb[(r, s)][:, e, :, :], in_=x_frames[r][s][:, :, :, e],
+                    func=ACT.Identity, scale=rstd[:, col:col + 1], bias=shift[:, col:col + 1],
+                )
+
+        def to_channels(r, s, half):
+            bank = ps_z.tile([P, 2, 2, P], F32, name="z_bank", tag="z_bank")
+            z_chan[(r, s, half)] = bank
             for jl in range(2):
                 for e in range(2):
-                    nc.tensor.transpose(p2[:, jl, e, :], z[:, e, 2 * jp + jl, :], ident[:])
-            if jp == 1:
-                z_t.pop((r, i))
+                    nc.tensor.transpose(bank[:, jl, e, :], z_sb[(r, s)][:, e, 2 * half + jl, :], ident[:])
 
-        def e2(r, i, jp, on_vector=False):
+        def gain_shift(r, s, half, on_vector=False):
             if r < 0:
                 return
-            u = 4 * r + i
-            if i % 2 == 0 and jp == 0:
-                xp_t[(r, i // 2)] = qpool.tile([P, 4, 2, 256], BF16, name="xp", tag="xp")
-            xp = xp_t[(r, i // 2)]
-            p2 = p2_t.pop((r, i, jp))
+            if s % 2 == 0 and half == 0:
+                xn_planes[(r, s // 2)] = ppool.tile([P, PACK, 2, COLS], BF16, name="xn_planes", tag="xn_planes")
+            n = PASSES * r + s
             for jl in range(2):
-                j = 2 * jp + jl
+                j = 2 * half + jl
+                dst = xn_planes[(r, s // 2)][:, j, s % 2, :]
+                src = z_chan[(r, s, half)][:, jl, :, :].rearrange("p e q -> p (e q)")
                 if on_vector:
                     nc.vector.tensor_scalar(
-                        out=xp[:, j, i % 2, :], in0=p2[:, jl, :, :].rearrange("p e q -> p (e q)"),
-                        scalar1=gb[:, j, u:u + 1], scalar2=gb[:, j, 64 + u:65 + u], op0=ALU.mult, op1=ALU.add,
+                        out=dst, in0=src, scalar1=gain_bias[:, j, n:n + 1], scalar2=gain_bias[:, j, 64 + n:65 + n],
+                        op0=ALU.mult, op1=ALU.add,
                     )
                 else:
                     nc.scalar.activation(
-                        out=xp[:, j, i % 2, :], in_=p2[:, jl, :, :].rearrange("p e q -> p (e q)"),
-                        func=ACT.Identity, scale=gb[:, j, u:u + 1], bias=gb[:, j, 64 + u:65 + u],
+                        out=dst, in_=src, func=ACT.Identity,
+                        scale=gain_bias[:, j, n:n + 1], bias=gain_bias[:, j, 64 + n:65 + n],
                     )
 
-        def rg(r, u0, u1, on_gpsimd=False):
+        def regroup_x(r, s0, s1, on_gpsimd=False):
             if r < 0:
                 return
-            if u0 == 0:
-                xg_t[r] = gpool.tile([P, 1024, 4], BF16, name="xg", tag="xg", align_bytes=64)
-            xg = xg_t[r]
+            if s0 == 0:
+                xn_grouped[r] = gpool.tile([P, PASSES * COLS, PACK], BF16, name="xn_grouped", tag="xn_grouped", align_bytes=64)
+            dst = xn_grouped[r]
             if on_gpsimd:
-                for i in range(u0, u1):
+                for s in range(s0, s1):
                     nc.gpsimd.tensor_scalar(
-                        out=xg[:, 256 * i:256 * i + 256, :],
-                        in0=xp_t[(r, i // 2)][:, :, i % 2, :].rearrange("p j c -> p c j"),
+                        out=dst[:, COLS * s:COLS * (s + 1), :],
+                        in0=xn_planes[(r, s // 2)][:, :, s % 2, :].rearrange("p j c -> p c j"),
                         scalar1=1.0, scalar2=0.0, op0=ALU.mult, op1=ALU.add,
                     )
-            elif u1 - u0 == 2:
-                nc.vector.tensor_copy(
-                    out=xg[:, 256 * u0:256 * u1, :].rearrange("p (c i) j -> p c j i", i=4),
-                    in_=xp_t[(r, u0 // 2)][:].rearrange("p j u c -> p j (u c)").rearrange("p j (c i) -> p c j i", i=4),
-                )
-            else:
-                nc.vector.tensor_copy(
-                    out=xg[:, 256 * u0:256 * u1, :].rearrange("p (c i) j -> p c j i", i=4),
-                    in_=xp_t[(r, u0 // 2)][:, :, u0 % 2, :].rearrange("p j (c i) -> p c j i", i=4),
-                )
-
-        def qx(r, u0, u1):
-            if r < 0:
                 return
-            xg = xg_t[r]
-            if u0 == 0:
-                xq_t[r] = (
-                    gpool.tile([P, 1024], U32, name="xc", tag="xc", align_bytes=64),
-                    gpool.tile([P, 1024], U8, name="xsc", tag="xsc", align_bytes=64),
-                )
-            xc, xsc = xq_t[r]
-            nc.vector.quantize_mx(
-                out=xc[:, 256 * u0:256 * u1].bitcast(FP8X4), scales=xsc[:, 256 * u0:256 * u1],
-                in_=xg[:, 256 * u0:256 * u1, :].rearrange("p c j -> p (c j)"),
+            if s1 - s0 == 2:
+                src = xn_planes[(r, s0 // 2)][:].rearrange("p j s c -> p j (s c)")
+            else:
+                src = xn_planes[(r, s0 // 2)][:, :, s0 % 2, :]
+            nc.vector.tensor_copy(
+                out=dst[:, COLS * s0:COLS * s1, :].rearrange("p (c i) j -> p c j i", i=4),
+                in_=src.rearrange("p j (c i) -> p c j i", i=4),
             )
 
-        def mx(r, u0, u1):
+        def quantise_x(r, s0, s1):
             if r < 0:
                 return
-            nb = bands_of(r)
-            upb = 4 // nb
-            wc, wsc = wq_t[r]
-            xc, xsc = xq_t[r]
-            for i in range(u0, u1):
-                if i == 0 or (nb == 4 and i == 2):
-                    acc_t[r] = psa.tile([P, 512], F32, name="acc", tag="acc")
-                acc = acc_t[r]
-                col = 256 * (i % 2) if nb == 4 else (256 * (i // 2) if nb == 2 else 0)
+            if s0 == 0:
+                xn_mx[r] = (
+                    gpool.tile([P, PASSES * COLS], U32, name="x_codes", tag="x_codes", align_bytes=64),
+                    gpool.tile([P, PASSES * COLS], U8, name="x_scales", tag="x_scales", align_bytes=64),
+                )
+            codes, scales = xn_mx[r]
+            nc.vector.quantize_mx(
+                out=codes[:, COLS * s0:COLS * s1].bitcast(FP8X4), scales=scales[:, COLS * s0:COLS * s1],
+                in_=xn_grouped[r][:, COLS * s0:COLS * s1, :].rearrange("p c j -> p (c j)"),
+            )
+
+        def multiply(r, s0, s1):
+            if r < 0:
+                return
+            nb = bands_in(r)
+            per_band = PASSES // nb
+            w_codes, w_scales = w_mx[r]
+            x_codes, x_scales = xn_mx[r]
+            for s in range(s0, s1):
+                band = s // per_band
+                if band % 2 == 0 and s % per_band == 0:
+                    sums[r] = ps_y.tile([P, 2 * COLS], F32, name="sums", tag="sums")
+                c0 = COLS * (band % 2)
                 nc.tensor.matmul_mx(
-                    out=acc[:, col:col + 256],
-                    lhsT=wc[:, i * P:(i + 1) * P].bitcast(FP8X4),
-                    lhsT_scale=wsc[:, i * P:(i + 1) * P],
-                    rhs=xc[:, 256 * i:256 * i + 256].bitcast(FP8X4),
-                    rhs_scale=xsc[:, 256 * i:256 * i + 256],
-                    start=(i % upb == 0),
-                    stop=(i % upb == upb - 1),
+                    out=sums[r][:, c0:c0 + COLS],
+                    lhsT=w_codes[:, s * P:(s + 1) * P].bitcast(FP8X4),
+                    lhsT_scale=w_scales[:, s * P:(s + 1) * P],
+                    rhs=x_codes[:, COLS * s:COLS * (s + 1)].bitcast(FP8X4),
+                    rhs_scale=x_scales[:, COLS * s:COLS * (s + 1)],
+                    start=(s % per_band == 0),
+                    stop=(s % per_band == per_band - 1),
                 )
 
-        def oe(r, pair):
+        def finish_bands(r, k0, k1):
             if r < 0:
                 return
-            nb = bands_of(r)
-            if nb == 1 and pair == 0:
-                return
-            acc = acc_t[r]
-            band0 = first_band(r)
-            if nb == 4:
-                todo = [(band0 + 2 * pair, 0), (band0 + 2 * pair + 1, 256)]
-            elif nb == 2:
-                todo = [(band0 + pair, 256 * pair)]
-            else:
-                todo = [(band0, 0)]
-            for band, col in todo:
+            for k in range(k0, min(k1, bands_in(r))):
+                band = first_band(r) + k
                 if band % 4 == 0:
-                    o_t[0] = opool.tile([P, 2, 4, P], F32, name="osb", tag="osb")
-                osb = o_t[0]
+                    out_sb[0] = opool.tile([P, 2, 4, P], F32, name="out_sb", tag="out_sb")
+                c0 = COLS * (k % 2)
                 nc.vector.tensor_scalar(
-                    out=osb[:, :, band % 4, :].rearrange("n b (q e) -> n b q e", e=2),
-                    in0=acc[:, col:col + 256].rearrange("n (e b q) -> n b q e", e=2, b=2),
-                    scalar1=csb[:, band:band + 1], scalar2=None, op0=ALU.add,
+                    out=out_sb[0][:, :, band % 4, :].rearrange("n b (q e) -> n b q e", e=2),
+                    in0=sums[r][:, c0:c0 + COLS].rearrange("n (e b q) -> n b q e", e=2, b=2),
+                    scalar1=c_sb[:, band:band + 1], scalar2=None, op0=ALU.add,
                 )
-                if band == 30:
+                first = {3: 0, 7: 4, 11: 8, 15: 12, 19: 16, 23: 20, 27: 24, 30: 28, 31: 31}.get(band)
+                if first is not None:
                     nc.sync.dma_start(
-                        out=out[:, :, 28:31, :].rearrange("b n k t -> n b (k t)"),
-                        in_=osb[:, :, 0:3, :].rearrange("n b k t -> n b (k t)"),
-                    )
-                elif band == 31:
-                    nc.sync.dma_start(
-                        out=out[:, :, 31, :].rearrange("b n t -> n b t"),
-                        in_=osb[:, :, 3, :],
-                    )
-                elif band % 4 == 3:
-                    nc.sync.dma_start(
-                        out=out[:, :, band - 3:band + 1, :].rearrange("b n k t -> n b (k t)"),
-                        in_=osb[:].rearrange("n b k t -> n b (k t)"),
+                        out=out[:, :, first:band + 1, :].rearrange("b n k t -> n b (k t)"),
+                        in_=out_sb[0][:, :, first % 4:band % 4 + 1, :].rearrange("n b k t -> n b (k t)"),
                     )
 
         ident = const.tile([P, P], F32, name="ident")
         make_identity(nc, ident[:])
-        load(0)
-        gbrow = const.tile([P, 512], BF16, name="gbrow")
-        nc.scalar.dma_start(out=gbrow[0:16, :], in_=g16)
-        nc.scalar.dma_start(out=gbrow[16:32, :], in_=g32.rearrange("k (u c) -> (k u) c", u=2))
-        nc.scalar.dma_start(out=gbrow[32:64, :], in_=g64.rearrange("k (u c) -> (k u) c", u=4))
-        nc.scalar.dma_start(out=gbrow[64:80, :], in_=b16)
-        nc.scalar.dma_start(out=gbrow[80:96, :], in_=b32.rearrange("k (u c) -> (k u) c", u=2))
-        nc.scalar.dma_start(out=gbrow[96:128, :], in_=b64.rearrange("k (u c) -> (k u) c", u=4))
-        crow = const.tile([P, P], BF16, name="crow")
-        nc.vector.memset(crow[:], 0.0)
-        nc.scalar.dma_start(out=crow[0:16, :], in_=c16)
-        nc.scalar.dma_start(out=crow[16:24, :], in_=c32)
-        nc.scalar.dma_start(out=crow[24:32, :], in_=c64)
-        load(1)
-        load(2)
+        load_round(0)
+        gb_rows = const.tile([P, PACK * P], BF16, name="gb_rows")
+        for row0, vec, per_band in ((0, g16, 1), (16, g32, 2), (32, g64, 4), (64, b16, 1), (80, b32, 2), (96, b64, 4)):
+            nc.scalar.dma_start(
+                out=gb_rows[row0:row0 + vec.shape[0] * per_band, :],
+                in_=vec.rearrange("k (s c) -> (k s) c", s=per_band),
+            )
+        c_rows = const.tile([P, P], BF16, name="c_rows")
+        nc.vector.memset(c_rows[:], 0.0)
+        nc.scalar.dma_start(out=c_rows[0:16, :], in_=c16)
+        nc.scalar.dma_start(out=c_rows[16:24, :], in_=c32)
+        nc.scalar.dma_start(out=c_rows[24:32, :], in_=c64)
+        load_round(1)
+        load_round(2)
 
-        t1bn(0, 0)
-        t1bn(0, 1)
-        chain_a(0, 0, 2)
-        chain_b(0, 0, 2)
-        chain_c(0, 0, 2)
+        to_frames(0, 0)
+        to_frames(0, 1)
+        stats_join(0, 0, 2)
+        stats_sqrt(0, 0, 2)
+        stats_finish(0, 0, 2)
 
-        gbp = const.tile([P, 4, P], F32, name="gbp")
-        nc.vector.tensor_copy(out=gbp[:], in_=gbrow[:].rearrange("r (p j) -> r j p", j=4))
-        pg = ps2.tile([P, 4, P], F32, name="pg", tag="p2")
-        for j in range(4):
-            nc.tensor.transpose(pg[:, j, :], gbp[:, j, :], ident[:])
-        crf = const.tile([P, P], F32, name="crf")
-        nc.vector.tensor_copy(out=crf[:], in_=crow[:])
-        pc = ps2.tile([P, 4, P], F32, name="pc", tag="p2")
-        nc.tensor.transpose(pc[:, 0, :], crf[:], ident[:])
+        gb_sorted = const.tile([P, PACK, P], F32, name="gb_sorted")
+        nc.vector.tensor_copy(out=gb_sorted[:], in_=gb_rows[:].rearrange("r (p j) -> r j p", j=PACK))
+        gb_bank = ps_z.tile([P, PACK, P], F32, name="gb_bank", tag="z_bank")
+        for j in range(PACK):
+            nc.tensor.transpose(gb_bank[:, j, :], gb_sorted[:, j, :], ident[:])
+        c_f32 = const.tile([P, P], F32, name="c_f32")
+        nc.vector.tensor_copy(out=c_f32[:], in_=c_rows[:])
+        c_bank = ps_z.tile([P, PACK, P], F32, name="c_bank", tag="z_bank")
+        nc.tensor.transpose(c_bank[:, 0, :], c_f32[:], ident[:])
 
-        t1bn(0, 2)
-        t1bn(0, 3)
-        chain_a(0, 2, 4)
+        to_frames(0, 2)
+        to_frames(0, 3)
+        stats_join(0, 2, 4)
 
-        gb = const.tile([P, 4, P], F32, name="gb")
-        nc.vector.tensor_copy(out=gb[:], in_=pg[:])
-        csb = const.tile([P, 32], F32, name="csb")
-        nc.vector.tensor_copy(out=csb[:], in_=pc[:, 0, 0:32])
+        gain_bias = const.tile([P, PACK, P], F32, name="gain_bias")
+        nc.vector.tensor_copy(out=gain_bias[:], in_=gb_bank[:])
+        c_sb = const.tile([P, 32], F32, name="c_sb")
+        nc.vector.tensor_copy(out=c_sb[:], in_=c_bank[:, 0, 0:32])
 
-        wrg(0)
-        wq(0)
+        copy_w(0, 0, PASSES)
+        quantise_w(0)
 
         for r in range(ROUNDS):
-            nb = bands_of(r)
-            old4 = r > 1 and bands_of(r - 2) == 4
+            four_bands_old = r >= 2 and bands_in(r - 2) == 4
             last = r == LAST
-            load(r + 3)
-            oe(r - 2, 0)
-            if not old4:
-                oe(r - 2, 1)
-            if r - 1 in SHARE:
-                e2(r - 1, 3, 1, True)
-            wrg(r + 1, 0, 1)
-            rg(r - 1, 2, 4, not last)
-            wrg(r + 1, 1, 4)
+            load_round(r + 3)
 
-            e1(r, 0)
-            if nb != 4:
-                t1bn(r + 1, 0)
-            t2(r, 0, 0)
-            e1(r, 1)
+            finish_bands(r - 2, 0, 2)
+            gain_shift(r - 1, 3, 1, on_vector=True)
+            copy_w(r + 1, 0, 1)
+            regroup_x(r - 1, 2, 4, on_gpsimd=not last)
+            copy_w(r + 1, 1, PASSES)
+
+            normalise(r, 0)
+            to_frames(r + 1, 0)
+            to_channels(r, 0, 0)
+            normalise(r, 1)
             if r == 0:
-                chain_b(0, 2, 4)
-                chain_c(0, 2, 4)
-            t1bn(r + 1, 0 if nb == 4 else 1)
-            t2(r, 0, 1)
-            if nb == 4:
-                t1bn(r + 1, 1)
-            if old4:
-                mx(r - 2, 2, 4)
+                stats_sqrt(0, 2, 4)
+                stats_finish(0, 2, 4)
+            to_frames(r + 1, 1)
+            to_channels(r, 0, 1)
+            if four_bands_old:
+                multiply(r - 2, 2, 4)
             if last:
-                qx(r - 1, 0, 4)
-                mx(r - 1, 0, 4)
-            e1(r, 2)
-            if nb != 4:
-                t1bn(r + 1, 2)
-            t2(r, 1, 0)
-            e1(r, 3)
-            if nb == 4:
-                t1bn(r + 1, 2)
-            if old4:
-                oe(r - 2, 1)
-            t1bn(r + 1, 3)
-            chain_a(r + 1)
+                quantise_x(r - 1, 0, PASSES)
+                multiply(r - 1, 0, PASSES)
+            normalise(r, 2)
+            to_frames(r + 1, 2)
+            to_channels(r, 1, 0)
+            normalise(r, 3)
+            if four_bands_old:
+                finish_bands(r - 2, 2, 4)
+            to_frames(r + 1, 3)
+            stats_join(r + 1, 0, bands_in(min(r + 1, LAST)))
             if last:
-                oe(r - 1, 1)
+                finish_bands(r - 1, 0, 1)
 
-            e2(r, 0, 0)
-            t2(r, 1, 1)
-            e2(r, 0, 1)
-            t2(r, 2, 0)
+            gain_shift(r, 0, 0)
+            to_channels(r, 1, 1)
+            gain_shift(r, 0, 1)
+            to_channels(r, 2, 0)
             if last:
-                rg(r, 0, 1)
-            e2(r, 1, 0)
-            t2(r, 2, 1)
-            e2(r, 1, 1)
-            t2(r, 3, 0)
-            chain_b(r + 1)
+                regroup_x(r, 0, 1)
+            gain_shift(r, 1, 0)
+            to_channels(r, 2, 1)
+            gain_shift(r, 1, 1)
+            to_channels(r, 3, 0)
+            stats_sqrt(r + 1, 0, bands_in(min(r + 1, LAST)))
             if not last:
-                qx(r - 1, 0, 4)
-                chain_c(r + 1)
-                rg(r, 0, 2)
-                wq(r + 1)
+                quantise_x(r - 1, 0, PASSES)
+                stats_finish(r + 1, 0, bands_in(r + 1))
+                regroup_x(r, 0, 2)
+                quantise_w(r + 1)
             else:
-                rg(r, 1, 2)
-                qx(r, 0, 2)
-                mx(r, 0, 2)
-            e2(r, 2, 0)
-            t2(r, 3, 1)
-            e2(r, 2, 1)
+                regroup_x(r, 1, 2)
+                quantise_x(r, 0, 2)
+                multiply(r, 0, 2)
+            gain_shift(r, 2, 0)
+            to_channels(r, 3, 1)
+            gain_shift(r, 2, 1)
             if last:
-                rg(r, 2, 3)
-                qx(r, 2, 3)
-                mx(r, 2, 3)
-            e2(r, 3, 0)
-            if r not in SHARE:
-                e2(r, 3, 1)
+                regroup_x(r, 2, 3)
+                quantise_x(r, 2, 3)
+                multiply(r, 2, 3)
+            gain_shift(r, 3, 0)
             if not last:
-                mx(r - 1, 0, 2 if (r > 0 and bands_of(r - 1) == 4) else 4)
+                multiply(r - 1, 0, 2 if (r >= 1 and bands_in(r - 1) == 4) else PASSES)
 
-        if LAST in SHARE:
-            e2(LAST, 3, 1, True)
-        rg(LAST, 3, 4)
-        qx(LAST, 3, 4)
-        mx(LAST, 3, 4)
-        oe(LAST, 1)
+        gain_shift(LAST, 3, 1, on_vector=True)
+        regroup_x(LAST, 3, 4)
+        quantise_x(LAST, 3, 4)
+        multiply(LAST, 3, 4)
+        finish_bands(LAST, 0, 1)

@@ -30,6 +30,10 @@ def first_band(r):
     return 4 * r if r < 4 else (2 * r + 8 if r < 8 else r + 16)
 
 
+def vector_helps(r):
+    return 0 <= r and bands_in(r) < 4
+
+
 def tile_bandsplitmodule_kernel(
     tc, x_real, x_imag, sample_rate,
     g16, b16, W16, c16, g32, b32, W32, c32, g64, b64, W64, c64, out,
@@ -327,7 +331,8 @@ def tile_bandsplitmodule_kernel(
             load_round(r + 3)
 
             finish_bands(r - 2, 0, 2)
-            gain_shift(r - 1, 3, 1, on_vector=True)
+            if vector_helps(r - 1):
+                gain_shift(r - 1, 3, 1, on_vector=True)
             copy_w(r + 1, 0, 1)
             regroup_x(r - 1, 2, 4, on_gpsimd=not last)
             copy_w(r + 1, 1, PASSES)
@@ -385,6 +390,8 @@ def tile_bandsplitmodule_kernel(
                 quantise_x(r, 2, 3)
                 multiply(r, 2, 3)
             gain_shift(r, 3, 0)
+            if not vector_helps(r):
+                gain_shift(r, 3, 1)
             if not last:
                 multiply(r - 1, 0, 2 if (r >= 1 and bands_in(r - 1) == 4) else PASSES)
 

@@ -19,7 +19,12 @@ COLS = 256
 EPS = 1e-8
 ROUNDS = 16
 LAST = ROUNDS - 1
+ROUND_BINS = 1024
 PASSES = 4
+ALL_PASSES = ROUNDS * PASSES
+BANDS = 32
+STAT_COLS = 8
+BN_VALUES = 3
 
 
 def bands_in(r):
@@ -28,10 +33,6 @@ def bands_in(r):
 
 def first_band(r):
     return 4 * r if r < 4 else (2 * r + 8 if r < 8 else r + 16)
-
-
-def vector_helps(r):
-    return 0 <= r and bands_in(r) < 4
 
 
 def tile_bandsplitmodule_kernel(
@@ -61,26 +62,26 @@ def tile_bandsplitmodule_kernel(
         def load_round(r):
             if r > LAST:
                 return
-            nb = bands_in(r)
+            bin0 = ROUND_BINS * r
             x_sb[r] = xpool.tile([P, PASSES * PACK * COLS], BF16, name="x_sb", tag="x_sb")
-            xv = x_sb[r][:].rearrange("p (s j b t) -> p s j b t", s=PASSES, j=PACK, b=2)
+            x_view = x_sb[r][:].rearrange("p (s j i t) -> p s j i t", s=PASSES, j=PACK, i=2)
             for s in range(PASSES):
-                if nb == 4:
-                    parts = [(x_real, 1024 * r + 256 * s, 0, 64), (x_imag, 1024 * r + 256 * s, 64, 64)]
-                elif nb == 2:
-                    parts = [((x_real, x_imag)[s % 2], 1024 * r + 512 * (s // 2), 0, P)]
+                if bands_in(r) == 4:
+                    parts = [(x_real, bin0 + 256 * s, 0, 64), (x_imag, bin0 + 256 * s, 64, 64)]
+                elif bands_in(r) == 2:
+                    parts = [((x_real, x_imag)[s % 2], bin0 + 512 * (s // 2), 0, P)]
                 else:
-                    parts = [((x_real, x_imag)[s // 2], 1024 * r + 512 * (s % 2), 0, P)]
-                for src, bin0, p0, n in parts:
-                    for b in range(2):
+                    parts = [((x_real, x_imag)[s // 2], bin0 + 512 * (s % 2), 0, P)]
+                for src, first, p0, count in parts:
+                    for i in range(2):
                         nc.sync.dma_start(
-                            out=xv[p0:p0 + n, s, :, b, :],
-                            in_=src[b, bin0:bin0 + PACK * n, :].rearrange("(p j) t -> p j t", j=PACK),
+                            out=x_view[p0:p0 + count, s, :, i, :],
+                            in_=src[i, first:first + PACK * count, :].rearrange("(p j) t -> p j t", j=PACK),
                         )
             w_raw[r] = wpool.tile([P, PASSES, PACK * P], BF16, name="w_raw", tag="w_raw")
-            if nb == 4:
+            if bands_in(r) == 4:
                 w_rows = W16[4 * r:4 * r + 4].rearrange("k (p j) n -> p k (j n)", j=PACK)
-            elif nb == 2:
+            elif bands_in(r) == 2:
                 w_rows = W32[2 * r - 8:2 * r - 6].rearrange("k (s p j) n -> p (k s) (j n)", s=2, j=PACK)
             else:
                 w_rows = W64[r - 8].rearrange("(s p j) n -> p s (j n)", s=PASSES, j=PACK)
@@ -112,13 +113,13 @@ def tile_bandsplitmodule_kernel(
             if r > LAST:
                 return
             if s == 0:
-                pieces[r] = small.tile([P, 2 * PASSES, 6], F32, name="pieces", tag="pieces")
+                pieces[r] = small.tile([P, 2 * PASSES, 2 * BN_VALUES], F32, name="pieces", tag="pieces")
                 x_frames[r] = []
-            words = x_sb[r][:].bitcast(F32)
+            pairs = x_sb[r][:].bitcast(F32)
             bank = ps_x.tile([P, PACK * P], F32, name="x_bank", tag="x_bank")
             for j in range(PACK):
                 c0 = (s * PACK + j) * P
-                nc.tensor.transpose(bank[:, j * P:(j + 1) * P], words[:, c0:c0 + P], ident[:])
+                nc.tensor.transpose(bank[:, j * P:(j + 1) * P], pairs[:, c0:c0 + P], ident[:])
             view = bank[:].bitcast(BF16).rearrange("q (j p e) -> q j p e", j=PACK, e=2)
             x_frames[r].append(view)
             for h in range(2):
@@ -127,50 +128,53 @@ def tile_bandsplitmodule_kernel(
                     in_=view[:, 2 * h:2 * h + 2, :, :].rearrange("q j p e -> q (j p e)"),
                 )
 
-        def stats_join(r, k0, k1):
+        def stats_join(r, k0=0, k1=None):
             if r > LAST:
                 return
-            per_band = 2 * PASSES // bands_in(r)
+            k1 = bands_in(r) if k1 is None else k1
+            pieces_per_band = 2 * PASSES // bands_in(r)
             if k0 == 0:
                 stats[r] = [
-                    small.tile([P, 8, 2], F32, name="mean_var", tag="mean_var"),
-                    small.tile([P, 8], F32, name="std", tag="std"),
-                    small.tile([P, 8], F32, name="rstd", tag="rstd"),
-                    small.tile([P, 8], F32, name="shift", tag="shift"),
+                    small.tile([P, STAT_COLS, 2], F32, name="mean_var", tag="mean_var"),
+                    small.tile([P, STAT_COLS], F32, name="std", tag="std"),
+                    small.tile([P, STAT_COLS], F32, name="rstd", tag="rstd"),
+                    small.tile([P, STAT_COLS], F32, name="offset", tag="offset"),
                 ]
             for k in range(k0, k1):
                 for e in range(2):
                     nc.vector.bn_aggr(
                         out=stats[r][0][:, 2 * k + e, :],
-                        in_=pieces[r][:, per_band * k:per_band * (k + 1), 3 * e:3 * e + 3],
+                        in_=pieces[r][:, pieces_per_band * k:pieces_per_band * (k + 1), BN_VALUES * e:BN_VALUES * (e + 1)],
                     )
 
-        def stats_sqrt(r, k0, k1):
+        def stats_sqrt(r, k0=0, k1=None):
             if r > LAST:
                 return
+            k1 = bands_in(r) if k1 is None else k1
             nc.scalar.activation(
                 out=stats[r][1][:, 2 * k0:2 * k1], in_=stats[r][0][:, 2 * k0:2 * k1, 1],
                 func=ACT.Sqrt, bias=EPS, scale=1.0,
             )
 
-        def stats_finish(r, k0, k1):
+        def stats_finish(r, k0=0, k1=None):
             if r > LAST:
                 return
-            mean_var, std, rstd, shift = stats[r]
+            k1 = bands_in(r) if k1 is None else k1
+            mean_var, std, rstd, offset = stats[r]
             nc.vector.reciprocal(out=rstd[:, 2 * k0:2 * k1], in_=std[:, 2 * k0:2 * k1])
             nc.vector.scalar_tensor_tensor(
-                out=shift[:, 2 * k0:2 * k1], in0=mean_var[:, 2 * k0:2 * k1, 0], scalar=-1.0,
+                out=offset[:, 2 * k0:2 * k1], in0=mean_var[:, 2 * k0:2 * k1, 0], scalar=-1.0,
                 in1=rstd[:, 2 * k0:2 * k1], op0=ALU.mult, op1=ALU.mult,
             )
 
         def normalise(r, s):
-            rstd, shift = stats[r][2], stats[r][3]
+            rstd, offset = stats[r][2], stats[r][3]
             z_sb[(r, s)] = zpool.tile([P, 2, PACK, P], F32, name="z_sb", tag="z_sb")
             for e in range(2):
                 col = 2 * (s * bands_in(r) // PASSES) + e
                 nc.scalar.activation(
                     out=z_sb[(r, s)][:, e, :, :], in_=x_frames[r][s][:, :, :, e],
-                    func=ACT.Identity, scale=rstd[:, col:col + 1], bias=shift[:, col:col + 1],
+                    func=ACT.Identity, scale=rstd[:, col:col + 1], bias=offset[:, col:col + 1],
                 )
 
         def to_channels(r, s, half):
@@ -185,20 +189,21 @@ def tile_bandsplitmodule_kernel(
                 return
             if s % 2 == 0 and half == 0:
                 xn_planes[(r, s // 2)] = ppool.tile([P, PACK, 2, COLS], BF16, name="xn_planes", tag="xn_planes")
-            n = PASSES * r + s
+            g_col = PASSES * r + s
+            b_col = ALL_PASSES + g_col
             for jl in range(2):
                 j = 2 * half + jl
                 dst = xn_planes[(r, s // 2)][:, j, s % 2, :]
                 src = z_chan[(r, s, half)][:, jl, :, :].rearrange("p e q -> p (e q)")
                 if on_vector:
                     nc.vector.tensor_scalar(
-                        out=dst, in0=src, scalar1=gain_bias[:, j, n:n + 1], scalar2=gain_bias[:, j, 64 + n:65 + n],
+                        out=dst, in0=src, scalar1=g_and_b[:, j, g_col:g_col + 1], scalar2=g_and_b[:, j, b_col:b_col + 1],
                         op0=ALU.mult, op1=ALU.add,
                     )
                 else:
                     nc.scalar.activation(
                         out=dst, in_=src, func=ACT.Identity,
-                        scale=gain_bias[:, j, n:n + 1], bias=gain_bias[:, j, 64 + n:65 + n],
+                        scale=g_and_b[:, j, g_col:g_col + 1], bias=g_and_b[:, j, b_col:b_col + 1],
                     )
 
         def regroup_x(r, s0, s1, on_gpsimd=False):
@@ -220,8 +225,8 @@ def tile_bandsplitmodule_kernel(
             else:
                 src = xn_planes[(r, s0 // 2)][:, :, s0 % 2, :]
             nc.vector.tensor_copy(
-                out=dst[:, COLS * s0:COLS * s1, :].rearrange("p (c i) j -> p c j i", i=4),
-                in_=src.rearrange("p j (c i) -> p c j i", i=4),
+                out=dst[:, COLS * s0:COLS * s1, :].rearrange("p (c u) j -> p c j u", u=4),
+                in_=src.rearrange("p j (c u) -> p c j u", u=4),
             )
 
         def quantise_x(r, s0, s1):
@@ -241,23 +246,22 @@ def tile_bandsplitmodule_kernel(
         def multiply(r, s0, s1):
             if r < 0:
                 return
-            nb = bands_in(r)
-            per_band = PASSES // nb
+            passes_per_band = PASSES // bands_in(r)
             w_codes, w_scales = w_mx[r]
             x_codes, x_scales = xn_mx[r]
             for s in range(s0, s1):
-                band = s // per_band
-                if band % 2 == 0 and s % per_band == 0:
+                k = s // passes_per_band
+                if k % 2 == 0 and s % passes_per_band == 0:
                     sums[r] = ps_y.tile([P, 2 * COLS], F32, name="sums", tag="sums")
-                c0 = COLS * (band % 2)
+                c0 = COLS * (k % 2)
                 nc.tensor.matmul_mx(
                     out=sums[r][:, c0:c0 + COLS],
                     lhsT=w_codes[:, s * P:(s + 1) * P].bitcast(FP8X4),
                     lhsT_scale=w_scales[:, s * P:(s + 1) * P],
                     rhs=x_codes[:, COLS * s:COLS * (s + 1)].bitcast(FP8X4),
                     rhs_scale=x_scales[:, COLS * s:COLS * (s + 1)],
-                    start=(s % per_band == 0),
-                    stop=(s % per_band == per_band - 1),
+                    start=(s % passes_per_band == 0),
+                    stop=(s % passes_per_band == passes_per_band - 1),
                 )
 
         def finish_bands(r, k0, k1):
@@ -265,29 +269,38 @@ def tile_bandsplitmodule_kernel(
                 return
             for k in range(k0, min(k1, bands_in(r))):
                 band = first_band(r) + k
+                four = band // 4
                 if band % 4 == 0:
-                    out_sb[0] = opool.tile([P, 2, 4, P], F32, name="out_sb", tag="out_sb")
+                    out_sb[four] = opool.tile([P, 2, 4, P], F32, name="out_sb", tag="out_sb")
                 c0 = COLS * (k % 2)
                 nc.vector.tensor_scalar(
-                    out=out_sb[0][:, :, band % 4, :].rearrange("n b (q e) -> n b q e", e=2),
-                    in0=sums[r][:, c0:c0 + COLS].rearrange("n (e b q) -> n b q e", e=2, b=2),
+                    out=out_sb[four][:, :, band % 4, :].rearrange("n i (q e) -> n i q e", e=2),
+                    in0=sums[r][:, c0:c0 + COLS].rearrange("n (e i q) -> n i q e", e=2, i=2),
                     scalar1=c_sb[:, band:band + 1], scalar2=None, op0=ALU.add,
                 )
-                first = {3: 0, 7: 4, 11: 8, 15: 12, 19: 16, 23: 20, 27: 24, 30: 28, 31: 31}.get(band)
+                if band == BANDS - 1:
+                    first = band
+                elif band % 4 == 3 or band == BANDS - 2:
+                    first = 4 * four
+                else:
+                    first = None
                 if first is not None:
                     nc.sync.dma_start(
-                        out=out[:, :, first:band + 1, :].rearrange("b n k t -> n b (k t)"),
-                        in_=out_sb[0][:, :, first % 4:band % 4 + 1, :].rearrange("n b k t -> n b (k t)"),
+                        out=out[:, :, first:band + 1, :].rearrange("i n k t -> n i (k t)"),
+                        in_=out_sb[four][:, :, first % 4:band % 4 + 1, :].rearrange("n i k t -> n i (k t)"),
                     )
 
         ident = const.tile([P, P], F32, name="ident")
         make_identity(nc, ident[:])
         load_round(0)
         gb_rows = const.tile([P, PACK * P], BF16, name="gb_rows")
-        for row0, vec, per_band in ((0, g16, 1), (16, g32, 2), (32, g64, 4), (64, b16, 1), (80, b32, 2), (96, b64, 4)):
+        for row0, vec, passes_per_band in (
+            (0, g16, 1), (16, g32, 2), (32, g64, 4),
+            (ALL_PASSES, b16, 1), (ALL_PASSES + 16, b32, 2), (ALL_PASSES + 32, b64, 4),
+        ):
             nc.scalar.dma_start(
-                out=gb_rows[row0:row0 + vec.shape[0] * per_band, :],
-                in_=vec.rearrange("k (s c) -> (k s) c", s=per_band),
+                out=gb_rows[row0:row0 + vec.shape[0] * passes_per_band, :],
+                in_=vec.rearrange("k (s c) -> (k s) c", s=passes_per_band),
             )
         c_rows = const.tile([P, P], BF16, name="c_rows")
         nc.vector.memset(c_rows[:], 0.0)
@@ -304,7 +317,7 @@ def tile_bandsplitmodule_kernel(
         stats_finish(0, 0, 2)
 
         gb_sorted = const.tile([P, PACK, P], F32, name="gb_sorted")
-        nc.vector.tensor_copy(out=gb_sorted[:], in_=gb_rows[:].rearrange("r (p j) -> r j p", j=PACK))
+        nc.vector.tensor_copy(out=gb_sorted[:], in_=gb_rows[:].rearrange("m (p j) -> m j p", j=PACK))
         gb_bank = ps_z.tile([P, PACK, P], F32, name="gb_bank", tag="z_bank")
         for j in range(PACK):
             nc.tensor.transpose(gb_bank[:, j, :], gb_sorted[:, j, :], ident[:])
@@ -317,10 +330,10 @@ def tile_bandsplitmodule_kernel(
         to_frames(0, 3)
         stats_join(0, 2, 4)
 
-        gain_bias = const.tile([P, PACK, P], F32, name="gain_bias")
-        nc.vector.tensor_copy(out=gain_bias[:], in_=gb_bank[:])
-        c_sb = const.tile([P, 32], F32, name="c_sb")
-        nc.vector.tensor_copy(out=c_sb[:], in_=c_bank[:, 0, 0:32])
+        g_and_b = const.tile([P, PACK, P], F32, name="g_and_b")
+        nc.vector.tensor_copy(out=g_and_b[:], in_=gb_bank[:])
+        c_sb = const.tile([P, BANDS], F32, name="c_sb")
+        nc.vector.tensor_copy(out=c_sb[:], in_=c_bank[:, 0, 0:BANDS])
 
         copy_w(0, 0, PASSES)
         quantise_w(0)
@@ -331,8 +344,7 @@ def tile_bandsplitmodule_kernel(
             load_round(r + 3)
 
             finish_bands(r - 2, 0, 2)
-            if vector_helps(r - 1):
-                gain_shift(r - 1, 3, 1, on_vector=True)
+            gain_shift(r - 1, 3, 1, on_vector=True)
             copy_w(r + 1, 0, 1)
             regroup_x(r - 1, 2, 4, on_gpsimd=not last)
             copy_w(r + 1, 1, PASSES)
@@ -358,7 +370,7 @@ def tile_bandsplitmodule_kernel(
             if four_bands_old:
                 finish_bands(r - 2, 2, 4)
             to_frames(r + 1, 3)
-            stats_join(r + 1, 0, bands_in(min(r + 1, LAST)))
+            stats_join(r + 1)
             if last:
                 finish_bands(r - 1, 0, 1)
 
@@ -372,10 +384,10 @@ def tile_bandsplitmodule_kernel(
             to_channels(r, 2, 1)
             gain_shift(r, 1, 1)
             to_channels(r, 3, 0)
-            stats_sqrt(r + 1, 0, bands_in(min(r + 1, LAST)))
+            stats_sqrt(r + 1)
             if not last:
                 quantise_x(r - 1, 0, PASSES)
-                stats_finish(r + 1, 0, bands_in(r + 1))
+                stats_finish(r + 1)
                 regroup_x(r, 0, 2)
                 quantise_w(r + 1)
             else:
@@ -390,8 +402,6 @@ def tile_bandsplitmodule_kernel(
                 quantise_x(r, 2, 3)
                 multiply(r, 2, 3)
             gain_shift(r, 3, 0)
-            if not vector_helps(r):
-                gain_shift(r, 3, 1)
             if not last:
                 multiply(r - 1, 0, 2 if (r >= 1 and bands_in(r - 1) == 4) else PASSES)
 

@@ -31,6 +31,10 @@ def bands_in(r):
     return 4 if r < 4 else (2 if r < 8 else 1)
 
 
+def third_plane(r):
+    return 8 <= r < LAST
+
+
 def first_band(r):
     return 4 * r if r < 4 else (2 * r + 8 if r < 8 else r + 16)
 
@@ -152,8 +156,8 @@ def tile_bandsplitmodule_kernel(
                 return
             k1 = bands_in(r) if k1 is None else k1
             nc.scalar.activation(
-                out=stats[r][1][:, 2 * k0:2 * k1], in_=stats[r][0][:, 2 * k0:2 * k1, 1],
-                func=ACT.Sqrt, bias=EPS, scale=1.0,
+                out=stats[r][2][:, 2 * k0:2 * k1], in_=stats[r][0][:, 2 * k0:2 * k1, 1],
+                func=ACT.Abs_reciprocal_sqrt, bias=EPS, scale=1.0,
             )
 
         def stats_finish(r, k0=0, k1=None):
@@ -161,7 +165,6 @@ def tile_bandsplitmodule_kernel(
                 return
             k1 = bands_in(r) if k1 is None else k1
             mean_var, std, rstd, offset = stats[r]
-            nc.vector.reciprocal(out=rstd[:, 2 * k0:2 * k1], in_=std[:, 2 * k0:2 * k1])
             nc.vector.scalar_tensor_tensor(
                 out=offset[:, 2 * k0:2 * k1], in0=mean_var[:, 2 * k0:2 * k1, 0], scalar=-1.0,
                 in1=rstd[:, 2 * k0:2 * k1], op0=ALU.mult, op1=ALU.mult,
@@ -184,14 +187,14 @@ def tile_bandsplitmodule_kernel(
                 for e in range(2):
                     nc.tensor.transpose(bank[:, jl, e, :], z_sb[(r, s)][:, e, 2 * half + jl, :], ident[:])
 
-        def gain_shift(r, s, half, on_vector=False):
+        def gain_shift(r, s, half, on_vector=False, planes=(0, 1)):
             if r < 0:
                 return
-            if s % 2 == 0 and half == 0:
+            if s % 2 == 0 and half == 0 and planes[0] == 0:
                 xn_planes[(r, s // 2)] = ppool.tile([P, PACK, 2, COLS], BF16, name="xn_planes", tag="xn_planes")
             g_col = PASSES * r + s
             b_col = ALL_PASSES + g_col
-            for jl in range(2):
+            for jl in planes:
                 j = 2 * half + jl
                 dst = xn_planes[(r, s // 2)][:, j, s % 2, :]
                 src = z_chan[(r, s, half)][:, jl, :, :].rearrange("p e q -> p (e q)")
@@ -310,54 +313,62 @@ def tile_bandsplitmodule_kernel(
         load_round(1)
         load_round(2)
 
+        gb_sorted = const.tile([P, PACK, P], F32, name="gb_sorted")
+        nc.scalar.copy(out=gb_sorted[:], in_=gb_rows[:].rearrange("m (p j) -> m j p", j=PACK))
+        c_f32 = const.tile([P, P], F32, name="c_f32")
+        nc.scalar.copy(out=c_f32[:], in_=c_rows[:])
+
         to_frames(0, 0)
         to_frames(0, 1)
         stats_join(0, 0, 2)
         stats_sqrt(0, 0, 2)
         stats_finish(0, 0, 2)
-
-        gb_sorted = const.tile([P, PACK, P], F32, name="gb_sorted")
-        nc.vector.tensor_copy(out=gb_sorted[:], in_=gb_rows[:].rearrange("m (p j) -> m j p", j=PACK))
-        gb_bank = ps_z.tile([P, PACK, P], F32, name="gb_bank", tag="z_bank")
-        for j in range(PACK):
-            nc.tensor.transpose(gb_bank[:, j, :], gb_sorted[:, j, :], ident[:])
-        c_f32 = const.tile([P, P], F32, name="c_f32")
-        nc.vector.tensor_copy(out=c_f32[:], in_=c_rows[:])
-        c_bank = ps_z.tile([P, PACK, P], F32, name="c_bank", tag="z_bank")
-        nc.tensor.transpose(c_bank[:, 0, :], c_f32[:], ident[:])
-
         to_frames(0, 2)
         to_frames(0, 3)
         stats_join(0, 2, 4)
 
+        gb_bank = ps_z.tile([P, PACK, P], F32, name="gb_bank", tag="z_bank")
+        for j in range(PACK):
+            nc.tensor.transpose(gb_bank[:, j, :], gb_sorted[:, j, :], ident[:])
+        c_bank = ps_z.tile([P, PACK, P], F32, name="c_bank", tag="z_bank")
+        nc.tensor.transpose(c_bank[:, 0, :], c_f32[:], ident[:])
         g_and_b = const.tile([P, PACK, P], F32, name="g_and_b")
-        nc.vector.tensor_copy(out=g_and_b[:], in_=gb_bank[:])
         c_sb = const.tile([P, BANDS], F32, name="c_sb")
-        nc.vector.tensor_copy(out=c_sb[:], in_=c_bank[:, 0, 0:BANDS])
-
-        copy_w(0, 0, PASSES)
-        quantise_w(0)
+        for s in range(PASSES):
+            copy_w(0, s, s + 1)
 
         for r in range(ROUNDS):
             four_bands_old = r >= 2 and bands_in(r - 2) == 4
             last = r == LAST
             load_round(r + 3)
 
-            finish_bands(r - 2, 0, 2)
+            if four_bands_old:
+                finish_bands(r - 2, 0, 2)
+            if third_plane(r - 1):
+                gain_shift(r - 1, 3, 0, on_vector=True, planes=(1,))
             gain_shift(r - 1, 3, 1, on_vector=True)
-            copy_w(r + 1, 0, 1)
-            regroup_x(r - 1, 2, 4, on_gpsimd=not last)
-            copy_w(r + 1, 1, PASSES)
+            if r > 0:
+                copy_w(r + 1, 0, 1)
+                regroup_x(r - 1, 2, 4, on_gpsimd=not last)
+                copy_w(r + 1, 1, PASSES)
 
             normalise(r, 0)
-            to_frames(r + 1, 0)
-            to_channels(r, 0, 0)
-            normalise(r, 1)
             if r == 0:
+                normalise(r, 1)
                 stats_sqrt(0, 2, 4)
                 stats_finish(0, 2, 4)
+                nc.scalar.copy(out=g_and_b[:], in_=gb_bank[:])
+                nc.scalar.copy(out=c_sb[:], in_=c_bank[:, 0, 0:BANDS])
+            to_frames(r + 1, 0)
+            to_channels(r, 0, 0)
+            if r > 0:
+                normalise(r, 1)
             to_frames(r + 1, 1)
             to_channels(r, 0, 1)
+            if r == 0:
+                quantise_w(0)
+                for s in range(PASSES):
+                    copy_w(1, s, s + 1)
             if four_bands_old:
                 multiply(r - 2, 2, 4)
             if last:
@@ -367,9 +378,8 @@ def tile_bandsplitmodule_kernel(
             to_frames(r + 1, 2)
             to_channels(r, 1, 0)
             normalise(r, 3)
-            if four_bands_old:
-                finish_bands(r - 2, 2, 4)
             to_frames(r + 1, 3)
+            finish_bands(r - 2, 2 if four_bands_old else 0, 4)
             stats_join(r + 1)
             if last:
                 finish_bands(r - 1, 0, 1)
@@ -401,7 +411,7 @@ def tile_bandsplitmodule_kernel(
                 regroup_x(r, 2, 3)
                 quantise_x(r, 2, 3)
                 multiply(r, 2, 3)
-            gain_shift(r, 3, 0)
+            gain_shift(r, 3, 0, planes=(0,) if third_plane(r) else (0, 1))
             if not last:
                 multiply(r - 1, 0, 2 if (r >= 1 and bands_in(r - 1) == 4) else PASSES)
 

@@ -216,12 +216,11 @@ def tile_bandsplitmodule_kernel(
                 xn_grouped[r] = gpool.tile([P, PASSES * COLS, PACK], BF16, name="xn_grouped", tag="xn_grouped", align_bytes=64)
             dst = xn_grouped[r]
             if on_gpsimd:
-                for s in range(s0, s1):
-                    nc.gpsimd.tensor_scalar(
-                        out=dst[:, COLS * s:COLS * (s + 1), :],
-                        in0=xn_planes[(r, s // 2)][:, :, s % 2, :].rearrange("p j c -> p c j"),
-                        scalar1=1.0, scalar2=0.0, op0=ALU.mult, op1=ALU.add,
-                    )
+                nc.gpsimd.tensor_scalar(
+                    out=dst[:, COLS * s0:COLS * s1, :],
+                    in0=xn_planes[(r, s0 // 2)][:].rearrange("p j s c -> p (s c) j"),
+                    scalar1=1.0, scalar2=0.0, op0=ALU.mult, op1=ALU.add,
+                )
                 return
             if s1 - s0 == 2:
                 src = xn_planes[(r, s0 // 2)][:].rearrange("p j s c -> p j (s c)")
@@ -348,9 +347,8 @@ def tile_bandsplitmodule_kernel(
                 gain_shift(r - 1, 3, 0, on_vector=True, planes=(1,))
             gain_shift(r - 1, 3, 1, on_vector=True)
             if r > 0:
-                copy_w(r + 1, 0, 1)
+                copy_w(r + 1, 0, PASSES)
                 regroup_x(r - 1, 2, 4, on_gpsimd=not last)
-                copy_w(r + 1, 1, PASSES)
 
             normalise(r, 0)
             if r == 0:

@@ -54,7 +54,8 @@ def tile_bandsplitmodule_kernel(
         ppool = ctx.enter_context(tc.tile_pool(name="ppool", bufs=4))
         gpool = ctx.enter_context(tc.tile_pool(name="gpool", bufs=2))
         opool = ctx.enter_context(tc.tile_pool(name="opool", bufs=2))
-        ps_x = ctx.enter_context(tc.psum_pool(name="ps_x", bufs=4))
+        ps_s = ctx.enter_context(tc.psum_pool(name="ps_s", bufs=2))
+        ps_x = ctx.enter_context(tc.psum_pool(name="ps_x", bufs=2))
         ps_z = ctx.enter_context(tc.psum_pool(name="ps_z", bufs=3))
         ps_y = ctx.enter_context(tc.psum_pool(name="ps_y", bufs=1))
         ctx.enter_context(tc.manual_schedule())
@@ -113,19 +114,27 @@ def tile_bandsplitmodule_kernel(
             )
             w_mx[r] = (codes, scales)
 
+        def frame_bank(pool, tag, r, s):
+            pairs = x_sb[r][:].bitcast(F32)
+            bank = pool.tile([P, PACK * P], F32, name=tag, tag=tag)
+            for j in range(PACK):
+                c0 = (s * PACK + j) * P
+                nc.tensor.transpose(bank[:, j * P:(j + 1) * P], pairs[:, c0:c0 + P], ident[:])
+            return bank[:].bitcast(BF16).rearrange("q (j p e) -> q j p e", j=PACK, e=2)
+
         def to_frames(r, s):
             if r > LAST:
                 return
             if s == 0:
-                pieces[r] = small.tile([P, 2 * PASSES, 2 * BN_VALUES], F32, name="pieces", tag="pieces")
                 x_frames[r] = []
-            pairs = x_sb[r][:].bitcast(F32)
-            bank = ps_x.tile([P, PACK * P], F32, name="x_bank", tag="x_bank")
-            for j in range(PACK):
-                c0 = (s * PACK + j) * P
-                nc.tensor.transpose(bank[:, j * P:(j + 1) * P], pairs[:, c0:c0 + P], ident[:])
-            view = bank[:].bitcast(BF16).rearrange("q (j p e) -> q j p e", j=PACK, e=2)
-            x_frames[r].append(view)
+            x_frames[r].append(frame_bank(ps_x, "x_bank", r, s))
+
+        def to_stats(r, s):
+            if r > LAST:
+                return
+            if s == 0:
+                pieces[r] = small.tile([P, 2 * PASSES, 2 * BN_VALUES], F32, name="pieces", tag="pieces")
+            view = frame_bank(ps_s, "s_bank", r, s)
             for h in range(2):
                 nc.vector.bn_stats(
                     out=pieces[r][:, 2 * s + h, :],
@@ -317,13 +326,15 @@ def tile_bandsplitmodule_kernel(
         c_f32 = const.tile([P, P], F32, name="c_f32")
         nc.scalar.copy(out=c_f32[:], in_=c_rows[:])
 
+        to_stats(0, 0)
+        to_stats(0, 1)
         to_frames(0, 0)
         to_frames(0, 1)
         stats_join(0, 0, 2)
         stats_sqrt(0, 0, 2)
         stats_finish(0, 0, 2)
-        to_frames(0, 2)
-        to_frames(0, 3)
+        to_stats(0, 2)
+        to_stats(0, 3)
         stats_join(0, 2, 4)
 
         gb_bank = ps_z.tile([P, PACK, P], F32, name="gb_bank", tag="z_bank")
@@ -350,6 +361,8 @@ def tile_bandsplitmodule_kernel(
                 copy_w(r + 1, 0, PASSES)
                 regroup_x(r - 1, 2, 4, on_gpsimd=not last)
 
+            to_stats(r + 1, 0)
+            to_stats(r + 1, 1)
             normalise(r, 0)
             if r == 0:
                 normalise(r, 1)
@@ -357,12 +370,13 @@ def tile_bandsplitmodule_kernel(
                 stats_finish(0, 2, 4)
                 nc.scalar.copy(out=g_and_b[:], in_=gb_bank[:])
                 nc.scalar.copy(out=c_sb[:], in_=c_bank[:, 0, 0:BANDS])
-            to_frames(r + 1, 0)
+            to_frames(r, 2)
             to_channels(r, 0, 0)
             if r > 0:
                 normalise(r, 1)
-            to_frames(r + 1, 1)
+            to_frames(r, 3)
             to_channels(r, 0, 1)
+            to_stats(r + 1, 2)
             if r == 0:
                 quantise_w(0)
                 for s in range(PASSES):
@@ -373,10 +387,11 @@ def tile_bandsplitmodule_kernel(
                 quantise_x(r - 1, 0, PASSES)
                 multiply(r - 1, 0, PASSES)
             normalise(r, 2)
-            to_frames(r + 1, 2)
+            to_frames(r + 1, 0)
             to_channels(r, 1, 0)
+            to_stats(r + 1, 3)
             normalise(r, 3)
-            to_frames(r + 1, 3)
+            to_frames(r + 1, 1)
             finish_bands(r - 2, 2 if four_bands_old else 0, 4)
             stats_join(r + 1)
             if last:

@@ -149,7 +149,6 @@ def tile_bandsplitmodule_kernel(
             if k0 == 0:
                 stats[r] = [
                     small.tile([P, STAT_COLS, 2], F32, name="mean_var", tag="mean_var"),
-                    small.tile([P, STAT_COLS], F32, name="std", tag="std"),
                     small.tile([P, STAT_COLS], F32, name="rstd", tag="rstd"),
                     small.tile([P, STAT_COLS], F32, name="offset", tag="offset"),
                 ]
@@ -165,7 +164,7 @@ def tile_bandsplitmodule_kernel(
                 return
             k1 = bands_in(r) if k1 is None else k1
             nc.scalar.activation(
-                out=stats[r][2][:, 2 * k0:2 * k1], in_=stats[r][0][:, 2 * k0:2 * k1, 1],
+                out=stats[r][1][:, 2 * k0:2 * k1], in_=stats[r][0][:, 2 * k0:2 * k1, 1],
                 func=ACT.Abs_reciprocal_sqrt, bias=EPS, scale=1.0,
             )
 
@@ -173,14 +172,14 @@ def tile_bandsplitmodule_kernel(
             if r > LAST:
                 return
             k1 = bands_in(r) if k1 is None else k1
-            mean_var, std, rstd, offset = stats[r]
+            mean_var, rstd, offset = stats[r]
             nc.vector.scalar_tensor_tensor(
                 out=offset[:, 2 * k0:2 * k1], in0=mean_var[:, 2 * k0:2 * k1, 0], scalar=-1.0,
                 in1=rstd[:, 2 * k0:2 * k1], op0=ALU.mult, op1=ALU.mult,
             )
 
         def normalise(r, s):
-            rstd, offset = stats[r][2], stats[r][3]
+            rstd, offset = stats[r][1], stats[r][2]
             z_sb[(r, s)] = zpool.tile([P, 2, PACK, P], F32, name="z_sb", tag="z_sb")
             for e in range(2):
                 col = 2 * (s * bands_in(r) // PASSES) + e
@@ -218,7 +217,7 @@ def tile_bandsplitmodule_kernel(
                         scale=g_and_b[:, j, g_col:g_col + 1], bias=g_and_b[:, j, b_col:b_col + 1],
                     )
 
-        def regroup_x(r, s0, s1, on_gpsimd=False):
+        def regroup_x(r, s0, s1, on_gpsimd=False, on_scalar=False):
             if r < 0:
                 return
             if s0 == 0:
@@ -235,6 +234,12 @@ def tile_bandsplitmodule_kernel(
                 src = xn_planes[(r, s0 // 2)][:].rearrange("p j s c -> p j (s c)")
             else:
                 src = xn_planes[(r, s0 // 2)][:, :, s0 % 2, :]
+            if on_scalar:
+                nc.scalar.copy(
+                    out=dst[:, COLS * s0:COLS * s1, :].rearrange("p (c u) j -> p c j u", u=4),
+                    in_=src.rearrange("p j (c u) -> p c j u", u=4),
+                )
+                return
             nc.vector.tensor_copy(
                 out=dst[:, COLS * s0:COLS * s1, :].rearrange("p (c u) j -> p c j u", u=4),
                 in_=src.rearrange("p j (c u) -> p c j u", u=4),
@@ -347,9 +352,8 @@ def tile_bandsplitmodule_kernel(
         for s in range(PASSES):
             copy_w(0, s, s + 1)
 
-        for r in range(ROUNDS):
+        for r in range(LAST):
             four_bands_old = r >= 2 and bands_in(r - 2) == 4
-            last = r == LAST
             load_round(r + 3)
 
             if four_bands_old:
@@ -359,10 +363,11 @@ def tile_bandsplitmodule_kernel(
             gain_shift(r - 1, 3, 1, on_vector=True)
             if r > 0:
                 copy_w(r + 1, 0, PASSES)
-                regroup_x(r - 1, 2, 4, on_gpsimd=not last)
+                regroup_x(r - 1, 2, 4, on_gpsimd=True)
 
-            to_stats(r + 1, 0)
-            to_stats(r + 1, 1)
+            if r > 0:
+                to_stats(r + 1, 0)
+                to_stats(r + 1, 1)
             normalise(r, 0)
             if r == 0:
                 normalise(r, 1)
@@ -370,6 +375,8 @@ def tile_bandsplitmodule_kernel(
                 stats_finish(0, 2, 4)
                 nc.scalar.copy(out=g_and_b[:], in_=gb_bank[:])
                 nc.scalar.copy(out=c_sb[:], in_=c_bank[:, 0, 0:BANDS])
+                to_stats(1, 0)
+                to_stats(1, 1)
             to_frames(r, 2)
             to_channels(r, 0, 0)
             if r > 0:
@@ -383,9 +390,6 @@ def tile_bandsplitmodule_kernel(
                     copy_w(1, s, s + 1)
             if four_bands_old:
                 multiply(r - 2, 2, 4)
-            if last:
-                quantise_x(r - 1, 0, PASSES)
-                multiply(r - 1, 0, PASSES)
             normalise(r, 2)
             to_frames(r + 1, 0)
             to_channels(r, 1, 0)
@@ -394,42 +398,64 @@ def tile_bandsplitmodule_kernel(
             to_frames(r + 1, 1)
             finish_bands(r - 2, 2 if four_bands_old else 0, 4)
             stats_join(r + 1)
-            if last:
-                finish_bands(r - 1, 0, 1)
 
             gain_shift(r, 0, 0)
             to_channels(r, 1, 1)
             gain_shift(r, 0, 1)
             to_channels(r, 2, 0)
-            if last:
-                regroup_x(r, 0, 1)
             gain_shift(r, 1, 0)
             to_channels(r, 2, 1)
             gain_shift(r, 1, 1)
             to_channels(r, 3, 0)
             stats_sqrt(r + 1)
-            if not last:
-                quantise_x(r - 1, 0, PASSES)
-                stats_finish(r + 1)
-                regroup_x(r, 0, 2)
-                quantise_w(r + 1)
-            else:
-                regroup_x(r, 1, 2)
-                quantise_x(r, 0, 2)
-                multiply(r, 0, 2)
+            quantise_x(r - 1, 0, PASSES)
+            stats_finish(r + 1)
+            regroup_x(r, 0, 2)
+            quantise_w(r + 1)
             gain_shift(r, 2, 0)
             to_channels(r, 3, 1)
             gain_shift(r, 2, 1)
-            if last:
-                regroup_x(r, 2, 3)
-                quantise_x(r, 2, 3)
-                multiply(r, 2, 3)
             gain_shift(r, 3, 0, planes=(0,) if third_plane(r) else (0, 1))
-            if not last:
-                multiply(r - 1, 0, 2 if (r >= 1 and bands_in(r - 1) == 4) else PASSES)
+            multiply(r - 1, 0, 2 if (r >= 1 and bands_in(r - 1) == 4) else PASSES)
 
-        gain_shift(LAST, 3, 1, on_vector=True)
-        regroup_x(LAST, 3, 4)
-        quantise_x(LAST, 3, 4)
-        multiply(LAST, 3, 4)
-        finish_bands(LAST, 0, 1)
+
+        r = LAST
+        gain_shift(r - 1, 3, 0, on_vector=True, planes=(1,))
+        gain_shift(r - 1, 3, 1, on_vector=True)
+        regroup_x(r - 1, 2, 4, on_gpsimd=True)
+        normalise(r, 0)
+        to_frames(r, 2)
+        to_channels(r, 0, 0)
+        to_channels(r, 0, 1)
+        normalise(r, 1)
+        to_frames(r, 3)
+        to_channels(r, 1, 0)
+        finish_bands(r - 2, 0, 4)
+        gain_shift(r, 0, 0, on_vector=True)
+        to_channels(r, 1, 1)
+        gain_shift(r, 0, 1, on_vector=True)
+        normalise(r, 2)
+        to_channels(r, 2, 0)
+        gain_shift(r, 1, 0, on_vector=True)
+        to_channels(r, 2, 1)
+        normalise(r, 3)
+        gain_shift(r, 1, 1)
+        to_channels(r, 3, 0)
+        quantise_x(r - 1, 0, PASSES)
+        gain_shift(r, 2, 0)
+        to_channels(r, 3, 1)
+        multiply(r - 1, 0, PASSES)
+        regroup_x(r, 0, 2)
+        gain_shift(r, 2, 1)
+        finish_bands(r - 1, 0, 1)
+        quantise_x(r, 0, 2)
+        multiply(r, 0, 2)
+        gain_shift(r, 3, 0)
+        regroup_x(r, 2, 3)
+        gain_shift(r, 3, 1)
+        regroup_x(r, 3, 4, on_scalar=True)
+        quantise_x(r, 2, 3)
+        multiply(r, 2, 3)
+        quantise_x(r, 3, 4)
+        multiply(r, 3, 4)
+        finish_bands(r, 0, 1)

@@ -396,8 +396,10 @@ def tile_bandsplitmodule_kernel(
             to_stats(r + 1, 3)
             normalise(r, 3)
             to_frames(r + 1, 1)
-            finish_bands(r - 2, 2 if four_bands_old else 0, 4)
+            finish_bands(r - 2, 2 if four_bands_old else 0, 3 if four_bands_old else 4)
             stats_join(r + 1)
+            if four_bands_old:
+                finish_bands(r - 2, 3, 4)
 
             gain_shift(r, 0, 0)
             to_channels(r, 1, 1)
@@ -407,13 +409,13 @@ def tile_bandsplitmodule_kernel(
             to_channels(r, 2, 1)
             gain_shift(r, 1, 1)
             to_channels(r, 3, 0)
-            stats_sqrt(r + 1)
             quantise_x(r - 1, 0, PASSES)
+            gain_shift(r, 2, 0)
+            to_channels(r, 3, 1)
+            stats_sqrt(r + 1)
             stats_finish(r + 1)
             regroup_x(r, 0, 2)
             quantise_w(r + 1)
-            gain_shift(r, 2, 0)
-            to_channels(r, 3, 1)
             gain_shift(r, 2, 1)
             gain_shift(r, 3, 0, planes=(0,) if third_plane(r) else (0, 1))
             multiply(r - 1, 0, 2 if (r >= 1 and bands_in(r - 1) == 4) else PASSES)

@@ -35,6 +35,10 @@ def third_plane(r):
     return 8 <= r < LAST
 
 
+def heavy(r):
+    return 1 <= r <= 5
+
+
 def first_band(r):
     return 4 * r if r < 4 else (2 * r + 8 if r < 8 else r + 16)
 
@@ -226,7 +230,8 @@ def tile_bandsplitmodule_kernel(
             if on_gpsimd:
                 nc.gpsimd.tensor_scalar(
                     out=dst[:, COLS * s0:COLS * s1, :],
-                    in0=xn_planes[(r, s0 // 2)][:].rearrange("p j s c -> p (s c) j"),
+                    in0=xn_planes[(r, s0 // 2)][:].rearrange("p j s c -> p (s c) j") if s1 - s0 == 2
+                    else xn_planes[(r, s0 // 2)][:, :, s0 % 2, :].rearrange("p j c -> p c j"),
                     scalar1=1.0, scalar2=0.0, op0=ALU.mult, op1=ALU.add,
                 )
                 return
@@ -363,6 +368,8 @@ def tile_bandsplitmodule_kernel(
             gain_shift(r - 1, 3, 1, on_vector=True)
             if r > 0:
                 copy_w(r + 1, 0, PASSES)
+                if heavy(r - 1):
+                    regroup_x(r - 1, 1, 2, on_gpsimd=True)
                 regroup_x(r - 1, 2, 4, on_gpsimd=True)
 
             if r > 0:
@@ -414,7 +421,7 @@ def tile_bandsplitmodule_kernel(
             to_channels(r, 3, 1)
             stats_sqrt(r + 1)
             stats_finish(r + 1)
-            regroup_x(r, 0, 2)
+            regroup_x(r, 0, 1 if heavy(r) else 2)
             quantise_w(r + 1)
             gain_shift(r, 2, 1)
             gain_shift(r, 3, 0, planes=(0,) if third_plane(r) else (0, 1))

@@ -32,11 +32,15 @@ def bands_in(r):
 
 
 def third_plane(r):
-    return 8 <= r < LAST
+    return False
 
 
 def heavy(r):
     return 1 <= r <= 5
+
+
+def out_on_scalar(band):
+    return False
 
 
 def first_band(r):
@@ -58,8 +62,7 @@ def tile_bandsplitmodule_kernel(
         ppool = ctx.enter_context(tc.tile_pool(name="ppool", bufs=4))
         gpool = ctx.enter_context(tc.tile_pool(name="gpool", bufs=2))
         opool = ctx.enter_context(tc.tile_pool(name="opool", bufs=2))
-        ps_s = ctx.enter_context(tc.psum_pool(name="ps_s", bufs=2))
-        ps_x = ctx.enter_context(tc.psum_pool(name="ps_x", bufs=2))
+        ps_x = ctx.enter_context(tc.psum_pool(name="ps_x", bufs=4))
         ps_z = ctx.enter_context(tc.psum_pool(name="ps_z", bufs=3))
         ps_y = ctx.enter_context(tc.psum_pool(name="ps_y", bufs=1))
         ctx.enter_context(tc.manual_schedule())
@@ -133,12 +136,12 @@ def tile_bandsplitmodule_kernel(
                 x_frames[r] = []
             x_frames[r].append(frame_bank(ps_x, "x_bank", r, s))
 
-        def to_stats(r, s):
+        def take_stats(r, s):
             if r > LAST:
                 return
             if s == 0:
                 pieces[r] = small.tile([P, 2 * PASSES, 2 * BN_VALUES], F32, name="pieces", tag="pieces")
-            view = frame_bank(ps_s, "s_bank", r, s)
+            view = x_frames[r][s]
             for h in range(2):
                 nc.vector.bn_stats(
                     out=pieces[r][:, 2 * s + h, :],
@@ -221,33 +224,21 @@ def tile_bandsplitmodule_kernel(
                         scale=g_and_b[:, j, g_col:g_col + 1], bias=g_and_b[:, j, b_col:b_col + 1],
                     )
 
-        def regroup_x(r, s0, s1, on_gpsimd=False, on_scalar=False):
+        def regroup_x(r, c0, c1, engine):
             if r < 0:
                 return
-            if s0 == 0:
+            if r not in xn_grouped:
                 xn_grouped[r] = gpool.tile([P, PASSES * COLS, PACK], BF16, name="xn_grouped", tag="xn_grouped", align_bytes=64)
-            dst = xn_grouped[r]
-            if on_gpsimd:
+            pair = c0 // (2 * COLS)
+            src = xn_planes[(r, pair)][:].rearrange("p j s c -> p j (s c)")[:, :, c0 - 2 * COLS * pair:c1 - 2 * COLS * pair]
+            dst = xn_grouped[r][:, c0:c1, :]
+            if engine == "gpsimd":
                 nc.gpsimd.tensor_scalar(
-                    out=dst[:, COLS * s0:COLS * s1, :],
-                    in0=xn_planes[(r, s0 // 2)][:].rearrange("p j s c -> p (s c) j") if s1 - s0 == 2
-                    else xn_planes[(r, s0 // 2)][:, :, s0 % 2, :].rearrange("p j c -> p c j"),
-                    scalar1=1.0, scalar2=0.0, op0=ALU.mult, op1=ALU.add,
+                    out=dst, in0=src.rearrange("p j c -> p c j"), scalar1=1.0, scalar2=0.0, op0=ALU.mult, op1=ALU.add,
                 )
                 return
-            if s1 - s0 == 2:
-                src = xn_planes[(r, s0 // 2)][:].rearrange("p j s c -> p j (s c)")
-            else:
-                src = xn_planes[(r, s0 // 2)][:, :, s0 % 2, :]
-            if on_scalar:
-                nc.scalar.copy(
-                    out=dst[:, COLS * s0:COLS * s1, :].rearrange("p (c u) j -> p c j u", u=4),
-                    in_=src.rearrange("p j (c u) -> p c j u", u=4),
-                )
-                return
-            nc.vector.tensor_copy(
-                out=dst[:, COLS * s0:COLS * s1, :].rearrange("p (c u) j -> p c j u", u=4),
-                in_=src.rearrange("p j (c u) -> p c j u", u=4),
+            (nc.scalar.copy if engine == "scalar" else nc.vector.tensor_copy)(
+                out=dst.rearrange("p (c u) j -> p c j u", u=4), in_=src.rearrange("p j (c u) -> p c j u", u=4),
             )
 
         def quantise_x(r, s0, s1):
@@ -294,11 +285,14 @@ def tile_bandsplitmodule_kernel(
                 if band % 4 == 0:
                     out_sb[four] = opool.tile([P, 2, 4, P], F32, name="out_sb", tag="out_sb")
                 c0 = COLS * (k % 2)
-                nc.vector.tensor_scalar(
-                    out=out_sb[four][:, :, band % 4, :].rearrange("n i (q e) -> n i q e", e=2),
-                    in0=sums[r][:, c0:c0 + COLS].rearrange("n (e i q) -> n i q e", e=2, i=2),
-                    scalar1=c_sb[:, band:band + 1], scalar2=None, op0=ALU.add,
-                )
+                dst = out_sb[four][:, :, band % 4, :].rearrange("n i (q e) -> n i q e", e=2)
+                src = sums[r][:, c0:c0 + COLS].rearrange("n (e i q) -> n i q e", e=2, i=2)
+                if out_on_scalar(band):
+                    nc.scalar.activation(out=dst, in_=src, func=ACT.Identity, scale=1.0, bias=c_sb[:, band:band + 1])
+                else:
+                    nc.vector.tensor_scalar(
+                        out=dst, in0=src, scalar1=c_sb[:, band:band + 1], scalar2=None, op0=ALU.add,
+                    )
                 if band == BANDS - 1:
                     first = band
                 elif band % 4 == 3 or band == BANDS - 2:
@@ -336,15 +330,15 @@ def tile_bandsplitmodule_kernel(
         c_f32 = const.tile([P, P], F32, name="c_f32")
         nc.scalar.copy(out=c_f32[:], in_=c_rows[:])
 
-        to_stats(0, 0)
-        to_stats(0, 1)
-        to_frames(0, 0)
-        to_frames(0, 1)
+        for s in range(PASSES):
+            to_frames(0, s)
+        take_stats(0, 0)
+        take_stats(0, 1)
         stats_join(0, 0, 2)
         stats_sqrt(0, 0, 2)
+        take_stats(0, 2)
         stats_finish(0, 0, 2)
-        to_stats(0, 2)
-        to_stats(0, 3)
+        take_stats(0, 3)
         stats_join(0, 2, 4)
 
         gb_bank = ps_z.tile([P, PACK, P], F32, name="gb_bank", tag="z_bank")
@@ -360,54 +354,44 @@ def tile_bandsplitmodule_kernel(
         for r in range(LAST):
             four_bands_old = r >= 2 and bands_in(r - 2) == 4
             load_round(r + 3)
-
-            if four_bands_old:
-                finish_bands(r - 2, 0, 2)
             if third_plane(r - 1):
                 gain_shift(r - 1, 3, 0, on_vector=True, planes=(1,))
             gain_shift(r - 1, 3, 1, on_vector=True)
             if r > 0:
                 copy_w(r + 1, 0, PASSES)
-                if heavy(r - 1):
-                    regroup_x(r - 1, 1, 2, on_gpsimd=True)
-                regroup_x(r - 1, 2, 4, on_gpsimd=True)
-
-            if r > 0:
-                to_stats(r + 1, 0)
-                to_stats(r + 1, 1)
+                regroup_x(r - 1, 512, 1024, "gpsimd")
             normalise(r, 0)
             if r == 0:
-                normalise(r, 1)
                 stats_sqrt(0, 2, 4)
                 stats_finish(0, 2, 4)
-                nc.scalar.copy(out=g_and_b[:], in_=gb_bank[:])
-                nc.scalar.copy(out=c_sb[:], in_=c_bank[:, 0, 0:BANDS])
-                to_stats(1, 0)
-                to_stats(1, 1)
-            to_frames(r, 2)
-            to_channels(r, 0, 0)
-            if r > 0:
                 normalise(r, 1)
-            to_frames(r, 3)
-            to_channels(r, 0, 1)
-            to_stats(r + 1, 2)
+            to_frames(r + 1, 0)
+            if four_bands_old:
+                finish_bands(r - 2, 0, 2)
+            take_stats(r + 1, 0)
+            to_channels(r, 0, 0)
             if r == 0:
                 quantise_w(0)
                 for s in range(PASSES):
                     copy_w(1, s, s + 1)
+            else:
+                normalise(r, 1)
+            to_frames(r + 1, 1)
+            take_stats(r + 1, 1)
+            to_channels(r, 0, 1)
+            normalise(r, 2)
+            to_frames(r + 1, 2)
+            take_stats(r + 1, 2)
+            to_channels(r, 1, 0)
+            normalise(r, 3)
+            if r == 0:
+                nc.scalar.copy(out=g_and_b[:], in_=gb_bank[:])
+                nc.scalar.copy(out=c_sb[:], in_=c_bank[:, 0, 0:BANDS])
+            to_frames(r + 1, 3)
+            take_stats(r + 1, 3)
             if four_bands_old:
                 multiply(r - 2, 2, 4)
-            normalise(r, 2)
-            to_frames(r + 1, 0)
-            to_channels(r, 1, 0)
-            to_stats(r + 1, 3)
-            normalise(r, 3)
-            to_frames(r + 1, 1)
-            finish_bands(r - 2, 2 if four_bands_old else 0, 3 if four_bands_old else 4)
             stats_join(r + 1)
-            if four_bands_old:
-                finish_bands(r - 2, 3, 4)
-
             gain_shift(r, 0, 0)
             to_channels(r, 1, 1)
             gain_shift(r, 0, 1)
@@ -416,28 +400,26 @@ def tile_bandsplitmodule_kernel(
             to_channels(r, 2, 1)
             gain_shift(r, 1, 1)
             to_channels(r, 3, 0)
+            finish_bands(r - 2, 2 if four_bands_old else 0, 4)
             quantise_x(r - 1, 0, PASSES)
             gain_shift(r, 2, 0)
-            to_channels(r, 3, 1)
             stats_sqrt(r + 1)
             stats_finish(r + 1)
-            regroup_x(r, 0, 1 if heavy(r) else 2)
+            to_channels(r, 3, 1)
+            regroup_x(r, 0, 512, "vector")
             quantise_w(r + 1)
             gain_shift(r, 2, 1)
             gain_shift(r, 3, 0, planes=(0,) if third_plane(r) else (0, 1))
             multiply(r - 1, 0, 2 if (r >= 1 and bands_in(r - 1) == 4) else PASSES)
 
-
         r = LAST
         gain_shift(r - 1, 3, 0, on_vector=True, planes=(1,))
         gain_shift(r - 1, 3, 1, on_vector=True)
-        regroup_x(r - 1, 2, 4, on_gpsimd=True)
+        regroup_x(r - 1, 512, 1024, "gpsimd")
         normalise(r, 0)
-        to_frames(r, 2)
         to_channels(r, 0, 0)
         to_channels(r, 0, 1)
         normalise(r, 1)
-        to_frames(r, 3)
         to_channels(r, 1, 0)
         finish_bands(r - 2, 0, 4)
         gain_shift(r, 0, 0, on_vector=True)
@@ -454,15 +436,15 @@ def tile_bandsplitmodule_kernel(
         gain_shift(r, 2, 0)
         to_channels(r, 3, 1)
         multiply(r - 1, 0, PASSES)
-        regroup_x(r, 0, 2)
+        regroup_x(r, 0, 512, "vector")
         gain_shift(r, 2, 1)
         finish_bands(r - 1, 0, 1)
         quantise_x(r, 0, 2)
         multiply(r, 0, 2)
         gain_shift(r, 3, 0)
-        regroup_x(r, 2, 3)
+        regroup_x(r, 512, 768, "vector")
         gain_shift(r, 3, 1)
-        regroup_x(r, 3, 4, on_scalar=True)
+        regroup_x(r, 768, 1024, "scalar")
         quantise_x(r, 2, 3)
         multiply(r, 2, 3)
         quantise_x(r, 3, 4)

@@ -31,16 +31,16 @@ def bands_in(r):
     return 4 if r < 4 else (2 if r < 8 else 1)
 
 
-def third_plane(r):
-    return False
-
-
-def heavy(r):
-    return 1 <= r <= 5
+def vector_planes(r):
+    if r == 0:
+        return 4
+    if r == LAST - 1:
+        return 1
+    return 2 if r < 5 else 3
 
 
 def out_on_scalar(band):
-    return False
+    return band < 24 and band % 4 == 3
 
 
 def first_band(r):
@@ -351,12 +351,19 @@ def tile_bandsplitmodule_kernel(
         for s in range(PASSES):
             copy_w(0, s, s + 1)
 
+        def vector_share(r):
+            if r < 0:
+                return
+            v = vector_planes(r)
+            if v > 2:
+                gain_shift(r, 3, 0, on_vector=True, planes=(1,) if v == 3 else (0, 1))
+            if v:
+                gain_shift(r, 3, 1, on_vector=True, planes=(1,) if v == 1 else (0, 1))
+
         for r in range(LAST):
             four_bands_old = r >= 2 and bands_in(r - 2) == 4
             load_round(r + 3)
-            if third_plane(r - 1):
-                gain_shift(r - 1, 3, 0, on_vector=True, planes=(1,))
-            gain_shift(r - 1, 3, 1, on_vector=True)
+            vector_share(r - 1)
             if r > 0:
                 copy_w(r + 1, 0, PASSES)
                 regroup_x(r - 1, 512, 1024, "gpsimd")
@@ -389,18 +396,21 @@ def tile_bandsplitmodule_kernel(
                 nc.scalar.copy(out=c_sb[:], in_=c_bank[:, 0, 0:BANDS])
             to_frames(r + 1, 3)
             take_stats(r + 1, 3)
-            if four_bands_old:
-                multiply(r - 2, 2, 4)
+            if not four_bands_old:
+                finish_bands(r - 2, 0, 4)
             stats_join(r + 1)
             gain_shift(r, 0, 0)
             to_channels(r, 1, 1)
+            if four_bands_old:
+                multiply(r - 2, 2, 4)
             gain_shift(r, 0, 1)
             to_channels(r, 2, 0)
             gain_shift(r, 1, 0)
             to_channels(r, 2, 1)
             gain_shift(r, 1, 1)
             to_channels(r, 3, 0)
-            finish_bands(r - 2, 2 if four_bands_old else 0, 4)
+            if four_bands_old:
+                finish_bands(r - 2, 2, 4)
             quantise_x(r - 1, 0, PASSES)
             gain_shift(r, 2, 0)
             stats_sqrt(r + 1)
@@ -409,12 +419,15 @@ def tile_bandsplitmodule_kernel(
             regroup_x(r, 0, 512, "vector")
             quantise_w(r + 1)
             gain_shift(r, 2, 1)
-            gain_shift(r, 3, 0, planes=(0,) if third_plane(r) else (0, 1))
+            v = vector_planes(r)
+            if v < 4:
+                gain_shift(r, 3, 0, planes=(0,) if v == 3 else (0, 1))
+            if v < 2:
+                gain_shift(r, 3, 1, planes=(0,) if v == 1 else (0, 1))
             multiply(r - 1, 0, 2 if (r >= 1 and bands_in(r - 1) == 4) else PASSES)
 
         r = LAST
-        gain_shift(r - 1, 3, 0, on_vector=True, planes=(1,))
-        gain_shift(r - 1, 3, 1, on_vector=True)
+        vector_share(r - 1)
         regroup_x(r - 1, 512, 1024, "gpsimd")
         normalise(r, 0)
         to_channels(r, 0, 0)
@@ -438,8 +451,8 @@ def tile_bandsplitmodule_kernel(
         multiply(r - 1, 0, PASSES)
         regroup_x(r, 0, 512, "vector")
         gain_shift(r, 2, 1)
-        finish_bands(r - 1, 0, 1)
         quantise_x(r, 0, 2)
+        finish_bands(r - 1, 0, 1)
         multiply(r, 0, 2)
         gain_shift(r, 3, 0)
         regroup_x(r, 512, 768, "vector")

@@ -34,13 +34,13 @@ def bands_in(r):
 def vector_planes(r):
     if r == 0:
         return 4
-    if r == LAST - 1:
+    if r < 5:
         return 1
-    return 2 if r < 5 else 3
+    return 2 if r == LAST - 1 else 3
 
 
 def out_on_scalar(band):
-    return band < 24 and band % 4 == 3
+    return False
 
 
 def first_band(r):
@@ -263,11 +263,13 @@ def tile_bandsplitmodule_kernel(
             x_codes, x_scales = xn_mx[r]
             for s in range(s0, s1):
                 k = s // passes_per_band
-                if k % 2 == 0 and s % passes_per_band == 0:
-                    sums[r] = ps_y.tile([P, 2 * COLS], F32, name="sums", tag="sums")
+                if s == 0:
+                    sums[(r, 0)] = ps_y.tile([P, 2 * COLS], F32, name="sums", tag="sums")
+                if s == 2 and k == 2:
+                    sums[(r, 1)] = ps_z.tile([P, 2 * COLS], F32, name="z_bank", tag="z_bank")
                 c0 = COLS * (k % 2)
                 nc.tensor.matmul_mx(
-                    out=sums[r][:, c0:c0 + COLS],
+                    out=sums[(r, k // 2)][:, c0:c0 + COLS],
                     lhsT=w_codes[:, s * P:(s + 1) * P].bitcast(FP8X4),
                     lhsT_scale=w_scales[:, s * P:(s + 1) * P],
                     rhs=x_codes[:, COLS * s:COLS * (s + 1)].bitcast(FP8X4),
@@ -286,7 +288,7 @@ def tile_bandsplitmodule_kernel(
                     out_sb[four] = opool.tile([P, 2, 4, P], F32, name="out_sb", tag="out_sb")
                 c0 = COLS * (k % 2)
                 dst = out_sb[four][:, :, band % 4, :].rearrange("n i (q e) -> n i q e", e=2)
-                src = sums[r][:, c0:c0 + COLS].rearrange("n (e i q) -> n i q e", e=2, i=2)
+                src = sums[(r, k // 2)][:, c0:c0 + COLS].rearrange("n (e i q) -> n i q e", e=2, i=2)
                 if out_on_scalar(band):
                     nc.scalar.activation(out=dst, in_=src, func=ACT.Identity, scale=1.0, bias=c_sb[:, band:band + 1])
                 else:
@@ -374,7 +376,7 @@ def tile_bandsplitmodule_kernel(
                 normalise(r, 1)
             to_frames(r + 1, 0)
             if four_bands_old:
-                finish_bands(r - 2, 0, 2)
+                finish_bands(r - 2, 0, 4)
             take_stats(r + 1, 0)
             to_channels(r, 0, 0)
             if r == 0:
@@ -401,16 +403,12 @@ def tile_bandsplitmodule_kernel(
             stats_join(r + 1)
             gain_shift(r, 0, 0)
             to_channels(r, 1, 1)
-            if four_bands_old:
-                multiply(r - 2, 2, 4)
             gain_shift(r, 0, 1)
             to_channels(r, 2, 0)
             gain_shift(r, 1, 0)
             to_channels(r, 2, 1)
             gain_shift(r, 1, 1)
             to_channels(r, 3, 0)
-            if four_bands_old:
-                finish_bands(r - 2, 2, 4)
             quantise_x(r - 1, 0, PASSES)
             gain_shift(r, 2, 0)
             stats_sqrt(r + 1)
@@ -424,7 +422,7 @@ def tile_bandsplitmodule_kernel(
                 gain_shift(r, 3, 0, planes=(0,) if v == 3 else (0, 1))
             if v < 2:
                 gain_shift(r, 3, 1, planes=(0,) if v == 1 else (0, 1))
-            multiply(r - 1, 0, 2 if (r >= 1 and bands_in(r - 1) == 4) else PASSES)
+            multiply(r - 1, 0, PASSES)
 
         r = LAST
         vector_share(r - 1)

@@ -34,13 +34,7 @@ def bands_in(r):
 def vector_planes(r):
     if r == 0:
         return 4
-    if r < 5:
-        return 1
-    return 2 if r == LAST - 1 else 3
-
-
-def out_on_scalar(band):
-    return False
+    return 1 if r < 5 else 2
 
 
 def first_band(r):
@@ -62,9 +56,8 @@ def tile_bandsplitmodule_kernel(
         ppool = ctx.enter_context(tc.tile_pool(name="ppool", bufs=4))
         gpool = ctx.enter_context(tc.tile_pool(name="gpool", bufs=2))
         opool = ctx.enter_context(tc.tile_pool(name="opool", bufs=2))
-        ps_x = ctx.enter_context(tc.psum_pool(name="ps_x", bufs=4))
+        ps_x = ctx.enter_context(tc.psum_pool(name="ps_x", bufs=5))
         ps_z = ctx.enter_context(tc.psum_pool(name="ps_z", bufs=3))
-        ps_y = ctx.enter_context(tc.psum_pool(name="ps_y", bufs=1))
         ctx.enter_context(tc.manual_schedule())
 
         x_sb, w_raw, w_grouped, w_mx = {}, {}, {}, {}
@@ -263,10 +256,8 @@ def tile_bandsplitmodule_kernel(
             x_codes, x_scales = xn_mx[r]
             for s in range(s0, s1):
                 k = s // passes_per_band
-                if s == 0:
-                    sums[(r, 0)] = ps_y.tile([P, 2 * COLS], F32, name="sums", tag="sums")
-                if s == 2 and k == 2:
-                    sums[(r, 1)] = ps_z.tile([P, 2 * COLS], F32, name="z_bank", tag="z_bank")
+                if s == 0 or (s == 2 and k == 2):
+                    sums[(r, k // 2)] = ps_z.tile([P, 2 * COLS], F32, name="z_bank", tag="z_bank")
                 c0 = COLS * (k % 2)
                 nc.tensor.matmul_mx(
                     out=sums[(r, k // 2)][:, c0:c0 + COLS],
@@ -278,33 +269,24 @@ def tile_bandsplitmodule_kernel(
                     stop=(s % passes_per_band == passes_per_band - 1),
                 )
 
-        def finish_bands(r, k0, k1):
+        def finish_bands(r):
             if r < 0:
                 return
-            for k in range(k0, min(k1, bands_in(r))):
+            for k in range(bands_in(r)):
                 band = first_band(r) + k
-                four = band // 4
-                if band % 4 == 0:
-                    out_sb[four] = opool.tile([P, 2, 4, P], F32, name="out_sb", tag="out_sb")
+                group, slot = (BANDS // 4, 0) if band == BANDS - 1 else divmod(band, 4)
+                if slot == 0:
+                    out_sb[group] = opool.tile([P, 2, 4, P], F32, name="out_sb", tag="out_sb")
                 c0 = COLS * (k % 2)
-                dst = out_sb[four][:, :, band % 4, :].rearrange("n i (q e) -> n i q e", e=2)
-                src = sums[(r, k // 2)][:, c0:c0 + COLS].rearrange("n (e i q) -> n i q e", e=2, i=2)
-                if out_on_scalar(band):
-                    nc.scalar.activation(out=dst, in_=src, func=ACT.Identity, scale=1.0, bias=c_sb[:, band:band + 1])
-                else:
-                    nc.vector.tensor_scalar(
-                        out=dst, in0=src, scalar1=c_sb[:, band:band + 1], scalar2=None, op0=ALU.add,
-                    )
-                if band == BANDS - 1:
-                    first = band
-                elif band % 4 == 3 or band == BANDS - 2:
-                    first = 4 * four
-                else:
-                    first = None
-                if first is not None:
+                nc.vector.tensor_scalar(
+                    out=out_sb[group][:, :, slot, :].rearrange("n i (q e) -> n i q e", e=2),
+                    in0=sums[(r, k // 2)][:, c0:c0 + COLS].rearrange("n (e i q) -> n i q e", e=2, i=2),
+                    scalar1=c_sb[:, band:band + 1], scalar2=None, op0=ALU.add,
+                )
+                if slot == 3 or band >= BANDS - 2:
                     nc.sync.dma_start(
-                        out=out[:, :, first:band + 1, :].rearrange("i n k t -> n i (k t)"),
-                        in_=out_sb[four][:, :, first % 4:band % 4 + 1, :].rearrange("n i k t -> n i (k t)"),
+                        out=out[:, :, band - slot:band + 1, :].rearrange("i n k t -> n i (k t)"),
+                        in_=out_sb[group][:, :, 0:slot + 1, :].rearrange("n i k t -> n i (k t)"),
                     )
 
         ident = const.tile([P, P], F32, name="ident")
@@ -350,6 +332,10 @@ def tile_bandsplitmodule_kernel(
         nc.tensor.transpose(c_bank[:, 0, :], c_f32[:], ident[:])
         g_and_b = const.tile([P, PACK, P], F32, name="g_and_b")
         c_sb = const.tile([P, BANDS], F32, name="c_sb")
+        nc.scalar.copy(out=g_and_b[:], in_=gb_bank[:])
+        nc.scalar.copy(out=c_sb[:], in_=c_bank[:, 0, 0:BANDS])
+
+        to_frames(1, 0)
         for s in range(PASSES):
             copy_w(0, s, s + 1)
 
@@ -363,20 +349,18 @@ def tile_bandsplitmodule_kernel(
                 gain_shift(r, 3, 1, on_vector=True, planes=(1,) if v == 1 else (0, 1))
 
         for r in range(LAST):
-            four_bands_old = r >= 2 and bands_in(r - 2) == 4
             load_round(r + 3)
             vector_share(r - 1)
             if r > 0:
                 copy_w(r + 1, 0, PASSES)
                 regroup_x(r - 1, 512, 1024, "gpsimd")
+            finish_bands(r - 2)
             normalise(r, 0)
             if r == 0:
                 stats_sqrt(0, 2, 4)
                 stats_finish(0, 2, 4)
                 normalise(r, 1)
-            to_frames(r + 1, 0)
-            if four_bands_old:
-                finish_bands(r - 2, 0, 4)
+            to_frames(r + 1, 1)
             take_stats(r + 1, 0)
             to_channels(r, 0, 0)
             if r == 0:
@@ -385,22 +369,15 @@ def tile_bandsplitmodule_kernel(
                     copy_w(1, s, s + 1)
             else:
                 normalise(r, 1)
-            to_frames(r + 1, 1)
+            to_frames(r + 1, 2)
             take_stats(r + 1, 1)
             to_channels(r, 0, 1)
             normalise(r, 2)
-            to_frames(r + 1, 2)
+            to_frames(r + 1, 3)
             take_stats(r + 1, 2)
             to_channels(r, 1, 0)
             normalise(r, 3)
-            if r == 0:
-                nc.scalar.copy(out=g_and_b[:], in_=gb_bank[:])
-                nc.scalar.copy(out=c_sb[:], in_=c_bank[:, 0, 0:BANDS])
-            to_frames(r + 1, 3)
             take_stats(r + 1, 3)
-            if not four_bands_old:
-                finish_bands(r - 2, 0, 4)
-            stats_join(r + 1)
             gain_shift(r, 0, 0)
             to_channels(r, 1, 1)
             gain_shift(r, 0, 1)
@@ -409,14 +386,16 @@ def tile_bandsplitmodule_kernel(
             to_channels(r, 2, 1)
             gain_shift(r, 1, 1)
             to_channels(r, 3, 0)
+            stats_join(r + 1)
             quantise_x(r - 1, 0, PASSES)
             gain_shift(r, 2, 0)
             stats_sqrt(r + 1)
-            stats_finish(r + 1)
             to_channels(r, 3, 1)
-            regroup_x(r, 0, 512, "vector")
-            quantise_w(r + 1)
+            to_frames(r + 2, 0)
             gain_shift(r, 2, 1)
+            stats_finish(r + 1)
+            quantise_w(r + 1)
+            regroup_x(r, 0, 512, "vector")
             v = vector_planes(r)
             if v < 4:
                 gain_shift(r, 3, 0, planes=(0,) if v == 3 else (0, 1))
@@ -432,7 +411,7 @@ def tile_bandsplitmodule_kernel(
         to_channels(r, 0, 1)
         normalise(r, 1)
         to_channels(r, 1, 0)
-        finish_bands(r - 2, 0, 4)
+        finish_bands(r - 2)
         gain_shift(r, 0, 0, on_vector=True)
         to_channels(r, 1, 1)
         gain_shift(r, 0, 1, on_vector=True)
@@ -441,7 +420,7 @@ def tile_bandsplitmodule_kernel(
         gain_shift(r, 1, 0, on_vector=True)
         to_channels(r, 2, 1)
         normalise(r, 3)
-        gain_shift(r, 1, 1)
+        gain_shift(r, 1, 1, on_vector=True)
         to_channels(r, 3, 0)
         quantise_x(r - 1, 0, PASSES)
         gain_shift(r, 2, 0)
@@ -449,15 +428,15 @@ def tile_bandsplitmodule_kernel(
         multiply(r - 1, 0, PASSES)
         regroup_x(r, 0, 512, "vector")
         gain_shift(r, 2, 1)
+        regroup_x(r, 512, 768, "vector")
         quantise_x(r, 0, 2)
-        finish_bands(r - 1, 0, 1)
         multiply(r, 0, 2)
         gain_shift(r, 3, 0)
-        regroup_x(r, 512, 768, "vector")
         gain_shift(r, 3, 1)
         regroup_x(r, 768, 1024, "scalar")
+        finish_bands(r - 1)
         quantise_x(r, 2, 3)
         multiply(r, 2, 3)
         quantise_x(r, 3, 4)
         multiply(r, 3, 4)
-        finish_bands(r, 0, 1)
+        finish_bands(r)

@@ -32,9 +32,9 @@ def bands_in(r):
 
 
 def vector_planes(r):
-    if r == 0:
-        return 4
-    return 1 if r < 5 else 2
+    if r == LAST - 1:
+        return 2
+    return 4 if r == 0 else {4: 1, 2: 2, 1: 3}[bands_in(r - 1)]
 
 
 def first_band(r):
@@ -93,8 +93,6 @@ def tile_bandsplitmodule_kernel(
             nc.sync.dma_start(out=w_raw[r][:], in_=w_rows)
 
         def copy_w(r, s0, s1):
-            if r > LAST:
-                return
             if s0 == 0:
                 w_grouped[r] = wgpool.tile([P, PASSES, P, PACK], BF16, name="w_grouped", tag="w_grouped", align_bytes=64)
             nc.gpsimd.tensor_scalar(
@@ -104,8 +102,6 @@ def tile_bandsplitmodule_kernel(
             )
 
         def quantise_w(r):
-            if r > LAST:
-                return
             codes = wpool.tile([P, PASSES * P], U32, name="w_codes", tag="w_codes", align_bytes=64)
             scales = wpool.tile([P, PASSES * P], U8, name="w_scales", tag="w_scales", align_bytes=64)
             nc.vector.quantize_mx(
@@ -114,36 +110,26 @@ def tile_bandsplitmodule_kernel(
             )
             w_mx[r] = (codes, scales)
 
-        def frame_bank(pool, tag, r, s):
-            pairs = x_sb[r][:].bitcast(F32)
-            bank = pool.tile([P, PACK * P], F32, name=tag, tag=tag)
-            for j in range(PACK):
-                c0 = (s * PACK + j) * P
-                nc.tensor.transpose(bank[:, j * P:(j + 1) * P], pairs[:, c0:c0 + P], ident[:])
-            return bank[:].bitcast(BF16).rearrange("q (j p e) -> q j p e", j=PACK, e=2)
-
         def to_frames(r, s):
             if r > LAST:
                 return
-            if s == 0:
-                x_frames[r] = []
-            x_frames[r].append(frame_bank(ps_x, "x_bank", r, s))
+            pairs = x_sb[r][:].bitcast(F32)
+            bank = ps_x.tile([P, PACK * P], F32, name="x_bank", tag="x_bank")
+            for j in range(PACK):
+                c0 = (s * PACK + j) * P
+                nc.tensor.transpose(bank[:, j * P:(j + 1) * P], pairs[:, c0:c0 + P], ident[:])
+            x_frames[(r, s)] = bank[:].bitcast(BF16).rearrange("q (j p e) -> q j p e", j=PACK, e=2)
 
         def take_stats(r, s):
-            if r > LAST:
-                return
             if s == 0:
                 pieces[r] = small.tile([P, 2 * PASSES, 2 * BN_VALUES], F32, name="pieces", tag="pieces")
-            view = x_frames[r][s]
             for h in range(2):
                 nc.vector.bn_stats(
                     out=pieces[r][:, 2 * s + h, :],
-                    in_=view[:, 2 * h:2 * h + 2, :, :].rearrange("q j p e -> q (j p e)"),
+                    in_=x_frames[(r, s)][:, 2 * h:2 * h + 2, :, :].rearrange("q j p e -> q (j p e)"),
                 )
 
         def stats_join(r, k0=0, k1=None):
-            if r > LAST:
-                return
             k1 = bands_in(r) if k1 is None else k1
             pieces_per_band = 2 * PASSES // bands_in(r)
             if k0 == 0:
@@ -160,8 +146,6 @@ def tile_bandsplitmodule_kernel(
                     )
 
         def stats_sqrt(r, k0=0, k1=None):
-            if r > LAST:
-                return
             k1 = bands_in(r) if k1 is None else k1
             nc.scalar.activation(
                 out=stats[r][1][:, 2 * k0:2 * k1], in_=stats[r][0][:, 2 * k0:2 * k1, 1],
@@ -169,8 +153,6 @@ def tile_bandsplitmodule_kernel(
             )
 
         def stats_finish(r, k0=0, k1=None):
-            if r > LAST:
-                return
             k1 = bands_in(r) if k1 is None else k1
             mean_var, rstd, offset = stats[r]
             nc.vector.scalar_tensor_tensor(
@@ -184,7 +166,7 @@ def tile_bandsplitmodule_kernel(
             for e in range(2):
                 col = 2 * (s * bands_in(r) // PASSES) + e
                 nc.scalar.activation(
-                    out=z_sb[(r, s)][:, e, :, :], in_=x_frames[r][s][:, :, :, e],
+                    out=z_sb[(r, s)][:, e, :, :], in_=x_frames[(r, s)][:, :, :, e],
                     func=ACT.Identity, scale=rstd[:, col:col + 1], bias=offset[:, col:col + 1],
                 )
 
@@ -195,17 +177,14 @@ def tile_bandsplitmodule_kernel(
                 for e in range(2):
                     nc.tensor.transpose(bank[:, jl, e, :], z_sb[(r, s)][:, e, 2 * half + jl, :], ident[:])
 
-        def gain_shift(r, s, half, on_vector=False, planes=(0, 1)):
-            if r < 0:
-                return
-            if s % 2 == 0 and half == 0 and planes[0] == 0:
+        def gain_shift(r, s, j0, j1, on_vector=False):
+            if s % 2 == 0 and j0 == 0:
                 xn_planes[(r, s // 2)] = ppool.tile([P, PACK, 2, COLS], BF16, name="xn_planes", tag="xn_planes")
             g_col = PASSES * r + s
             b_col = ALL_PASSES + g_col
-            for jl in planes:
-                j = 2 * half + jl
+            for j in range(j0, j1):
                 dst = xn_planes[(r, s // 2)][:, j, s % 2, :]
-                src = z_chan[(r, s, half)][:, jl, :, :].rearrange("p e q -> p (e q)")
+                src = z_chan[(r, s, j // 2)][:, j % 2, :, :].rearrange("p e q -> p (e q)")
                 if on_vector:
                     nc.vector.tensor_scalar(
                         out=dst, in0=src, scalar1=g_and_b[:, j, g_col:g_col + 1], scalar2=g_and_b[:, j, b_col:b_col + 1],
@@ -217,14 +196,12 @@ def tile_bandsplitmodule_kernel(
                         scale=g_and_b[:, j, g_col:g_col + 1], bias=g_and_b[:, j, b_col:b_col + 1],
                     )
 
-        def regroup_x(r, c0, c1, engine):
-            if r < 0:
-                return
+        def regroup_x(r, s0, s1, engine):
             if r not in xn_grouped:
                 xn_grouped[r] = gpool.tile([P, PASSES * COLS, PACK], BF16, name="xn_grouped", tag="xn_grouped", align_bytes=64)
-            pair = c0 // (2 * COLS)
-            src = xn_planes[(r, pair)][:].rearrange("p j s c -> p j (s c)")[:, :, c0 - 2 * COLS * pair:c1 - 2 * COLS * pair]
-            dst = xn_grouped[r][:, c0:c1, :]
+            first = s0 - s0 % 2
+            src = xn_planes[(r, s0 // 2)][:, :, s0 - first:s1 - first, :].rearrange("p j s c -> p j (s c)")
+            dst = xn_grouped[r][:, COLS * s0:COLS * s1, :]
             if engine == "gpsimd":
                 nc.gpsimd.tensor_scalar(
                     out=dst, in0=src.rearrange("p j c -> p c j"), scalar1=1.0, scalar2=0.0, op0=ALU.mult, op1=ALU.add,
@@ -256,8 +233,8 @@ def tile_bandsplitmodule_kernel(
             x_codes, x_scales = xn_mx[r]
             for s in range(s0, s1):
                 k = s // passes_per_band
-                if s == 0 or (s == 2 and k == 2):
-                    sums[(r, k // 2)] = ps_z.tile([P, 2 * COLS], F32, name="z_bank", tag="z_bank")
+                if k % 2 == 0 and s % passes_per_band == 0:
+                    sums[(r, k // 2)] = ps_z.tile([P, 2 * COLS], F32, name="sums", tag="z_bank")
                 c0 = COLS * (k % 2)
                 nc.tensor.matmul_mx(
                     out=sums[(r, k // 2)][:, c0:c0 + COLS],
@@ -328,38 +305,29 @@ def tile_bandsplitmodule_kernel(
         gb_bank = ps_z.tile([P, PACK, P], F32, name="gb_bank", tag="z_bank")
         for j in range(PACK):
             nc.tensor.transpose(gb_bank[:, j, :], gb_sorted[:, j, :], ident[:])
-        c_bank = ps_z.tile([P, PACK, P], F32, name="c_bank", tag="z_bank")
-        nc.tensor.transpose(c_bank[:, 0, :], c_f32[:], ident[:])
+        c_bank = ps_z.tile([P, P], F32, name="c_bank", tag="z_bank")
+        nc.tensor.transpose(c_bank[:], c_f32[:], ident[:])
         g_and_b = const.tile([P, PACK, P], F32, name="g_and_b")
-        c_sb = const.tile([P, BANDS], F32, name="c_sb")
         nc.scalar.copy(out=g_and_b[:], in_=gb_bank[:])
-        nc.scalar.copy(out=c_sb[:], in_=c_bank[:, 0, 0:BANDS])
+        c_sb = const.tile([P, BANDS], F32, name="c_sb")
+        nc.scalar.copy(out=c_sb[:], in_=c_bank[:, 0:BANDS])
 
         to_frames(1, 0)
         for s in range(PASSES):
             copy_w(0, s, s + 1)
 
-        def vector_share(r):
-            if r < 0:
-                return
-            v = vector_planes(r)
-            if v > 2:
-                gain_shift(r, 3, 0, on_vector=True, planes=(1,) if v == 3 else (0, 1))
-            if v:
-                gain_shift(r, 3, 1, on_vector=True, planes=(1,) if v == 1 else (0, 1))
-
         for r in range(LAST):
             load_round(r + 3)
-            vector_share(r - 1)
             if r > 0:
+                gain_shift(r - 1, 3, PACK - vector_planes(r - 1), PACK, on_vector=True)
                 copy_w(r + 1, 0, PASSES)
-                regroup_x(r - 1, 512, 1024, "gpsimd")
+                regroup_x(r - 1, 2, 4, "gpsimd")
             finish_bands(r - 2)
             normalise(r, 0)
             if r == 0:
                 stats_sqrt(0, 2, 4)
                 stats_finish(0, 2, 4)
-                normalise(r, 1)
+            normalise(r, 1)
             to_frames(r + 1, 1)
             take_stats(r + 1, 0)
             to_channels(r, 0, 0)
@@ -367,8 +335,6 @@ def tile_bandsplitmodule_kernel(
                 quantise_w(0)
                 for s in range(PASSES):
                     copy_w(1, s, s + 1)
-            else:
-                normalise(r, 1)
             to_frames(r + 1, 2)
             take_stats(r + 1, 1)
             to_channels(r, 0, 1)
@@ -378,65 +344,61 @@ def tile_bandsplitmodule_kernel(
             to_channels(r, 1, 0)
             normalise(r, 3)
             take_stats(r + 1, 3)
-            gain_shift(r, 0, 0)
+            gain_shift(r, 0, 0, 2)
             to_channels(r, 1, 1)
-            gain_shift(r, 0, 1)
+            gain_shift(r, 0, 2, 4)
             to_channels(r, 2, 0)
-            gain_shift(r, 1, 0)
+            gain_shift(r, 1, 0, 2)
             to_channels(r, 2, 1)
-            gain_shift(r, 1, 1)
+            gain_shift(r, 1, 2, 4)
             to_channels(r, 3, 0)
+            quantise_x(r - 1, 0, 1)
             stats_join(r + 1)
-            quantise_x(r - 1, 0, PASSES)
-            gain_shift(r, 2, 0)
+            quantise_x(r - 1, 1, 2)
+            quantise_x(r - 1, 2, 4)
+            gain_shift(r, 2, 0, 2)
             stats_sqrt(r + 1)
             to_channels(r, 3, 1)
             to_frames(r + 2, 0)
-            gain_shift(r, 2, 1)
+            gain_shift(r, 2, 2, 4)
             stats_finish(r + 1)
             quantise_w(r + 1)
-            regroup_x(r, 0, 512, "vector")
-            v = vector_planes(r)
-            if v < 4:
-                gain_shift(r, 3, 0, planes=(0,) if v == 3 else (0, 1))
-            if v < 2:
-                gain_shift(r, 3, 1, planes=(0,) if v == 1 else (0, 1))
+            regroup_x(r, 0, 2, "vector")
+            gain_shift(r, 3, 0, PACK - vector_planes(r))
             multiply(r - 1, 0, PASSES)
 
         r = LAST
-        vector_share(r - 1)
-        regroup_x(r - 1, 512, 1024, "gpsimd")
+        gain_shift(r - 1, 3, PACK - vector_planes(r - 1), PACK, on_vector=True)
+        regroup_x(r - 1, 2, 4, "gpsimd")
         normalise(r, 0)
         to_channels(r, 0, 0)
         to_channels(r, 0, 1)
         normalise(r, 1)
         to_channels(r, 1, 0)
         finish_bands(r - 2)
-        gain_shift(r, 0, 0, on_vector=True)
+        gain_shift(r, 0, 0, 2, on_vector=True)
         to_channels(r, 1, 1)
-        gain_shift(r, 0, 1, on_vector=True)
+        gain_shift(r, 0, 2, 4, on_vector=True)
         normalise(r, 2)
         to_channels(r, 2, 0)
-        gain_shift(r, 1, 0, on_vector=True)
+        gain_shift(r, 1, 0, 2, on_vector=True)
         to_channels(r, 2, 1)
         normalise(r, 3)
-        gain_shift(r, 1, 1, on_vector=True)
+        gain_shift(r, 1, 2, 4, on_vector=True)
         to_channels(r, 3, 0)
         quantise_x(r - 1, 0, PASSES)
-        gain_shift(r, 2, 0)
+        gain_shift(r, 2, 0, 2)
         to_channels(r, 3, 1)
         multiply(r - 1, 0, PASSES)
-        regroup_x(r, 0, 512, "vector")
-        gain_shift(r, 2, 1)
-        regroup_x(r, 512, 768, "vector")
+        regroup_x(r, 0, 2, "vector")
+        gain_shift(r, 2, 2, 4)
+        regroup_x(r, 2, 3, "vector")
         quantise_x(r, 0, 2)
         multiply(r, 0, 2)
-        gain_shift(r, 3, 0)
-        gain_shift(r, 3, 1)
-        regroup_x(r, 768, 1024, "scalar")
+        gain_shift(r, 3, 0, 4)
+        regroup_x(r, 3, 4, "scalar")
         finish_bands(r - 1)
-        quantise_x(r, 2, 3)
-        multiply(r, 2, 3)
-        quantise_x(r, 3, 4)
-        multiply(r, 3, 4)
+        for s in (2, 3):
+            quantise_x(r, s, s + 1)
+            multiply(r, s, s + 1)
         finish_bands(r)

from contextlib import ExitStack

import concourse.mybir as mybir
from concourse.masks import make_identity

FLOPS = 2 * 256 * 32768 * 128

F32 = mybir.dt.float32
BF16 = mybir.dt.bfloat16
U32 = mybir.dt.uint32
U8 = mybir.dt.uint8
FP8X4 = mybir.dt.float8_e4m3fn_x4
ACT = mybir.ActivationFunctionType
ALU = mybir.AluOpType

P = 128
PACK = 4
COLS = 256
EPS = 1e-8
ROUNDS = 16
LAST = ROUNDS - 1
ROUND_BINS = 1024
PASSES = 4
ALL_PASSES = ROUNDS * PASSES
BANDS = 32
STAT_COLS = 8
BN_VALUES = 3


def bands_in(r):
    return 4 if r < 4 else (2 if r < 8 else 1)


def vector_planes(r):
    if r == LAST - 1:
        return 2
    return 4 if r == 0 else {4: 1, 2: 2, 1: 3}[bands_in(r - 1)]


def first_band(r):
    return 4 * r if r < 4 else (2 * r + 8 if r < 8 else r + 16)


def tile_bandsplitmodule_kernel(
    tc, x_real, x_imag, sample_rate,
    g16, b16, W16, c16, g32, b32, W32, c32, g64, b64, W64, c64, out,
):
    nc = tc.nc
    with ExitStack() as ctx:
        const = ctx.enter_context(tc.tile_pool(name="const", bufs=1))
        xpool = ctx.enter_context(tc.tile_pool(name="xpool", bufs=4))
        wpool = ctx.enter_context(tc.tile_pool(name="wpool", bufs=3))
        wgpool = ctx.enter_context(tc.tile_pool(name="wgpool", bufs=1))
        small = ctx.enter_context(tc.tile_pool(name="small", bufs=3))
        zpool = ctx.enter_context(tc.tile_pool(name="zpool", bufs=6))
        ppool = ctx.enter_context(tc.tile_pool(name="ppool", bufs=4))
        gpool = ctx.enter_context(tc.tile_pool(name="gpool", bufs=2))
        opool = ctx.enter_context(tc.tile_pool(name="opool", bufs=2))
        ps_x = ctx.enter_context(tc.psum_pool(name="ps_x", bufs=5))
        ps_z = ctx.enter_context(tc.psum_pool(name="ps_z", bufs=3))
        ctx.enter_context(tc.manual_schedule())

        x_sb, w_raw, w_grouped, w_mx = {}, {}, {}, {}
        x_frames, pieces, stats = {}, {}, {}
        z_sb, z_chan, xn_planes, xn_grouped, xn_mx, sums, out_sb = {}, {}, {}, {}, {}, {}, {}

        def load_round(r):
            if r > LAST:
                return
            bin0 = ROUND_BINS * r
            x_sb[r] = xpool.tile([P, PASSES * PACK * COLS], BF16, name="x_sb", tag="x_sb")
            x_view = x_sb[r][:].rearrange("p (s j i t) -> p s j i t", s=PASSES, j=PACK, i=2)
            for s in range(PASSES):
                if bands_in(r) == 4:
                    parts = [(x_real, bin0 + 256 * s, 0, 64), (x_imag, bin0 + 256 * s, 64, 64)]
                elif bands_in(r) == 2:
                    parts = [((x_real, x_imag)[s % 2], bin0 + 512 * (s // 2), 0, P)]
                else:
                    parts = [((x_real, x_imag)[s // 2], bin0 + 512 * (s % 2), 0, P)]
                for src, first, p0, count in parts:
                    for i in range(2):
                        nc.sync.dma_start(
                            out=x_view[p0:p0 + count, s, :, i, :],
                            in_=src[i, first:first + PACK * count, :].rearrange("(p j) t -> p j t", j=PACK),
                        )
            w_raw[r] = wpool.tile([P, PASSES, PACK * P], BF16, name="w_raw", tag="w_raw")
            if bands_in(r) == 4:
                w_rows = W16[4 * r:4 * r + 4].rearrange("k (p j) n -> p k (j n)", j=PACK)
            elif bands_in(r) == 2:
                w_rows = W32[2 * r - 8:2 * r - 6].rearrange("k (s p j) n -> p (k s) (j n)", s=2, j=PACK)
            else:
                w_rows = W64[r - 8].rearrange("(s p j) n -> p s (j n)", s=PASSES, j=PACK)
            nc.sync.dma_start(out=w_raw[r][:], in_=w_rows)

        def copy_w(r, s0, s1):
            if s0 == 0:
                w_grouped[r] = wgpool.tile([P, PASSES, P, PACK], BF16, name="w_grouped", tag="w_grouped", align_bytes=64)
            nc.gpsimd.tensor_scalar(
                out=w_grouped[r][:, s0:s1, :, :],
                in0=w_raw[r][:, s0:s1, :].rearrange("p s (j n) -> p s n j", j=PACK),
                scalar1=1.0, scalar2=0.0, op0=ALU.mult, op1=ALU.add,
            )

        def quantise_w(r):
            codes = wpool.tile([P, PASSES * P], U32, name="w_codes", tag="w_codes", align_bytes=64)
            scales = wpool.tile([P, PASSES * P], U8, name="w_scales", tag="w_scales", align_bytes=64)
            nc.vector.quantize_mx(
                out=codes[:].bitcast(FP8X4), scales=scales[:],
                in_=w_grouped[r][:].rearrange("p s n j -> p (s n j)"),
            )
            w_mx[r] = (codes, scales)

        def to_frames(r, s):
            if r > LAST:
                return
            pairs = x_sb[r][:].bitcast(F32)
            bank = ps_x.tile([P, PACK * P], F32, name="x_bank", tag="x_bank")
            for j in range(PACK):
                c0 = (s * PACK + j) * P
                nc.tensor.transpose(bank[:, j * P:(j + 1) * P], pairs[:, c0:c0 + P], ident[:])
            x_frames[(r, s)] = bank[:].bitcast(BF16).rearrange("q (j p e) -> q j p e", j=PACK, e=2)

        def take_stats(r, s):
            if s == 0:
                pieces[r] = small.tile([P, 2 * PASSES, 2 * BN_VALUES], F32, name="pieces", tag="pieces")
            for h in range(2):
                nc.vector.bn_stats(
                    out=pieces[r][:, 2 * s + h, :],
                    in_=x_frames[(r, s)][:, 2 * h:2 * h + 2, :, :].rearrange("q j p e -> q (j p e)"),
                )

        def stats_join(r, k0=0, k1=None):
            k1 = bands_in(r) if k1 is None else k1
            pieces_per_band = 2 * PASSES // bands_in(r)
            if k0 == 0:
                stats[r] = [
                    small.tile([P, STAT_COLS, 2], F32, name="mean_var", tag="mean_var"),
                    small.tile([P, STAT_COLS], F32, name="rstd", tag="rstd"),
                    small.tile([P, STAT_COLS], F32, name="offset", tag="offset"),
                ]
            for k in range(k0, k1):
                for e in range(2):
                    nc.vector.bn_aggr(
                        out=stats[r][0][:, 2 * k + e, :],
                        in_=pieces[r][:, pieces_per_band * k:pieces_per_band * (k + 1), BN_VALUES * e:BN_VALUES * (e + 1)],
                    )

        def stats_sqrt(r, k0=0, k1=None):
            k1 = bands_in(r) if k1 is None else k1
            nc.scalar.activation(
                out=stats[r][1][:, 2 * k0:2 * k1], in_=stats[r][0][:, 2 * k0:2 * k1, 1],
                func=ACT.Abs_reciprocal_sqrt, bias=EPS, scale=1.0,
            )

        def stats_finish(r, k0=0, k1=None):
            k1 = bands_in(r) if k1 is None else k1
            mean_var, rstd, offset = stats[r]
            nc.vector.scalar_tensor_tensor(
                out=offset[:, 2 * k0:2 * k1], in0=mean_var[:, 2 * k0:2 * k1, 0], scalar=-1.0,
                in1=rstd[:, 2 * k0:2 * k1], op0=ALU.mult, op1=ALU.mult,
            )

        def normalise(r, s):
            rstd, offset = stats[r][1], stats[r][2]
            z_sb[(r, s)] = zpool.tile([P, 2, PACK, P], F32, name="z_sb", tag="z_sb")
            for e in range(2):
                col = 2 * (s * bands_in(r) // PASSES) + e
                nc.scalar.activation(
                    out=z_sb[(r, s)][:, e, :, :], in_=x_frames[(r, s)][:, :, :, e],
                    func=ACT.Identity, scale=rstd[:, col:col + 1], bias=offset[:, col:col + 1],
                )

        def to_channels(r, s, half):
            bank = ps_z.tile([P, 2, 2, P], F32, name="z_bank", tag="z_bank")
            z_chan[(r, s, half)] = bank
            for jl in range(2):
                for e in range(2):
                    nc.tensor.transpose(bank[:, jl, e, :], z_sb[(r, s)][:, e, 2 * half + jl, :], ident[:])

        def gain_shift(r, s, j0, j1, on_vector=False):
            if s % 2 == 0 and j0 == 0:
                xn_planes[(r, s // 2)] = ppool.tile([P, PACK, 2, COLS], BF16, name="xn_planes", tag="xn_planes")
            g_col = PASSES * r + s
            b_col = ALL_PASSES + g_col
            for j in range(j0, j1):
                dst = xn_planes[(r, s // 2)][:, j, s % 2, :]
                src = z_chan[(r, s, j // 2)][:, j % 2, :, :].rearrange("p e q -> p (e q)")
                if on_vector:
                    nc.vector.tensor_scalar(
                        out=dst, in0=src, scalar1=g_and_b[:, j, g_col:g_col + 1], scalar2=g_and_b[:, j, b_col:b_col + 1],
                        op0=ALU.mult, op1=ALU.add,
                    )
                else:
                    nc.scalar.activation(
                        out=dst, in_=src, func=ACT.Identity,
                        scale=g_and_b[:, j, g_col:g_col + 1], bias=g_and_b[:, j, b_col:b_col + 1],
                    )

        def regroup_x(r, s0, s1, engine):
            if r not in xn_grouped:
                xn_grouped[r] = gpool.tile([P, PASSES * COLS, PACK], BF16, name="xn_grouped", tag="xn_grouped", align_bytes=64)
            first = s0 - s0 % 2
            src = xn_planes[(r, s0 // 2)][:, :, s0 - first:s1 - first, :].rearrange("p j s c -> p j (s c)")
            dst = xn_grouped[r][:, COLS * s0:COLS * s1, :]
            if engine == "gpsimd":
                nc.gpsimd.tensor_scalar(
                    out=dst, in0=src.rearrange("p j c -> p c j"), scalar1=1.0, scalar2=0.0, op0=ALU.mult, op1=ALU.add,
                )
                return
            (nc.scalar.copy if engine == "scalar" else nc.vector.tensor_copy)(
                out=dst.rearrange("p (c u) j -> p c j u", u=4), in_=src.rearrange("p j (c u) -> p c j u", u=4),
            )

        def quantise_x(r, s0, s1):
            if r < 0:
                return
            if s0 == 0:
                xn_mx[r] = (
                    gpool.tile([P, PASSES * COLS], U32, name="x_codes", tag="x_codes", align_bytes=64),
                    gpool.tile([P, PASSES * COLS], U8, name="x_scales", tag="x_scales", align_bytes=64),
                )
            codes, scales = xn_mx[r]
            nc.vector.quantize_mx(
                out=codes[:, COLS * s0:COLS * s1].bitcast(FP8X4), scales=scales[:, COLS * s0:COLS * s1],
                in_=xn_grouped[r][:, COLS * s0:COLS * s1, :].rearrange("p c j -> p (c j)"),
            )

        def multiply(r, s0, s1):
            if r < 0:
                return
            passes_per_band = PASSES // bands_in(r)
            w_codes, w_scales = w_mx[r]
            x_codes, x_scales = xn_mx[r]
            for s in range(s0, s1):
                k = s // passes_per_band
                if k % 2 == 0 and s % passes_per_band == 0:
                    sums[(r, k // 2)] = ps_z.tile([P, 2 * COLS], F32, name="sums", tag="z_bank")
                c0 = COLS * (k % 2)
                nc.tensor.matmul_mx(
                    out=sums[(r, k // 2)][:, c0:c0 + COLS],
                    lhsT=w_codes[:, s * P:(s + 1) * P].bitcast(FP8X4),
                    lhsT_scale=w_scales[:, s * P:(s + 1) * P],
                    rhs=x_codes[:, COLS * s:COLS * (s + 1)].bitcast(FP8X4),
                    rhs_scale=x_scales[:, COLS * s:COLS * (s + 1)],
                    start=(s % passes_per_band == 0),
                    stop=(s % passes_per_band == passes_per_band - 1),
                )

        def finish_bands(r):
            if r < 0:
                return
            for k in range(bands_in(r)):
                band = first_band(r) + k
                group, slot = (BANDS // 4, 0) if band == BANDS - 1 else divmod(band, 4)
                if slot == 0:
                    out_sb[group] = opool.tile([P, 2, 4, P], F32, name="out_sb", tag="out_sb")
                c0 = COLS * (k % 2)
                nc.vector.tensor_scalar(
                    out=out_sb[group][:, :, slot, :].rearrange("n i (q e) -> n i q e", e=2),
                    in0=sums[(r, k // 2)][:, c0:c0 + COLS].rearrange("n (e i q) -> n i q e", e=2, i=2),
                    scalar1=c_sb[:, band:band + 1], scalar2=None, op0=ALU.add,
                )
                if slot == 3 or band >= BANDS - 2:
                    nc.sync.dma_start(
                        out=out[:, :, band - slot:band + 1, :].rearrange("i n k t -> n i (k t)"),
                        in_=out_sb[group][:, :, 0:slot + 1, :].rearrange("n i k t -> n i (k t)"),
                    )

        ident = const.tile([P, P], F32, name="ident")
        make_identity(nc, ident[:])
        load_round(0)
        gb_rows = const.tile([P, PACK * P], BF16, name="gb_rows")
        for row0, vec, passes_per_band in (
            (0, g16, 1), (16, g32, 2), (32, g64, 4),
            (ALL_PASSES, b16, 1), (ALL_PASSES + 16, b32, 2), (ALL_PASSES + 32, b64, 4),
        ):
            nc.scalar.dma_start(
                out=gb_rows[row0:row0 + vec.shape[0] * passes_per_band, :],
                in_=vec.rearrange("k (s c) -> (k s) c", s=passes_per_band),
            )
        c_rows = const.tile([P, P], BF16, name="c_rows")
        nc.vector.memset(c_rows[:], 0.0)
        nc.scalar.dma_start(out=c_rows[0:16, :], in_=c16)
        nc.scalar.dma_start(out=c_rows[16:24, :], in_=c32)
        nc.scalar.dma_start(out=c_rows[24:32, :], in_=c64)
        load_round(1)
        load_round(2)

        gb_sorted = const.tile([P, PACK, P], F32, name="gb_sorted")
        nc.scalar.copy(out=gb_sorted[:], in_=gb_rows[:].rearrange("m (p j) -> m j p", j=PACK))
        c_f32 = const.tile([P, P], F32, name="c_f32")
        nc.scalar.copy(out=c_f32[:], in_=c_rows[:])

        for s in range(PASSES):
            to_frames(0, s)
        take_stats(0, 0)
        take_stats(0, 1)
        stats_join(0, 0, 2)
        stats_sqrt(0, 0, 2)
        take_stats(0, 2)
        stats_finish(0, 0, 2)
        take_stats(0, 3)
        stats_join(0, 2, 4)

        gb_bank = ps_z.tile([P, PACK, P], F32, name="gb_bank", tag="z_bank")
        for j in range(PACK):
            nc.tensor.transpose(gb_bank[:, j, :], gb_sorted[:, j, :], ident[:])
        c_bank = ps_z.tile([P, P], F32, name="c_bank", tag="z_bank")
        nc.tensor.transpose(c_bank[:], c_f32[:], ident[:])
        g_and_b = const.tile([P, PACK, P], F32, name="g_and_b")
        nc.scalar.copy(out=g_and_b[:], in_=gb_bank[:])
        c_sb = const.tile([P, BANDS], F32, name="c_sb")
        nc.scalar.copy(out=c_sb[:], in_=c_bank[:, 0:BANDS])

        to_frames(1, 0)
        for s in range(PASSES):
            copy_w(0, s, s + 1)

        for r in range(LAST):
            load_round(r + 3)
            if r > 0:
                gain_shift(r - 1, 3, PACK - vector_planes(r - 1), PACK, on_vector=True)
                copy_w(r + 1, 0, PASSES)
                regroup_x(r - 1, 2, 4, "gpsimd")
            finish_bands(r - 2)
            normalise(r, 0)
            if r == 0:
                stats_sqrt(0, 2, 4)
                stats_finish(0, 2, 4)
            normalise(r, 1)
            to_frames(r + 1, 1)
            take_stats(r + 1, 0)
            to_channels(r, 0, 0)
            if r == 0:
                quantise_w(0)
                for s in range(PASSES):
                    copy_w(1, s, s + 1)
            to_frames(r + 1, 2)
            take_stats(r + 1, 1)
            to_channels(r, 0, 1)
            normalise(r, 2)
            to_frames(r + 1, 3)
            take_stats(r + 1, 2)
            to_channels(r, 1, 0)
            normalise(r, 3)
            take_stats(r + 1, 3)
            gain_shift(r, 0, 0, 2)
            to_channels(r, 1, 1)
            gain_shift(r, 0, 2, 4)
            to_channels(r, 2, 0)
            gain_shift(r, 1, 0, 2)
            to_channels(r, 2, 1)
            gain_shift(r, 1, 2, 4)
            to_channels(r, 3, 0)
            quantise_x(r - 1, 0, 1)
            stats_join(r + 1)
            quantise_x(r - 1, 1, 2)
            quantise_x(r - 1, 2, 4)
            gain_shift(r, 2, 0, 2)
            stats_sqrt(r + 1)
            to_channels(r, 3, 1)
            to_frames(r + 2, 0)
            gain_shift(r, 2, 2, 4)
            stats_finish(r + 1)
            quantise_w(r + 1)
            regroup_x(r, 0, 2, "vector")
            gain_shift(r, 3, 0, PACK - vector_planes(r))
            multiply(r - 1, 0, PASSES)

        r = LAST
        gain_shift(r - 1, 3, PACK - vector_planes(r - 1), PACK, on_vector=True)
        regroup_x(r - 1, 2, 4, "gpsimd")
        normalise(r, 0)
        to_channels(r, 0, 0)
        to_channels(r, 0, 1)
        normalise(r, 1)
        to_channels(r, 1, 0)
        finish_bands(r - 2)
        gain_shift(r, 0, 0, 2, on_vector=True)
        to_channels(r, 1, 1)
        gain_shift(r, 0, 2, 4, on_vector=True)
        normalise(r, 2)
        to_channels(r, 2, 0)
        gain_shift(r, 1, 0, 2, on_vector=True)
        to_channels(r, 2, 1)
        normalise(r, 3)
        gain_shift(r, 1, 2, 4, on_vector=True)
        to_channels(r, 3, 0)
        quantise_x(r - 1, 0, PASSES)
        gain_shift(r, 2, 0, 2)
        to_channels(r, 3, 1)
        multiply(r - 1, 0, PASSES)
        regroup_x(r, 0, 2, "vector")
        gain_shift(r, 2, 2, 4)
        regroup_x(r, 2, 3, "vector")
        quantise_x(r, 0, 2)
        multiply(r, 0, 2)
        gain_shift(r, 3, 0, 4)
        regroup_x(r, 3, 4, "scalar")
        finish_bands(r - 1)
        for s in (2, 3):
            quantise_x(r, s, s + 1)
            multiply(r, s, s + 1)
        finish_bands(r)
